import numpy as np
import ml_dtypes


def mxq(x, axis, fmt="e4m3"):
    dtype, down = {"e4m3": (ml_dtypes.float8_e4m3fn, 7), "e5m2": (ml_dtypes.float8_e5m2, 14)}[fmt]
    v = np.moveaxis(np.asarray(x, np.float32).astype(ml_dtypes.bfloat16).astype(np.float64), axis, -1)
    blocks = v.reshape(v.shape[:-1] + (-1, 32))
    amax = np.abs(blocks).max(-1, keepdims=True)
    byte = np.maximum(np.where(amax > 0, np.frexp(amax)[1] - 1 + 127, 0) - down, 1)
    scale = np.exp2(byte - 127.0)
    codes = (blocks / scale).astype(np.float32).astype(dtype).astype(np.float64)
    return np.moveaxis((codes * scale).reshape(v.shape), -1, axis)


WIDE = False


def mx_kscale(k):
    if not WIDE:
        return np.ones(k)
    levels = np.array([10, -10, 5, -5, 0])
    a = np.random.permutation(np.resize(levels, k // 512 * 4)).reshape(k // 512, 4)
    idx = np.arange(k)
    return np.exp2(a[idx // 512, idx % 128 // 32])


BF16 = ml_dtypes.bfloat16


def bf(x):
    return np.asarray(x, np.float32).astype(BF16)


def f64(x):
    return np.asarray(x).astype(np.float64)


B, S, D, H = 2, 64, 512, 1024
NS = int(round(np.log2(H)))


def erf(z):
    z = np.clip(z, -6.0, 6.0)
    z2 = 2.0 * z * z
    term = z.copy()
    tot = z.copy()
    for n in range(1, 130):
        term = term * (z2 / (2 * n + 1))
        tot = tot + term
    return 2.0 / np.sqrt(np.pi) * np.exp(-z * z) * tot


def gelu_exact(v):
    return 0.5 * v * (1.0 + erf(v / np.sqrt(2.0)))


def butterfly(y, weights, dim):
    lead = y.shape[:-1]
    for stage in range(weights.shape[0]):
        s = 2 ** stage
        nb = dim // (2 * s)
        yr = y.reshape(*lead, nb, 2, s)
        a = yr[..., 0, :]
        b = yr[..., 1, :]
        w = weights[stage].reshape(nb, s, 2, 2)
        na = w[..., 0, 0] * a + w[..., 0, 1] * b
        nb2 = w[..., 1, 0] * a + w[..., 1, 1] * b
        y = np.stack([na, nb2], axis=-2).reshape(*lead, dim)
    return y


def bfly_draw():
    g = np.random.standard_normal((NS, H // 2, 2, 2))
    return np.sign(g) * 0.58 + 0.15 * g


def setup_inputs():
    s, t = mx_kscale(D), mx_kscale(H)
    x = np.random.standard_normal((B, S, D)) * s
    W_exp = np.random.standard_normal((D, H)) / np.sqrt(D) / s[:, None]
    b_exp = np.random.standard_normal(H) * 0.1
    up_weights = bfly_draw()
    up_bias = np.random.standard_normal(H) * 0.1
    down_weights = bfly_draw()
    down_weights[NS - 1] = down_weights[NS - 1] * t.reshape(2, H // 2).T[:, :, None]
    W_con = np.random.standard_normal((H, D)) * 1.5 / np.sqrt(H) / t[:, None]
    b_con = np.random.standard_normal(D) * 0.1
    down_bias = np.random.standard_normal(D) * 0.1
    return {"x": bf(x), "W_exp": bf(W_exp), "b_exp": bf(b_exp), "up_weights": bf(up_weights), "up_bias": bf(up_bias),
            "down_weights": bf(down_weights), "W_con": bf(W_con), "b_con": bf(b_con), "down_bias": bf(down_bias)}


def reference(x, W_exp, b_exp, up_weights, up_bias, down_weights, W_con, b_con, down_bias):
    h = (mxq(f64(x), 2, "e4m3") @ mxq(f64(W_exp), 0, "e4m3")) + f64(b_exp)
    h = butterfly(h, f64(up_weights), H)
    h = gelu_exact(h + f64(up_bias))
    h = butterfly(h, f64(down_weights), H)
    y = (mxq(h, 2, "e4m3") @ mxq(f64(W_con), 0, "e4m3")) + f64(b_con)
    return y + f64(down_bias)

@@ -1,0 +1,306 @@
+from contextlib import ExitStack
+
+import concourse.mybir as mybir
+from concourse.masks import make_identity
+
+F32 = mybir.dt.float32
+BF16 = mybir.dt.bfloat16
+U32 = mybir.dt.uint32
+U8 = mybir.dt.uint8
+FP8X4 = mybir.dt.float8_e4m3fn_x4
+ACT = mybir.ActivationFunctionType
+ALU = mybir.AluOpType
+
+P = 128
+TOKENS = 128
+D_IN = 512
+HIDDEN = 1024
+D_OUT = 512
+FEATURE_BITS = 10
+STAGES = 2 * FEATURE_BITS
+CHUNKS = 8
+CHUNK_BITS = 3
+PACK = 4
+LAYOUTS = 7
+
+FLOPS = 2 * TOKENS * D_IN * HIDDEN + 2 * TOKENS * HIDDEN * D_OUT + STAGES * TOKENS * HIDDEN * 3
+
+PAIR_ORDER = ((0, 2, 4, 6), (0, 1, 4, 5), (0, 2, 1, 3))
+FILL_ORDER = (1, 3, 0, 2, 5, 7, 4, 6)
+
+
+def free_pair_bits(s):
+    st = s % FEATURE_BITS
+    found = []
+    for j in range(CHUNK_BITS):
+        feature_bit = (s - s % CHUNK_BITS + j) % FEATURE_BITS
+        if feature_bit != st:
+            found.append((feature_bit if feature_bit < st else feature_bit - 1, j))
+    return sorted(found)
+
+
+def load_pair_weights(nc, queue, dst, stage_weights, s):
+    (low, j_low), (high, j_high) = free_pair_bits(s)
+    if high == low + 1:
+        n_lo = 2**low
+        n_hi = P // n_lo
+        if n_lo <= n_hi:
+            view = stage_weights.rearrange("(hi g lo) r c -> lo hi g (r c)", g=4, lo=n_lo)
+            for lo in range(n_lo):
+                queue.dma_start(out=dst[lo * n_hi : (lo + 1) * n_hi], in_=view[lo])
+        else:
+            view = stage_weights.rearrange("(hi g lo) r c -> hi lo g (r c)", g=4, lo=n_lo)
+            for hi in range(n_hi):
+                queue.dma_start(out=dst[hi:P:n_hi], in_=view[hi])
+    else:
+        assert (low, high) == (0, 8)
+        queue.dma_start(
+            out=dst.rearrange("p (x y) e -> p x (y e)", x=2),
+            in_=stage_weights.rearrange("(x p y) r c -> p x (y r c)", x=2, y=2),
+        )
+
+
+def group_of(s, chunk):
+    (low, j_low), (high, j_high) = free_pair_bits(s)
+    return 2 * ((chunk >> j_high) & 1) + ((chunk >> j_low) & 1)
+
+
+def tile_butterflymlp_s_kernel(
+    tc, x, W_exp, b_exp, up_weights, up_bias, down_weights, W_con, b_con, down_bias, out
+):
+    nc = tc.nc
+    with ExitStack() as ctx:
+        ctx.enter_context(tc.manual_schedule())
+        keep = ctx.enter_context(tc.tile_pool(name="keep", bufs=1))
+        data = ctx.enter_context(tc.tile_pool(name="data", bufs=3))
+        products = ctx.enter_context(tc.tile_pool(name="products", bufs=4))
+        psum = ctx.enter_context(tc.psum_pool(name="psum", bufs=1))
+
+        x_sb = keep.tile([P, D_IN], BF16)
+        nc.sync.dma_start(out=x_sb[:], in_=x.flatten_outer_dims())
+        w_exp_raw = keep.tile([P, PACK, HIDDEN], BF16)
+        for u in range(2):
+            nc.sync.dma_start(
+                out=w_exp_raw[:, 2 * u : 2 * u + 2, :],
+                in_=W_exp[256 * u : 256 * u + 256, :].rearrange("(q e) c -> q e c", e=2),
+            )
+
+        pair_w_bf = keep.tile([P, STAGES, 4, 4], BF16)
+        b_exp_bf = keep.tile([P, CHUNKS], BF16)
+        up_bias_bf = keep.tile([P, 2, 4], BF16)
+        w_con_raw = keep.tile([P, 2, PACK, D_OUT], BF16)
+        b_con_rows = keep.tile([P, D_OUT], BF16)
+        down_bias_rows = keep.tile([P, D_OUT], BF16)
+
+        def load_stage(queue, s):
+            weights = up_weights if s < FEATURE_BITS else down_weights
+            load_pair_weights(nc, queue, pair_w_bf[:, s], weights[s % FEATURE_BITS], s)
+
+        for s in range(0, 3):
+            load_stage(nc.scalar, s)
+        nc.scalar.dma_start(out=b_exp_bf[:], in_=b_exp.rearrange("(p c) -> p c", c=CHUNKS))
+        for s in range(3, 6):
+            load_stage(nc.sync, s)
+        nc.sync.dma_start(
+            out=w_con_raw[:].rearrange("p g (u e) c -> p (g u) (e c)", u=2),
+            in_=W_con.rearrange("(a q e) c -> q a (e c)", a=4, e=2),
+        )
+        for s in range(6, 10):
+            load_stage(nc.sync, s)
+        nc.sync.dma_start(out=up_bias_bf[:], in_=up_bias.rearrange("(h p l) -> p h l", h=2, l=4))
+        for s in range(10, STAGES):
+            load_stage(nc.sync, s)
+        nc.sync.dma_start(out=b_con_rows[:], in_=b_con.partition_broadcast(P))
+        nc.sync.dma_start(out=down_bias_rows[:], in_=down_bias.partition_broadcast(P))
+
+        identity = keep.tile([P, P], F32)
+        make_identity(nc, identity[:])
+        zero_column = keep.tile([P, 1], F32)
+        gelu_of_zero = keep.tile([P, 1], F32)
+        nc.vector.memset(zero_column[:], 0.0)
+        nc.scalar.activation(out=gelu_of_zero[:], in_=zero_column[:], func=ACT.Gelu)
+
+        out_bias = keep.tile([P, D_OUT], F32)
+        nc.gpsimd.tensor_tensor(out=out_bias[:], in0=b_con_rows[:], in1=down_bias_rows[:], op=ALU.add)
+
+        pair_w = keep.tile([P, STAGES, 4, 4], F32)
+
+        def widen_pair_weights(layout):
+            first = CHUNK_BITS * layout
+            last = min(first + CHUNK_BITS, STAGES)
+            nc.vector.tensor_copy(out=pair_w[:, first:last], in_=pair_w_bf[:, first:last])
+
+        widen_pair_weights(0)
+        b_exp_f = keep.tile([P, 4, 2], F32)
+        nc.vector.tensor_copy(out=b_exp_f[:].rearrange("p g r -> p (g r)"), in_=b_exp_bf[:])
+        stage0_w = pair_w[:, 0].rearrange("p g (r c) -> p g r c", r=2)
+        from_a = keep.tile([P, 4, 2], F32)
+        from_b = keep.tile([P, 4, 2], F32)
+        stage0_bias = keep.tile([P, 4, 2], F32)
+        nc.vector.tensor_tensor(
+            out=from_a[:], in0=stage0_w[:, :, :, 0], in1=b_exp_f[:, :, 0:1].to_broadcast([P, 4, 2]), op=ALU.mult
+        )
+        nc.vector.tensor_tensor(
+            out=from_b[:], in0=stage0_w[:, :, :, 1], in1=b_exp_f[:, :, 1:2].to_broadcast([P, 4, 2]), op=ALU.mult
+        )
+        nc.vector.tensor_tensor(out=stage0_bias[:], in0=from_a[:], in1=from_b[:], op=ALU.add)
+        up_bias_f = keep.tile([P, 2, 4], F32)
+
+        x_words = x_sb[:].bitcast(F32)
+        x_t = psum.tile([P, 2, TOKENS], F32, tag="tok0")
+        for u in range(2):
+            nc.tensor.transpose(x_t[:, u, :], x_words[:, P * u : P * u + P], identity[:])
+        x_grouped = keep.tile([P, TOKENS, 2], F32, align_bytes=64)
+        nc.vector.tensor_copy(out=x_grouped[:], in_=x_t[:].rearrange("p u t -> p t u"))
+        x_codes = keep.tile([P, TOKENS], U32, align_bytes=64)
+        x_scales = keep.tile([P, TOKENS], U8, align_bytes=64)
+
+        w_exp_grouped = keep.tile([P, CHUNKS, P, PACK], BF16, align_bytes=64)
+        w_exp_view = w_exp_raw[:].rearrange("p t (m c) -> p c m t", c=CHUNKS)
+        w_exp_codes = keep.tile([P, CHUNKS, P], U32, align_bytes=64)
+        w_exp_scales = keep.tile([P, CHUNKS, P], U8, align_bytes=64)
+        nc.scalar.copy(out=w_exp_grouped[:, 6:8], in_=w_exp_view[:, 6:8])
+        nc.vector.tensor_copy(out=w_exp_grouped[:, 0:4], in_=w_exp_view[:, 0:4])
+        nc.vector.quantize_mx(
+            out=x_codes[:].bitcast(FP8X4),
+            scales=x_scales[:],
+            in_=x_grouped[:].rearrange("p t u -> p (t u)").bitcast(BF16),
+        )
+        nc.vector.tensor_copy(out=w_exp_grouped[:, 4:6], in_=w_exp_view[:, 4:6])
+        for half in range(2):
+            chunks = slice(4 * half, 4 * half + 4)
+            nc.vector.quantize_mx(
+                out=w_exp_codes[:, chunks].rearrange("p c m -> p (c m)").bitcast(FP8X4),
+                scales=w_exp_scales[:, chunks].rearrange("p c m -> p (c m)"),
+                in_=w_exp_grouped[:, chunks].rearrange("p c m t -> p (c m t)"),
+            )
+
+        def new_psum_chunks():
+            banks = [psum.tile([P, 2, TOKENS], F32, tag="chunks%d" % i, name="chunks%d" % i) for i in range(4)]
+            return [banks[2 * (c >> 2) + (c & 1)][:, (c >> 1) & 1, :] for c in range(CHUNKS)]
+
+        chunk = new_psum_chunks()
+        for c in FILL_ORDER:
+            nc.tensor.matmul_mx(
+                out=chunk[c],
+                lhsT=w_exp_codes[:, c, :].bitcast(FP8X4),
+                lhsT_scale=w_exp_scales[:, c, :],
+                rhs=x_codes[:].bitcast(FP8X4),
+                rhs_scale=x_scales[:],
+                start=True,
+                stop=True,
+            )
+
+        w_con_grouped = keep.tile([P, 2, D_OUT, PACK], BF16, align_bytes=64)
+        w_con_codes = keep.tile([P, 2, D_OUT], U32, align_bytes=64)
+        w_con_scales = keep.tile([P, 2, D_OUT], U8, align_bytes=64)
+
+        def regroup_w_con(quarter):
+            g, half = divmod(quarter, 2)
+            cols = slice(256 * half, 256 * half + 256)
+            nc.vector.tensor_copy(
+                out=w_con_grouped[:, g, cols, :].rearrange("p (c i) t -> p c t i", i=4),
+                in_=w_con_raw[:, g, :, cols].rearrange("p t (c i) -> p c t i", i=4),
+            )
+
+        def quantise_w_con():
+            nc.vector.quantize_mx(
+                out=w_con_codes[:].rearrange("p g c -> p (g c)").bitcast(FP8X4),
+                scales=w_con_scales[:].rearrange("p g c -> p (g c)"),
+                in_=w_con_grouped[:].rearrange("p g c t -> p (g c t)"),
+            )
+
+        def stage(s, chunk, bias_of, gelu):
+            j = s % CHUNK_BITS
+            new = data.tile([P, CHUNKS, TOKENS], F32, tag="chunks")
+            order = PAIR_ORDER[j]
+
+            def apply_gelu(a):
+                nc.scalar.activation(out=new[:, a : a + 2, :], in_=new[:, a : a + 2, :], func=ACT.Gelu)
+
+            for i, a in enumerate(order):
+                b = a | (1 << j)
+                w = pair_w[:, s, group_of(s, a)]
+                prod = products.tile([P, 2, TOKENS], F32, tag="prod")
+                for r, c in enumerate((a, b)):
+                    nc.scalar.activation(
+                        out=prod[:, r, :],
+                        in_=chunk[b],
+                        func=ACT.Identity,
+                        scale=w[:, 2 * r + 1 : 2 * r + 2],
+                        bias=bias_of(c) if bias_of else 0.0,
+                    )
+                for r, c in enumerate((a, b)):
+                    nc.vector.scalar_tensor_tensor(
+                        out=new[:, c, :],
+                        in0=chunk[a],
+                        scalar=w[:, 2 * r : 2 * r + 1],
+                        in1=prod[:, r, :],
+                        op0=ALU.mult,
+                        op1=ALU.add,
+                    )
+                if gelu and i > 0:
+                    apply_gelu(order[i - 1])
+            if gelu:
+                apply_gelu(order[-1])
+            return new
+
+        def next_layout(chunk, layout):
+            by_token = data.tile([P, CHUNKS, CHUNKS, 16], F32, tag="by_token")
+            for i, a in enumerate(PAIR_ORDER[2]):
+                flipped = psum.tile([P, 2, P], F32, tag="tok%d" % i, name="flipped%d" % i)
+                nc.tensor.transpose(flipped[:, 0, :], chunk[a], identity[:])
+                nc.tensor.transpose(flipped[:, 1, :], chunk[a + 4], identity[:])
+                copy = nc.scalar.copy if i < 3 else nc.vector.tensor_copy
+                copy(
+                    out=by_token[:, :, a : a + 5 : 4, :],
+                    in_=flipped[:].rearrange("t s (hi lo) -> t lo s hi", lo=CHUNKS),
+                )
+            new = new_psum_chunks()
+            for c in FILL_ORDER:
+                nc.tensor.transpose(new[c], by_token[:, c].rearrange("t c hi -> t (c hi)"), identity[:])
+            widen_pair_weights(layout)
+            if layout == 3:
+                nc.vector.tensor_copy(out=up_bias_f[:], in_=up_bias_bf[:])
+            if 2 <= layout <= 5:
+                regroup_w_con(layout - 2)
+            if layout == 6:
+                quantise_w_con()
+            return new
+
+        for s in range(STAGES):
+            if s > 0 and s % CHUNK_BITS == 0:
+                chunk = next_layout(chunk, s // CHUNK_BITS)
+            if s == 0:
+                hidden = stage(s, chunk, lambda c: stage0_bias[:, c >> 1, (c & 1) : (c & 1) + 1], False)
+            elif s == FEATURE_BITS - 1:
+                hidden = stage(s, chunk, lambda c: up_bias_f[:, c & 1, (c >> 1) : (c >> 1) + 1], True)
+            else:
+                hidden = stage(s, chunk, None, False)
+            chunk = [hidden[:, c, :] for c in range(CHUNKS)]
+
+        h_view = hidden[:].rearrange("p (e g u) t -> p g t u e", e=2, g=2, u=2)
+        h_grouped = keep.tile([P, 2, TOKENS, PACK], BF16, align_bytes=64)
+        h_codes = keep.tile([P, 2, TOKENS], U32, align_bytes=64)
+        h_scales = keep.tile([P, 2, TOKENS], U8, align_bytes=64)
+        nc.vector.tensor_copy(out=h_grouped[:, 0].rearrange("p t (u e) -> p t u e", u=2), in_=h_view[:, 0])
+        nc.scalar.copy(out=h_grouped[:, 1].rearrange("p t (u e) -> p t u e", u=2), in_=h_view[:, 1])
+        nc.vector.quantize_mx(
+            out=h_codes[:].rearrange("p g t -> p (g t)").bitcast(FP8X4),
+            scales=h_scales[:].rearrange("p g t -> p (g t)"),
+            in_=h_grouped[:].rearrange("p g t k -> p (g t k)"),
+        )
+        out_ps = psum.tile([P, D_OUT], F32, tag="tok1")
+        for g in range(2):
+            nc.tensor.matmul_mx(
+                out=out_ps[:],
+                lhsT=h_codes[:, g, :].bitcast(FP8X4),
+                lhsT_scale=h_scales[:, g, :],
+                rhs=w_con_codes[:, g, :].bitcast(FP8X4),
+                rhs_scale=w_con_scales[:, g, :],
+                start=(g == 0),
+                stop=(g == 1),
+            )
+        out_sb = keep.tile([P, D_OUT], F32)
+        nc.vector.tensor_tensor(out=out_sb[:], in0=out_ps[:], in1=out_bias[:], op=ALU.add)
+        nc.sync.dma_start(out=out.flatten_outer_dims(), in_=out_sb[:])

@@ -19,50 +19,50 @@ D_OUT = 512
 FEATURE_BITS = 10
 STAGES = 2 * FEATURE_BITS
 CHUNKS = 8
-CHUNK_BITS = 3
 PACK = 4
-LAYOUTS = 7
+W_EXP_BLOCKS = 4
 
 FLOPS = 2 * TOKENS * D_IN * HIDDEN + 2 * TOKENS * HIDDEN * D_OUT + STAGES * TOKENS * HIDDEN * 3
 
-PAIR_ORDER = ((0, 2, 4, 6), (0, 1, 4, 5), (0, 2, 1, 3))
-FILL_ORDER = (1, 3, 0, 2, 5, 7, 4, 6)
+
+def place_of(s):
+    st = s % FEATURE_BITS
+    if st == 0:
+        return (0 if s == 0 else 4), 0
+    turned = st - 1 + (0 if s < FEATURE_BITS else FEATURE_BITS - 1)
+    return turned // 2, 1 + turned % 2
 
 
 def free_pair_bits(s):
     st = s % FEATURE_BITS
+    layout, own = place_of(s)
     found = []
-    for j in range(CHUNK_BITS):
-        feature_bit = (s - s % CHUNK_BITS + j) % FEATURE_BITS
-        if feature_bit != st:
+    for j in range(3):
+        if j != own:
+            feature_bit = 0 if j == 0 else 1 + (2 * layout + j - 1) % (FEATURE_BITS - 1)
             found.append((feature_bit if feature_bit < st else feature_bit - 1, j))
     return sorted(found)
-
-
-def load_pair_weights(nc, queue, dst, stage_weights, s):
-    (low, j_low), (high, j_high) = free_pair_bits(s)
-    if high == low + 1:
-        n_lo = 2**low
-        n_hi = P // n_lo
-        if n_lo <= n_hi:
-            view = stage_weights.rearrange("(hi g lo) r c -> lo hi g (r c)", g=4, lo=n_lo)
-            for lo in range(n_lo):
-                queue.dma_start(out=dst[lo * n_hi : (lo + 1) * n_hi], in_=view[lo])
-        else:
-            view = stage_weights.rearrange("(hi g lo) r c -> hi lo g (r c)", g=4, lo=n_lo)
-            for hi in range(n_hi):
-                queue.dma_start(out=dst[hi:P:n_hi], in_=view[hi])
-    else:
-        assert (low, high) == (0, 8)
-        queue.dma_start(
-            out=dst.rearrange("p (x y) e -> p x (y e)", x=2),
-            in_=stage_weights.rearrange("(x p y) r c -> p x (y r c)", x=2, y=2),
-        )
 
 
 def group_of(s, chunk):
     (low, j_low), (high, j_high) = free_pair_bits(s)
     return 2 * ((chunk >> j_high) & 1) + ((chunk >> j_low) & 1)
+
+
+def load_pair_weights(queue, dst, stage_weights, s):
+    (low, j_low), (high, j_high) = free_pair_bits(s)
+    assert low == 0
+    n_mid = 2 ** (high - 1)
+    n_top = P // n_mid
+    dst = dst.rearrange("p (x y) e -> p x (y e)", x=2)
+    if n_mid <= n_top:
+        view = stage_weights.rearrange("(top x mid y) r c -> mid top x (y r c)", x=2, y=2, mid=n_mid)
+        for mid in range(n_mid):
+            queue.dma_start(out=dst[mid * n_top : (mid + 1) * n_top], in_=view[mid])
+    else:
+        view = stage_weights.rearrange("(top x mid y) r c -> top mid x (y r c)", x=2, y=2, mid=n_mid)
+        for top in range(n_top):
+            queue.dma_start(out=dst[top:P:n_top], in_=view[top])
 
 
 def tile_butterflymlp_s_kernel(
@@ -76,39 +76,40 @@ def tile_butterflymlp_s_kernel(
         products = ctx.enter_context(tc.tile_pool(name="products", bufs=4))
         psum = ctx.enter_context(tc.psum_pool(name="psum", bufs=1))
 
-        x_sb = keep.tile([P, D_IN], BF16)
-        nc.sync.dma_start(out=x_sb[:], in_=x.flatten_outer_dims())
-        w_exp_raw = keep.tile([P, PACK, HIDDEN], BF16)
-        for u in range(2):
-            nc.sync.dma_start(
-                out=w_exp_raw[:, 2 * u : 2 * u + 2, :],
-                in_=W_exp[256 * u : 256 * u + 256, :].rearrange("(q e) c -> q e c", e=2),
-            )
-
         pair_w_bf = keep.tile([P, STAGES, 4, 4], BF16)
         b_exp_bf = keep.tile([P, CHUNKS], BF16)
         up_bias_bf = keep.tile([P, 2, 4], BF16)
+        x_sb = keep.tile([P, D_IN], BF16)
+        w_exp_raw = keep.tile([P, PACK, HIDDEN], BF16)
         w_con_raw = keep.tile([P, 2, PACK, D_OUT], BF16)
         b_con_rows = keep.tile([P, D_OUT], BF16)
         down_bias_rows = keep.tile([P, D_OUT], BF16)
 
         def load_stage(queue, s):
             weights = up_weights if s < FEATURE_BITS else down_weights
-            load_pair_weights(nc, queue, pair_w_bf[:, s], weights[s % FEATURE_BITS], s)
+            load_pair_weights(queue, pair_w_bf[:, s], weights[s % FEATURE_BITS], s)
 
         for s in range(0, 3):
             load_stage(nc.scalar, s)
         nc.scalar.dma_start(out=b_exp_bf[:], in_=b_exp.rearrange("(p c) -> p c", c=CHUNKS))
-        for s in range(3, 6):
+        nc.sync.dma_start(out=x_sb[:], in_=x.flatten_outer_dims())
+        block = HIDDEN // W_EXP_BLOCKS
+        for i in range(W_EXP_BLOCKS):
+            for u in range(2):
+                nc.sync.dma_start(
+                    out=w_exp_raw[:, 2 * u : 2 * u + 2, block * i : block * (i + 1)],
+                    in_=W_exp[256 * u : 256 * u + 256, block * i : block * (i + 1)].rearrange("(q e) c -> q e c", e=2),
+                )
+        for s in range(3, 5):
             load_stage(nc.sync, s)
         nc.sync.dma_start(
             out=w_con_raw[:].rearrange("p g (u e) c -> p (g u) (e c)", u=2),
             in_=W_con.rearrange("(a q e) c -> q a (e c)", a=4, e=2),
         )
-        for s in range(6, 10):
+        for s in range(5, 12):
             load_stage(nc.sync, s)
         nc.sync.dma_start(out=up_bias_bf[:], in_=up_bias.rearrange("(h p l) -> p h l", h=2, l=4))
-        for s in range(10, STAGES):
+        for s in range(12, STAGES):
             load_stage(nc.sync, s)
         nc.sync.dma_start(out=b_con_rows[:], in_=b_con.partition_broadcast(P))
         nc.sync.dma_start(out=down_bias_rows[:], in_=down_bias.partition_broadcast(P))
@@ -119,16 +120,14 @@ def tile_butterflymlp_s_kernel(
         gelu_of_zero = keep.tile([P, 1], F32)
         nc.vector.memset(zero_column[:], 0.0)
         nc.scalar.activation(out=gelu_of_zero[:], in_=zero_column[:], func=ACT.Gelu)
-
         out_bias = keep.tile([P, D_OUT], F32)
         nc.gpsimd.tensor_tensor(out=out_bias[:], in0=b_con_rows[:], in1=down_bias_rows[:], op=ALU.add)
 
         pair_w = keep.tile([P, STAGES, 4, 4], F32)
 
         def widen_pair_weights(layout):
-            first = CHUNK_BITS * layout
-            last = min(first + CHUNK_BITS, STAGES)
-            nc.vector.tensor_copy(out=pair_w[:, first:last], in_=pair_w_bf[:, first:last])
+            mine = [s for s in range(STAGES) if place_of(s)[0] == layout]
+            nc.vector.tensor_copy(out=pair_w[:, mine[0] : mine[-1] + 1], in_=pair_w_bf[:, mine[0] : mine[-1] + 1])
 
         widen_pair_weights(0)
         b_exp_f = keep.tile([P, 4, 2], F32)
@@ -147,7 +146,7 @@ def tile_butterflymlp_s_kernel(
         up_bias_f = keep.tile([P, 2, 4], F32)
 
         x_words = x_sb[:].bitcast(F32)
-        x_t = psum.tile([P, 2, TOKENS], F32, tag="tok0")
+        x_t = psum.tile([P, 2, TOKENS], F32, tag="flipped00")
         for u in range(2):
             nc.tensor.transpose(x_t[:, u, :], x_words[:, P * u : P * u + P], identity[:])
         x_grouped = keep.tile([P, TOKENS, 2], F32, align_bytes=64)
@@ -159,14 +158,16 @@ def tile_butterflymlp_s_kernel(
         w_exp_view = w_exp_raw[:].rearrange("p t (m c) -> p c m t", c=CHUNKS)
         w_exp_codes = keep.tile([P, CHUNKS, P], U32, align_bytes=64)
         w_exp_scales = keep.tile([P, CHUNKS, P], U8, align_bytes=64)
-        nc.scalar.copy(out=w_exp_grouped[:, 6:8], in_=w_exp_view[:, 6:8])
-        nc.vector.tensor_copy(out=w_exp_grouped[:, 0:4], in_=w_exp_view[:, 0:4])
-        nc.vector.quantize_mx(
-            out=x_codes[:].bitcast(FP8X4),
-            scales=x_scales[:],
-            in_=x_grouped[:].rearrange("p t u -> p (t u)").bitcast(BF16),
-        )
-        nc.vector.tensor_copy(out=w_exp_grouped[:, 4:6], in_=w_exp_view[:, 4:6])
+        for i in range(W_EXP_BLOCKS):
+            columns = slice(P // W_EXP_BLOCKS * i, P // W_EXP_BLOCKS * (i + 1))
+            copy = nc.scalar.copy if i == W_EXP_BLOCKS - 2 else nc.vector.tensor_copy
+            copy(out=w_exp_grouped[:, :, columns, :], in_=w_exp_view[:, :, columns, :])
+            if i == 0:
+                nc.vector.quantize_mx(
+                    out=x_codes[:].bitcast(FP8X4),
+                    scales=x_scales[:],
+                    in_=x_grouped[:].rearrange("p t u -> p (t u)").bitcast(BF16),
+                )
         for half in range(2):
             chunks = slice(4 * half, 4 * half + 4)
             nc.vector.quantize_mx(
@@ -175,12 +176,17 @@ def tile_butterflymlp_s_kernel(
                 in_=w_exp_grouped[:, chunks].rearrange("p c m t -> p (c m t)"),
             )
 
-        def new_psum_chunks():
-            banks = [psum.tile([P, 2, TOKENS], F32, tag="chunks%d" % i, name="chunks%d" % i) for i in range(4)]
-            return [banks[2 * (c >> 2) + (c & 1)][:, (c >> 1) & 1, :] for c in range(CHUNKS)]
+        chunk = [None] * CHUNKS
 
-        chunk = new_psum_chunks()
-        for c in FILL_ORDER:
+        def new_psum_chunks(z, bank_bit):
+            banks = [psum.tile([P, 2, TOKENS], F32, tag="chunks%d%d" % (z, i), name="chunks%d%d" % (z, i)) for i in range(2)]
+            for y in range(4):
+                bank, place = ((y & 1), (y >> 1)) if bank_bit == 0 else ((y >> 1), (y & 1))
+                chunk[2 * y + z] = banks[bank][:, place, :]
+
+        for z in range(2):
+            new_psum_chunks(z, 1)
+        for c in (1, 3, 0, 2, 5, 7, 4, 6):
             nc.tensor.matmul_mx(
                 out=chunk[c],
                 lhsT=w_exp_codes[:, c, :].bitcast(FP8X4),
@@ -195,31 +201,26 @@ def tile_butterflymlp_s_kernel(
         w_con_codes = keep.tile([P, 2, D_OUT], U32, align_bytes=64)
         w_con_scales = keep.tile([P, 2, D_OUT], U8, align_bytes=64)
 
-        def regroup_w_con(quarter):
-            g, half = divmod(quarter, 2)
-            cols = slice(256 * half, 256 * half + 256)
-            nc.vector.tensor_copy(
-                out=w_con_grouped[:, g, cols, :].rearrange("p (c i) t -> p c t i", i=4),
-                in_=w_con_raw[:, g, :, cols].rearrange("p t (c i) -> p c t i", i=4),
-            )
+        def prepare_w_con(step):
+            if step < 4:
+                g, half = divmod(step, 2)
+                cols = slice(256 * half, 256 * half + 256)
+                nc.vector.tensor_copy(
+                    out=w_con_grouped[:, g, cols, :].rearrange("p (c i) t -> p c t i", i=4),
+                    in_=w_con_raw[:, g, :, cols].rearrange("p t (c i) -> p c t i", i=4),
+                )
+            else:
+                g = step - 4
+                nc.vector.quantize_mx(
+                    out=w_con_codes[:, g, :].bitcast(FP8X4),
+                    scales=w_con_scales[:, g, :],
+                    in_=w_con_grouped[:, g].rearrange("p c t -> p (c t)"),
+                )
 
-        def quantise_w_con():
-            nc.vector.quantize_mx(
-                out=w_con_codes[:].rearrange("p g c -> p (g c)").bitcast(FP8X4),
-                scales=w_con_scales[:].rearrange("p g c -> p (g c)"),
-                in_=w_con_grouped[:].rearrange("p g c t -> p (g c t)"),
-            )
-
-        def stage(s, chunk, bias_of, gelu):
-            j = s % CHUNK_BITS
-            new = data.tile([P, CHUNKS, TOKENS], F32, tag="chunks")
-            order = PAIR_ORDER[j]
-
-            def apply_gelu(a):
-                nc.scalar.activation(out=new[:, a : a + 2, :], in_=new[:, a : a + 2, :], func=ACT.Gelu)
-
-            for i, a in enumerate(order):
-                b = a | (1 << j)
+        def stage(s, firsts, new, bias_of=None):
+            own = place_of(s)[1]
+            for a in firsts:
+                b = a | (1 << own)
                 w = pair_w[:, s, group_of(s, a)]
                 prod = products.tile([P, 2, TOKENS], F32, tag="prod")
                 for r, c in enumerate((a, b)):
@@ -232,66 +233,99 @@ def tile_butterflymlp_s_kernel(
                     )
                 for r, c in enumerate((a, b)):
                     nc.vector.scalar_tensor_tensor(
-                        out=new[:, c, :],
+                        out=new[c],
                         in0=chunk[a],
                         scalar=w[:, 2 * r : 2 * r + 1],
                         in1=prod[:, r, :],
                         op0=ALU.mult,
                         op1=ALU.add,
                     )
-                if gelu and i > 0:
-                    apply_gelu(order[i - 1])
-            if gelu:
-                apply_gelu(order[-1])
-            return new
+            for a in firsts:
+                chunk[a] = new[a]
+                chunk[a | (1 << own)] = new[a | (1 << own)]
 
-        def next_layout(chunk, layout):
-            by_token = data.tile([P, CHUNKS, CHUNKS, 16], F32, tag="by_token")
-            for i, a in enumerate(PAIR_ORDER[2]):
-                flipped = psum.tile([P, 2, P], F32, tag="tok%d" % i, name="flipped%d" % i)
-                nc.tensor.transpose(flipped[:, 0, :], chunk[a], identity[:])
-                nc.tensor.transpose(flipped[:, 1, :], chunk[a + 4], identity[:])
-                copy = nc.scalar.copy if i < 3 else nc.vector.tensor_copy
+        def new_half(z):
+            return data.tile([P, 4, TOKENS], F32, tag="half%d" % z, name="half%d" % z)
+
+        def stage_on_both(s, bias_of=None):
+            halves = [new_half(z) for z in range(2)]
+            stage(s, (0, 2, 4, 6), [halves[c & 1][:, c >> 1, :] for c in range(CHUNKS)], bias_of)
+
+        flipped = [None, None]
+
+        def start_turn(z):
+            flipped[z] = []
+            for y0 in range(2):
+                bank = psum.tile([P, 2, P], F32, tag="flipped%d%d" % (z, y0), name="flipped%d%d" % (z, y0))
+                for y1 in range(2):
+                    nc.tensor.transpose(bank[:, y1, :], chunk[4 * y1 + 2 * y0 + z], identity[:])
+                flipped[z].append(bank)
+
+        def finish_turn(z, layout):
+            by_token = data.tile([P, 4, 4, 32], F32, tag="by_token%d" % z, name="by_token%d" % z)
+            for y0, copy in enumerate((nc.scalar.copy, nc.vector.tensor_copy)):
                 copy(
-                    out=by_token[:, :, a : a + 5 : 4, :],
-                    in_=flipped[:].rearrange("t s (hi lo) -> t lo s hi", lo=CHUNKS),
+                    out=by_token[:, :, y0 : y0 + 3 : 2, :],
+                    in_=flipped[z][y0][:].rearrange("t y1 (hi lo) -> t lo y1 hi", lo=4),
                 )
-            new = new_psum_chunks()
-            for c in FILL_ORDER:
-                nc.tensor.transpose(new[c], by_token[:, c].rearrange("t c hi -> t (c hi)"), identity[:])
-            widen_pair_weights(layout)
-            if layout == 3:
-                nc.vector.tensor_copy(out=up_bias_f[:], in_=up_bias_bf[:])
-            if 2 <= layout <= 5:
-                regroup_w_con(layout - 2)
-            if layout == 6:
-                quantise_w_con()
-            return new
+            flipped[z] = None
+            new_psum_chunks(z, 0)
+            for y in (1, 3, 0, 2):
+                nc.tensor.transpose(chunk[2 * y + z], by_token[:, y].rearrange("t y hi -> t (y hi)"), identity[:])
+            if z == 0:
+                widen_pair_weights(layout)
+                if layout == 4:
+                    nc.vector.tensor_copy(out=up_bias_f[:], in_=up_bias_bf[:])
+            step = 2 * (layout - 2) + z
+            if 0 <= step < 6:
+                prepare_w_con(step)
 
-        for s in range(STAGES):
-            if s > 0 and s % CHUNK_BITS == 0:
-                chunk = next_layout(chunk, s // CHUNK_BITS)
-            if s == 0:
-                hidden = stage(s, chunk, lambda c: stage0_bias[:, c >> 1, (c & 1) : (c & 1) + 1], False)
-            elif s == FEATURE_BITS - 1:
-                hidden = stage(s, chunk, lambda c: up_bias_f[:, c & 1, (c >> 1) : (c >> 1) + 1], True)
-            else:
-                hidden = stage(s, chunk, None, False)
-            chunk = [hidden[:, c, :] for c in range(CHUNKS)]
+        def run(z, stages, last=None):
+            for i, s in enumerate(stages):
+                own = place_of(s)[1]
+                firsts = (z, z + 4) if own == 1 else (z, z + 2)
+                bias_of = None
+                if s == FEATURE_BITS - 1:
+                    bias_of = lambda c: up_bias_f[:, (c >> 1) & 1, 2 * (c >> 2) + (c & 1) : 2 * (c >> 2) + (c & 1) + 1]
+                half = last if last is not None and i == len(stages) - 1 else new_half(z)
+                stage(s, firsts, [half[:, c >> 1, :] for c in range(CHUNKS)], bias_of)
+                if i == 0 and flipped[1 - z]:
+                    finish_turn(1 - z, place_of(s)[0] + z)
+            return half
 
-        h_view = hidden[:].rearrange("p (e g u) t -> p g t u e", e=2, g=2, u=2)
+        stage_on_both(0, lambda c: stage0_bias[:, c >> 1, (c & 1) : (c & 1) + 1])
+        for layout in range(0, 4):
+            for z in range(2):
+                run(z, (2 * layout + 1, 2 * layout + 2))
+                start_turn(z)
+        for z in range(2):
+            half = run(z, (9,))
+            nc.scalar.activation(out=half[:], in_=half[:], func=ACT.Gelu)
+        stage_on_both(10)
+        for z in range(2):
+            run(z, (11,))
+            start_turn(z)
+        hidden = keep.tile([P, CHUNKS, TOKENS], F32)
+        for layout in range(5, 9):
+            for z in range(2):
+                if layout < 8:
+                    run(z, (2 * layout + 2, 2 * layout + 3))
+                    start_turn(z)
+                else:
+                    run(z, (2 * layout + 2, 2 * layout + 3), hidden[:].rearrange("p (y z) t -> p z y t", z=2)[:, z])
+
         h_grouped = keep.tile([P, 2, TOKENS, PACK], BF16, align_bytes=64)
         h_codes = keep.tile([P, 2, TOKENS], U32, align_bytes=64)
         h_scales = keep.tile([P, 2, TOKENS], U8, align_bytes=64)
-        nc.vector.tensor_copy(out=h_grouped[:, 0].rearrange("p t (u e) -> p t u e", u=2), in_=h_view[:, 0])
-        nc.scalar.copy(out=h_grouped[:, 1].rearrange("p t (u e) -> p t u e", u=2), in_=h_view[:, 1])
-        nc.vector.quantize_mx(
-            out=h_codes[:].rearrange("p g t -> p (g t)").bitcast(FP8X4),
-            scales=h_scales[:].rearrange("p g t -> p (g t)"),
-            in_=h_grouped[:].rearrange("p g t k -> p (g t k)"),
-        )
-        out_ps = psum.tile([P, D_OUT], F32, tag="tok1")
+        for g, copy in enumerate((nc.scalar.copy, nc.vector.tensor_copy)):
+            copy(out=h_grouped[:, g], in_=hidden[:, PACK * g : PACK * (g + 1), :].rearrange("p k t -> p t k"))
+        out_ps = psum.tile([P, D_OUT], F32, tag="flipped01")
         for g in range(2):
+            nc.vector.quantize_mx(
+                out=h_codes[:, g, :].bitcast(FP8X4),
+                scales=h_scales[:, g, :],
+                in_=h_grouped[:, g].rearrange("p t k -> p (t k)"),
+            )
             nc.tensor.matmul_mx(
                 out=out_ps[:],
                 lhsT=h_codes[:, g, :].bitcast(FP8X4),

@@ -19,50 +19,50 @@ D_OUT = 512
 FEATURE_BITS = 10
 STAGES = 2 * FEATURE_BITS
 CHUNKS = 8
+CHUNK_BITS = 3
 PACK = 4
-W_EXP_BLOCKS = 4
+LAYOUTS = 7
 
 FLOPS = 2 * TOKENS * D_IN * HIDDEN + 2 * TOKENS * HIDDEN * D_OUT + STAGES * TOKENS * HIDDEN * 3
 
-
-def place_of(s):
-    st = s % FEATURE_BITS
-    if st == 0:
-        return (0 if s == 0 else 4), 0
-    turned = st - 1 + (0 if s < FEATURE_BITS else FEATURE_BITS - 1)
-    return turned // 2, 1 + turned % 2
+PAIR_ORDER = ((0, 2, 4, 6), (0, 1, 4, 5), (0, 2, 1, 3))
+FILL_ORDER = (1, 3, 0, 2, 5, 7, 4, 6)
 
 
 def free_pair_bits(s):
     st = s % FEATURE_BITS
-    layout, own = place_of(s)
     found = []
-    for j in range(3):
-        if j != own:
-            feature_bit = 0 if j == 0 else 1 + (2 * layout + j - 1) % (FEATURE_BITS - 1)
+    for j in range(CHUNK_BITS):
+        feature_bit = (s - s % CHUNK_BITS + j) % FEATURE_BITS
+        if feature_bit != st:
             found.append((feature_bit if feature_bit < st else feature_bit - 1, j))
     return sorted(found)
+
+
+def load_pair_weights(nc, queue, dst, stage_weights, s):
+    (low, j_low), (high, j_high) = free_pair_bits(s)
+    if high == low + 1:
+        n_lo = 2**low
+        n_hi = P // n_lo
+        if n_lo <= n_hi:
+            view = stage_weights.rearrange("(hi g lo) r c -> lo hi g (r c)", g=4, lo=n_lo)
+            for lo in range(n_lo):
+                queue.dma_start(out=dst[lo * n_hi : (lo + 1) * n_hi], in_=view[lo])
+        else:
+            view = stage_weights.rearrange("(hi g lo) r c -> hi lo g (r c)", g=4, lo=n_lo)
+            for hi in range(n_hi):
+                queue.dma_start(out=dst[hi:P:n_hi], in_=view[hi])
+    else:
+        assert (low, high) == (0, 8)
+        queue.dma_start(
+            out=dst.rearrange("p (x y) e -> p x (y e)", x=2),
+            in_=stage_weights.rearrange("(x p y) r c -> p x (y r c)", x=2, y=2),
+        )
 
 
 def group_of(s, chunk):
     (low, j_low), (high, j_high) = free_pair_bits(s)
     return 2 * ((chunk >> j_high) & 1) + ((chunk >> j_low) & 1)
-
-
-def load_pair_weights(queue, dst, stage_weights, s):
-    (low, j_low), (high, j_high) = free_pair_bits(s)
-    assert low == 0
-    n_mid = 2 ** (high - 1)
-    n_top = P // n_mid
-    dst = dst.rearrange("p (x y) e -> p x (y e)", x=2)
-    if n_mid <= n_top:
-        view = stage_weights.rearrange("(top x mid y) r c -> mid top x (y r c)", x=2, y=2, mid=n_mid)
-        for mid in range(n_mid):
-            queue.dma_start(out=dst[mid * n_top : (mid + 1) * n_top], in_=view[mid])
-    else:
-        view = stage_weights.rearrange("(top x mid y) r c -> top mid x (y r c)", x=2, y=2, mid=n_mid)
-        for top in range(n_top):
-            queue.dma_start(out=dst[top:P:n_top], in_=view[top])
 
 
 def tile_butterflymlp_s_kernel(
@@ -76,40 +76,40 @@ def tile_butterflymlp_s_kernel(
         products = ctx.enter_context(tc.tile_pool(name="products", bufs=4))
         psum = ctx.enter_context(tc.psum_pool(name="psum", bufs=1))
 
+        x_sb = keep.tile([P, D_IN], BF16)
+        w_exp_raw = keep.tile([P, PACK, HIDDEN], BF16)
         pair_w_bf = keep.tile([P, STAGES, 4, 4], BF16)
         b_exp_bf = keep.tile([P, CHUNKS], BF16)
         up_bias_bf = keep.tile([P, 2, 4], BF16)
-        x_sb = keep.tile([P, D_IN], BF16)
-        w_exp_raw = keep.tile([P, PACK, HIDDEN], BF16)
         w_con_raw = keep.tile([P, 2, PACK, D_OUT], BF16)
         b_con_rows = keep.tile([P, D_OUT], BF16)
         down_bias_rows = keep.tile([P, D_OUT], BF16)
 
         def load_stage(queue, s):
             weights = up_weights if s < FEATURE_BITS else down_weights
-            load_pair_weights(queue, pair_w_bf[:, s], weights[s % FEATURE_BITS], s)
+            load_pair_weights(nc, queue, pair_w_bf[:, s], weights[s % FEATURE_BITS], s)
 
         for s in range(0, 3):
             load_stage(nc.scalar, s)
         nc.scalar.dma_start(out=b_exp_bf[:], in_=b_exp.rearrange("(p c) -> p c", c=CHUNKS))
         nc.sync.dma_start(out=x_sb[:], in_=x.flatten_outer_dims())
-        block = HIDDEN // W_EXP_BLOCKS
-        for i in range(W_EXP_BLOCKS):
+        for side in range(2):
+            cols = slice(HIDDEN // 2 * side, HIDDEN // 2 * (side + 1))
             for u in range(2):
                 nc.sync.dma_start(
-                    out=w_exp_raw[:, 2 * u : 2 * u + 2, block * i : block * (i + 1)],
-                    in_=W_exp[256 * u : 256 * u + 256, block * i : block * (i + 1)].rearrange("(q e) c -> q e c", e=2),
+                    out=w_exp_raw[:, 2 * u : 2 * u + 2, cols],
+                    in_=W_exp[256 * u : 256 * u + 256, cols].rearrange("(q e) c -> q e c", e=2),
                 )
-        for s in range(3, 5):
+        for s in range(3, 6):
             load_stage(nc.sync, s)
         nc.sync.dma_start(
             out=w_con_raw[:].rearrange("p g (u e) c -> p (g u) (e c)", u=2),
             in_=W_con.rearrange("(a q e) c -> q a (e c)", a=4, e=2),
         )
-        for s in range(5, 12):
+        for s in range(6, 10):
             load_stage(nc.sync, s)
         nc.sync.dma_start(out=up_bias_bf[:], in_=up_bias.rearrange("(h p l) -> p h l", h=2, l=4))
-        for s in range(12, STAGES):
+        for s in range(10, STAGES):
             load_stage(nc.sync, s)
         nc.sync.dma_start(out=b_con_rows[:], in_=b_con.partition_broadcast(P))
         nc.sync.dma_start(out=down_bias_rows[:], in_=down_bias.partition_broadcast(P))
@@ -120,14 +120,16 @@ def tile_butterflymlp_s_kernel(
         gelu_of_zero = keep.tile([P, 1], F32)
         nc.vector.memset(zero_column[:], 0.0)
         nc.scalar.activation(out=gelu_of_zero[:], in_=zero_column[:], func=ACT.Gelu)
+
         out_bias = keep.tile([P, D_OUT], F32)
         nc.gpsimd.tensor_tensor(out=out_bias[:], in0=b_con_rows[:], in1=down_bias_rows[:], op=ALU.add)
 
         pair_w = keep.tile([P, STAGES, 4, 4], F32)
 
         def widen_pair_weights(layout):
-            mine = [s for s in range(STAGES) if place_of(s)[0] == layout]
-            nc.vector.tensor_copy(out=pair_w[:, mine[0] : mine[-1] + 1], in_=pair_w_bf[:, mine[0] : mine[-1] + 1])
+            first = CHUNK_BITS * layout
+            last = min(first + CHUNK_BITS, STAGES)
+            nc.vector.tensor_copy(out=pair_w[:, first:last], in_=pair_w_bf[:, first:last])
 
         widen_pair_weights(0)
         b_exp_f = keep.tile([P, 4, 2], F32)
@@ -146,7 +148,7 @@ def tile_butterflymlp_s_kernel(
         up_bias_f = keep.tile([P, 2, 4], F32)
 
         x_words = x_sb[:].bitcast(F32)
-        x_t = psum.tile([P, 2, TOKENS], F32, tag="flipped00")
+        x_t = psum.tile([P, 2, TOKENS], F32, tag="tok0")
         for u in range(2):
             nc.tensor.transpose(x_t[:, u, :], x_words[:, P * u : P * u + P], identity[:])
         x_grouped = keep.tile([P, TOKENS, 2], F32, align_bytes=64)
@@ -155,19 +157,20 @@ def tile_butterflymlp_s_kernel(
         x_scales = keep.tile([P, TOKENS], U8, align_bytes=64)
 
         w_exp_grouped = keep.tile([P, CHUNKS, P, PACK], BF16, align_bytes=64)
-        w_exp_view = w_exp_raw[:].rearrange("p t (m c) -> p c m t", c=CHUNKS)
+        w_exp_from = w_exp_raw[:].rearrange("p t (m c) -> p m t c", c=CHUNKS)
+        w_exp_to = w_exp_grouped[:].rearrange("p c m t -> p m t c")
         w_exp_codes = keep.tile([P, CHUNKS, P], U32, align_bytes=64)
         w_exp_scales = keep.tile([P, CHUNKS, P], U8, align_bytes=64)
-        for i in range(W_EXP_BLOCKS):
-            columns = slice(P // W_EXP_BLOCKS * i, P // W_EXP_BLOCKS * (i + 1))
-            copy = nc.scalar.copy if i == W_EXP_BLOCKS - 2 else nc.vector.tensor_copy
-            copy(out=w_exp_grouped[:, :, columns, :], in_=w_exp_view[:, :, columns, :])
-            if i == 0:
-                nc.vector.quantize_mx(
-                    out=x_codes[:].bitcast(FP8X4),
-                    scales=x_scales[:],
-                    in_=x_grouped[:].rearrange("p t u -> p (t u)").bitcast(BF16),
-                )
+        left, right = slice(0, P // 2), slice(P // 2, P)
+        nc.vector.tensor_copy(out=w_exp_to[:, left, :, 0:4], in_=w_exp_from[:, left, :, 0:4])
+        nc.vector.quantize_mx(
+            out=x_codes[:].bitcast(FP8X4),
+            scales=x_scales[:],
+            in_=x_grouped[:].rearrange("p t u -> p (t u)").bitcast(BF16),
+        )
+        nc.vector.tensor_copy(out=w_exp_to[:, left, :, 4:8], in_=w_exp_from[:, left, :, 4:8])
+        nc.scalar.copy(out=w_exp_to[:, right, :, 4:8], in_=w_exp_from[:, right, :, 4:8])
+        nc.vector.tensor_copy(out=w_exp_to[:, right, :, 0:4], in_=w_exp_from[:, right, :, 0:4])
         for half in range(2):
             chunks = slice(4 * half, 4 * half + 4)
             nc.vector.quantize_mx(
@@ -176,17 +179,12 @@ def tile_butterflymlp_s_kernel(
                 in_=w_exp_grouped[:, chunks].rearrange("p c m t -> p (c m t)"),
             )
 
-        chunk = [None] * CHUNKS
+        def new_psum_chunks():
+            banks = [psum.tile([P, 2, TOKENS], F32, tag="chunks%d" % i, name="chunks%d" % i) for i in range(4)]
+            return [banks[2 * (c >> 2) + (c & 1)][:, (c >> 1) & 1, :] for c in range(CHUNKS)]
 
-        def new_psum_chunks(z, bank_bit):
-            banks = [psum.tile([P, 2, TOKENS], F32, tag="chunks%d%d" % (z, i), name="chunks%d%d" % (z, i)) for i in range(2)]
-            for y in range(4):
-                bank, place = ((y & 1), (y >> 1)) if bank_bit == 0 else ((y >> 1), (y & 1))
-                chunk[2 * y + z] = banks[bank][:, place, :]
-
-        for z in range(2):
-            new_psum_chunks(z, 1)
-        for c in (1, 3, 0, 2, 5, 7, 4, 6):
+        chunk = new_psum_chunks()
+        for c in FILL_ORDER:
             nc.tensor.matmul_mx(
                 out=chunk[c],
                 lhsT=w_exp_codes[:, c, :].bitcast(FP8X4),
@@ -201,26 +199,31 @@ def tile_butterflymlp_s_kernel(
         w_con_codes = keep.tile([P, 2, D_OUT], U32, align_bytes=64)
         w_con_scales = keep.tile([P, 2, D_OUT], U8, align_bytes=64)
 
-        def prepare_w_con(step):
-            if step < 4:
-                g, half = divmod(step, 2)
-                cols = slice(256 * half, 256 * half + 256)
-                nc.vector.tensor_copy(
-                    out=w_con_grouped[:, g, cols, :].rearrange("p (c i) t -> p c t i", i=4),
-                    in_=w_con_raw[:, g, :, cols].rearrange("p t (c i) -> p c t i", i=4),
-                )
-            else:
-                g = step - 4
-                nc.vector.quantize_mx(
-                    out=w_con_codes[:, g, :].bitcast(FP8X4),
-                    scales=w_con_scales[:, g, :],
-                    in_=w_con_grouped[:, g].rearrange("p c t -> p (c t)"),
-                )
+        def regroup_w_con(quarter):
+            g, half = divmod(quarter, 2)
+            cols = slice(256 * half, 256 * half + 256)
+            nc.vector.tensor_copy(
+                out=w_con_grouped[:, g, cols, :].rearrange("p (c i) t -> p c t i", i=4),
+                in_=w_con_raw[:, g, :, cols].rearrange("p t (c i) -> p c t i", i=4),
+            )
 
-        def stage(s, firsts, new, bias_of=None):
-            own = place_of(s)[1]
-            for a in firsts:
-                b = a | (1 << own)
+        def quantise_w_con():
+            nc.vector.quantize_mx(
+                out=w_con_codes[:].rearrange("p g c -> p (g c)").bitcast(FP8X4),
+                scales=w_con_scales[:].rearrange("p g c -> p (g c)"),
+                in_=w_con_grouped[:].rearrange("p g c t -> p (g c t)"),
+            )
+
+        def stage(s, chunk, bias_of, gelu):
+            j = s % CHUNK_BITS
+            new = data.tile([P, CHUNKS, TOKENS], F32, tag="chunks")
+            order = PAIR_ORDER[j]
+
+            def apply_gelu(a):
+                nc.scalar.activation(out=new[:, a : a + 2, :], in_=new[:, a : a + 2, :], func=ACT.Gelu)
+
+            for i, a in enumerate(order):
+                b = a | (1 << j)
                 w = pair_w[:, s, group_of(s, a)]
                 prod = products.tile([P, 2, TOKENS], F32, tag="prod")
                 for r, c in enumerate((a, b)):
@@ -233,93 +236,60 @@ def tile_butterflymlp_s_kernel(
                     )
                 for r, c in enumerate((a, b)):
                     nc.vector.scalar_tensor_tensor(
-                        out=new[c],
+                        out=new[:, c, :],
                         in0=chunk[a],
                         scalar=w[:, 2 * r : 2 * r + 1],
                         in1=prod[:, r, :],
                         op0=ALU.mult,
                         op1=ALU.add,
                     )
-            for a in firsts:
-                chunk[a] = new[a]
-                chunk[a | (1 << own)] = new[a | (1 << own)]
+                if gelu and i > 0:
+                    apply_gelu(order[i - 1])
+            if gelu:
+                apply_gelu(order[-1])
+            return new
 
-        def new_half(z):
-            return data.tile([P, 4, TOKENS], F32, tag="half%d" % z, name="half%d" % z)
-
-        def stage_on_both(s, bias_of=None):
-            halves = [new_half(z) for z in range(2)]
-            stage(s, (0, 2, 4, 6), [halves[c & 1][:, c >> 1, :] for c in range(CHUNKS)], bias_of)
-
-        flipped = [None, None]
-
-        def start_turn(z):
-            flipped[z] = []
-            for y0 in range(2):
-                bank = psum.tile([P, 2, P], F32, tag="flipped%d%d" % (z, y0), name="flipped%d%d" % (z, y0))
-                for y1 in range(2):
-                    nc.tensor.transpose(bank[:, y1, :], chunk[4 * y1 + 2 * y0 + z], identity[:])
-                flipped[z].append(bank)
-
-        def finish_turn(z, layout):
-            by_token = data.tile([P, 4, 4, 32], F32, tag="by_token%d" % z, name="by_token%d" % z)
-            for y0, copy in enumerate((nc.scalar.copy, nc.vector.tensor_copy)):
+        def next_layout(chunk, layout):
+            by_token = data.tile([P, CHUNKS, CHUNKS, 16], F32, tag="by_token")
+            for i, a in enumerate(PAIR_ORDER[2]):
+                flipped = psum.tile([P, 2, P], F32, tag="tok%d" % i, name="flipped%d" % i)
+                nc.tensor.transpose(flipped[:, 0, :], chunk[a], identity[:])
+                nc.tensor.transpose(flipped[:, 1, :], chunk[a + 4], identity[:])
+                copy = nc.scalar.copy if i < 3 else nc.vector.tensor_copy
                 copy(
-                    out=by_token[:, :, y0 : y0 + 3 : 2, :],
-                    in_=flipped[z][y0][:].rearrange("t y1 (hi lo) -> t lo y1 hi", lo=4),
+                    out=by_token[:, :, a : a + 5 : 4, :],
+                    in_=flipped[:].rearrange("t s (hi lo) -> t lo s hi", lo=CHUNKS),
                 )
-            flipped[z] = None
-            new_psum_chunks(z, 0)
-            for y in (1, 3, 0, 2):
-                nc.tensor.transpose(chunk[2 * y + z], by_token[:, y].rearrange("t y hi -> t (y hi)"), identity[:])
-            if z == 0:
-                widen_pair_weights(layout)
-                if layout == 4:
-                    nc.vector.tensor_copy(out=up_bias_f[:], in_=up_bias_bf[:])
-            step = 2 * (layout - 2) + z
-            if 0 <= step < 6:
-                prepare_w_con(step)
+            new = new_psum_chunks()
+            for c in FILL_ORDER:
+                nc.tensor.transpose(new[c], by_token[:, c].rearrange("t c hi -> t (c hi)"), identity[:])
+            widen_pair_weights(layout)
+            if layout == 3:
+                nc.vector.tensor_copy(out=up_bias_f[:], in_=up_bias_bf[:])
+            if 2 <= layout <= 5:
+                regroup_w_con(layout - 2)
+            if layout == 6:
+                quantise_w_con()
+            return new
 
-        def run(z, stages, last=None):
-            for i, s in enumerate(stages):
-                own = place_of(s)[1]
-                firsts = (z, z + 4) if own == 1 else (z, z + 2)
-                bias_of = None
-                if s == FEATURE_BITS - 1:
-                    bias_of = lambda c: up_bias_f[:, (c >> 1) & 1, 2 * (c >> 2) + (c & 1) : 2 * (c >> 2) + (c & 1) + 1]
-                half = last if last is not None and i == len(stages) - 1 else new_half(z)
-                stage(s, firsts, [half[:, c >> 1, :] for c in range(CHUNKS)], bias_of)
-                if i == 0 and flipped[1 - z]:
-                    finish_turn(1 - z, place_of(s)[0] + z)
-            return half
+        for s in range(STAGES):
+            if s > 0 and s % CHUNK_BITS == 0:
+                chunk = next_layout(chunk, s // CHUNK_BITS)
+            if s == 0:
+                hidden = stage(s, chunk, lambda c: stage0_bias[:, c >> 1, (c & 1) : (c & 1) + 1], False)
+            elif s == FEATURE_BITS - 1:
+                hidden = stage(s, chunk, lambda c: up_bias_f[:, c & 1, (c >> 1) : (c >> 1) + 1], True)
+            else:
+                hidden = stage(s, chunk, None, False)
+            chunk = [hidden[:, c, :] for c in range(CHUNKS)]
 
-        stage_on_both(0, lambda c: stage0_bias[:, c >> 1, (c & 1) : (c & 1) + 1])
-        for layout in range(0, 4):
-            for z in range(2):
-                run(z, (2 * layout + 1, 2 * layout + 2))
-                start_turn(z)
-        for z in range(2):
-            half = run(z, (9,))
-            nc.scalar.activation(out=half[:], in_=half[:], func=ACT.Gelu)
-        stage_on_both(10)
-        for z in range(2):
-            run(z, (11,))
-            start_turn(z)
-        hidden = keep.tile([P, CHUNKS, TOKENS], F32)
-        for layout in range(5, 9):
-            for z in range(2):
-                if layout < 8:
-                    run(z, (2 * layout + 2, 2 * layout + 3))
-                    start_turn(z)
-                else:
-                    run(z, (2 * layout + 2, 2 * layout + 3), hidden[:].rearrange("p (y z) t -> p z y t", z=2)[:, z])
-
+        h_view = hidden[:].rearrange("p (e g u) t -> p g t u e", e=2, g=2, u=2)
         h_grouped = keep.tile([P, 2, TOKENS, PACK], BF16, align_bytes=64)
         h_codes = keep.tile([P, 2, TOKENS], U32, align_bytes=64)
         h_scales = keep.tile([P, 2, TOKENS], U8, align_bytes=64)
-        for g, copy in enumerate((nc.scalar.copy, nc.vector.tensor_copy)):
-            copy(out=h_grouped[:, g], in_=hidden[:, PACK * g : PACK * (g + 1), :].rearrange("p k t -> p t k"))
-        out_ps = psum.tile([P, D_OUT], F32, tag="flipped01")
+        nc.vector.tensor_copy(out=h_grouped[:, 0].rearrange("p t (u e) -> p t u e", u=2), in_=h_view[:, 0])
+        nc.scalar.copy(out=h_grouped[:, 1].rearrange("p t (u e) -> p t u e", u=2), in_=h_view[:, 1])
+        out_ps = psum.tile([P, D_OUT], F32, tag="tok1")
         for g in range(2):
             nc.vector.quantize_mx(
                 out=h_codes[:, g, :].bitcast(FP8X4),

@@ -22,6 +22,8 @@ CHUNKS = 8
 CHUNK_BITS = 3
 PACK = 4
 LAYOUTS = 7
+GELU_STAGE = FEATURE_BITS - 1
+MAX_RECIPROCAL = 2.0**40
 
 FLOPS = 2 * TOKENS * D_IN * HIDDEN + 2 * TOKENS * HIDDEN * D_OUT + STAGES * TOKENS * HIDDEN * 3
 
@@ -39,7 +41,7 @@ def free_pair_bits(s):
     return sorted(found)
 
 
-def load_pair_weights(nc, queue, dst, stage_weights, s):
+def load_pair_weights(queue, dst, stage_weights, s):
     (low, j_low), (high, j_high) = free_pair_bits(s)
     if high == low + 1:
         n_lo = 2**low
@@ -65,6 +67,11 @@ def group_of(s, chunk):
     return 2 * ((chunk >> j_high) & 1) + ((chunk >> j_low) & 1)
 
 
+def by_chunk_bits(s, view):
+    (low, j_low), (high, j_high) = free_pair_bits(s)
+    return view.rearrange("p (x y) r -> p x y r" if j_high > j_low else "p (y x) r -> p x y r", x=2)
+
+
 def tile_butterflymlp_s_kernel(
     tc, x, W_exp, b_exp, up_weights, up_bias, down_weights, W_con, b_con, down_bias, out
 ):
@@ -73,25 +80,25 @@ def tile_butterflymlp_s_kernel(
         ctx.enter_context(tc.manual_schedule())
         keep = ctx.enter_context(tc.tile_pool(name="keep", bufs=1))
         data = ctx.enter_context(tc.tile_pool(name="data", bufs=3))
-        products = ctx.enter_context(tc.tile_pool(name="products", bufs=4))
+        products = ctx.enter_context(tc.tile_pool(name="products", bufs=8))
         psum = ctx.enter_context(tc.psum_pool(name="psum", bufs=1))
 
         x_sb = keep.tile([P, D_IN], BF16)
         w_exp_raw = keep.tile([P, PACK, HIDDEN], BF16)
-        pair_w_bf = keep.tile([P, STAGES, 4, 4], BF16)
-        b_exp_bf = keep.tile([P, CHUNKS], BF16)
-        up_bias_bf = keep.tile([P, 2, 4], BF16)
+        pair_w = keep.tile([P, STAGES, 4, 4], BF16)
+        b_exp_sb = keep.tile([P, CHUNKS], BF16)
+        up_bias_sb = keep.tile([P, 2, 4], BF16)
         w_con_raw = keep.tile([P, 2, PACK, D_OUT], BF16)
         b_con_rows = keep.tile([P, D_OUT], BF16)
         down_bias_rows = keep.tile([P, D_OUT], BF16)
 
         def load_stage(queue, s):
             weights = up_weights if s < FEATURE_BITS else down_weights
-            load_pair_weights(nc, queue, pair_w_bf[:, s], weights[s % FEATURE_BITS], s)
+            load_pair_weights(queue, pair_w[:, s], weights[s % FEATURE_BITS], s)
 
         for s in range(0, 3):
             load_stage(nc.scalar, s)
-        nc.scalar.dma_start(out=b_exp_bf[:], in_=b_exp.rearrange("(p c) -> p c", c=CHUNKS))
+        nc.scalar.dma_start(out=b_exp_sb[:], in_=b_exp.rearrange("(p c) -> p c", c=CHUNKS))
         nc.sync.dma_start(out=x_sb[:], in_=x.flatten_outer_dims())
         for side in range(2):
             cols = slice(HIDDEN // 2 * side, HIDDEN // 2 * (side + 1))
@@ -108,7 +115,7 @@ def tile_butterflymlp_s_kernel(
         )
         for s in range(6, 10):
             load_stage(nc.sync, s)
-        nc.sync.dma_start(out=up_bias_bf[:], in_=up_bias.rearrange("(h p l) -> p h l", h=2, l=4))
+        nc.sync.dma_start(out=up_bias_sb[:], in_=up_bias.rearrange("(h p l) -> p h l", h=2, l=4))
         for s in range(10, STAGES):
             load_stage(nc.sync, s)
         nc.sync.dma_start(out=b_con_rows[:], in_=b_con.partition_broadcast(P))
@@ -123,29 +130,6 @@ def tile_butterflymlp_s_kernel(
 
         out_bias = keep.tile([P, D_OUT], F32)
         nc.gpsimd.tensor_tensor(out=out_bias[:], in0=b_con_rows[:], in1=down_bias_rows[:], op=ALU.add)
-
-        pair_w = keep.tile([P, STAGES, 4, 4], F32)
-
-        def widen_pair_weights(layout):
-            first = CHUNK_BITS * layout
-            last = min(first + CHUNK_BITS, STAGES)
-            nc.vector.tensor_copy(out=pair_w[:, first:last], in_=pair_w_bf[:, first:last])
-
-        widen_pair_weights(0)
-        b_exp_f = keep.tile([P, 4, 2], F32)
-        nc.vector.tensor_copy(out=b_exp_f[:].rearrange("p g r -> p (g r)"), in_=b_exp_bf[:])
-        stage0_w = pair_w[:, 0].rearrange("p g (r c) -> p g r c", r=2)
-        from_a = keep.tile([P, 4, 2], F32)
-        from_b = keep.tile([P, 4, 2], F32)
-        stage0_bias = keep.tile([P, 4, 2], F32)
-        nc.vector.tensor_tensor(
-            out=from_a[:], in0=stage0_w[:, :, :, 0], in1=b_exp_f[:, :, 0:1].to_broadcast([P, 4, 2]), op=ALU.mult
-        )
-        nc.vector.tensor_tensor(
-            out=from_b[:], in0=stage0_w[:, :, :, 1], in1=b_exp_f[:, :, 1:2].to_broadcast([P, 4, 2]), op=ALU.mult
-        )
-        nc.vector.tensor_tensor(out=stage0_bias[:], in0=from_a[:], in1=from_b[:], op=ALU.add)
-        up_bias_f = keep.tile([P, 2, 4], F32)
 
         x_words = x_sb[:].bitcast(F32)
         x_t = psum.tile([P, 2, TOKENS], F32, tag="tok0")
@@ -195,6 +179,68 @@ def tile_butterflymlp_s_kernel(
                 stop=True,
             )
 
+        reciprocal_w = keep.tile([P, LAYOUTS, 2, 4, 2], F32)
+        divisor = keep.tile([P, LAYOUTS, 2, 4, 2], F32)
+        ratio = keep.tile([P, LAYOUTS, 2, 4, 2], F32)
+        correction = keep.tile([P, LAYOUTS, 4, 2], F32)
+        carried = keep.tile([P, LAYOUTS, 4, 2], F32)
+        full_w = keep.tile([P, LAYOUTS, 4, 4], F32)
+
+        def prepare_scalars(n):
+            first = CHUNK_BITS * n
+            units = min(CHUNK_BITS - 1, STAGES - 1 - first)
+            rec = reciprocal_w[:, n, :units].rearrange("p j g r -> p (j g) r")
+            div = divisor[:, n, :units].rearrange("p j g r -> p (j g) r")
+            w = pair_w[:, first : first + units].rearrange("p j g e -> p (j g) e")
+            nc.vector.reciprocal(out=rec, in_=w[:, :, 0:4:3])
+            nc.vector.tensor_scalar(
+                out=rec, in0=rec, scalar1=MAX_RECIPROCAL, scalar2=-MAX_RECIPROCAL, op0=ALU.min, op1=ALU.max
+            )
+            nc.vector.tensor_tensor(
+                out=ratio[:, n, :units].rearrange("p j g r -> p (j g) r"), in0=w[:, :, 1:3], in1=rec, op=ALU.mult
+            )
+            nc.vector.reciprocal(out=div, in_=rec)
+            by_chunk = by_chunk_bits(first, divisor[:, n, 0])
+            rec_by_chunk = by_chunk_bits(first, reciprocal_w[:, n, 0])
+            last = [pair_w[:, first + units, :, 2 * r : 2 * r + 2] for r in range(2)]
+            full = [full_w[:, n, :, 2 * r : 2 * r + 2] for r in range(2)]
+            if units == 1:
+                for r in range(2):
+                    nc.vector.tensor_tensor(
+                        out=by_chunk_bits(first + 1, full[r]),
+                        in0=by_chunk_bits(first + 1, last[r]),
+                        in1=by_chunk.rearrange("p x y z -> p x z y"),
+                        op=ALU.mult,
+                    )
+                return
+            if first == GELU_STAGE:
+                both = by_chunk_bits(first + 1, divisor[:, n, 1])
+            else:
+                both = by_chunk_bits(first + 1, carried[:, n])
+                nc.vector.tensor_tensor(
+                    out=both,
+                    in0=by_chunk_bits(first + 1, divisor[:, n, 1]),
+                    in1=by_chunk.rearrange("p x y z -> p x z y"),
+                    op=ALU.mult,
+                )
+                for r in range(2):
+                    nc.vector.tensor_tensor(
+                        out=by_chunk_bits(first + 1, correction[:, n])[:, :, :, r],
+                        in0=by_chunk[:, :, 1 - r, :],
+                        in1=rec_by_chunk[:, :, r, :],
+                        op=ALU.mult,
+                    )
+                nc.vector.tensor_tensor(out=ratio[:, n, 1], in0=ratio[:, n, 1], in1=correction[:, n], op=ALU.mult)
+            for r in range(2):
+                nc.vector.tensor_tensor(
+                    out=by_chunk_bits(first + 2, full[r]),
+                    in0=by_chunk_bits(first + 2, last[r]),
+                    in1=both.rearrange("p x z y -> p y z x"),
+                    op=ALU.mult,
+                )
+
+        prepare_scalars(0)
+
         w_con_grouped = keep.tile([P, 2, D_OUT, PACK], BF16, align_bytes=64)
         w_con_codes = keep.tile([P, 2, D_OUT], U32, align_bytes=64)
         w_con_scales = keep.tile([P, 2, D_OUT], U8, align_bytes=64)
@@ -214,39 +260,60 @@ def tile_butterflymlp_s_kernel(
                 in_=w_con_grouped[:].rearrange("p g c t -> p (g c t)"),
             )
 
-        def stage(s, chunk, bias_of, gelu):
-            j = s % CHUNK_BITS
+        def multiply_add(out, in0, scalar, in1):
+            nc.vector.scalar_tensor_tensor(out=out, in0=in0, scalar=scalar, in1=in1, op0=ALU.mult, op1=ALU.add)
+
+        def unit_stage(s, chunk):
+            n, j = divmod(s, CHUNK_BITS)
             new = data.tile([P, CHUNKS, TOKENS], F32, tag="chunks")
             order = PAIR_ORDER[j]
 
-            def apply_gelu(a):
-                nc.scalar.activation(out=new[:, a : a + 2, :], in_=new[:, a : a + 2, :], func=ACT.Gelu)
+            def out_of_psum(c):
+                copied = products.tile([P, TOKENS], F32, tag="prod", name="copied")
+                if s == 0:
+                    nc.scalar.activation(
+                        out=copied[:], in_=chunk[c], func=ACT.Identity, bias=b_exp_sb[:, c : c + 1]
+                    )
+                else:
+                    nc.scalar.copy(out=copied[:], in_=chunk[c])
+                return copied[:]
+
+            def gelu(a):
+                for r, c in enumerate((a, a + 1)):
+                    nc.scalar.activation(
+                        out=new[:, c, :],
+                        in_=new[:, c, :],
+                        func=ACT.Gelu,
+                        scale=divisor[:, n, 0, group_of(s, a), r : r + 1],
+                        bias=up_bias_sb[:, c & 1, (c >> 1) : (c >> 1) + 1],
+                    )
 
             for i, a in enumerate(order):
                 b = a | (1 << j)
-                w = pair_w[:, s, group_of(s, a)]
-                prod = products.tile([P, 2, TOKENS], F32, tag="prod")
-                for r, c in enumerate((a, b)):
+                factor = ratio[:, n, j, group_of(s, a)]
+                in_b = out_of_psum(b) if j == 0 else chunk[b]
+                in_a = out_of_psum(a) if s == 0 else chunk[a]
+                multiply_add(new[:, a, :], in_b, factor[:, 0:1], in_a)
+                multiply_add(new[:, b, :], in_a, factor[:, 1:2], in_b)
+                if s == GELU_STAGE and i > 0:
+                    gelu(order[i - 1])
+            if s == GELU_STAGE:
+                gelu(order[-1])
+            return new
+
+        def full_stage(s, chunk):
+            n, j = divmod(s, CHUNK_BITS)
+            new = data.tile([P, CHUNKS, TOKENS], F32, tag="chunks")
+            for a in PAIR_ORDER[j]:
+                b = a | (1 << j)
+                u = full_w[:, n, group_of(s, a)]
+                prod = [products.tile([P, TOKENS], F32, tag="prod", name="prod") for r in range(2)]
+                for r in range(2):
                     nc.scalar.activation(
-                        out=prod[:, r, :],
-                        in_=chunk[b],
-                        func=ACT.Identity,
-                        scale=w[:, 2 * r + 1 : 2 * r + 2],
-                        bias=bias_of(c) if bias_of else 0.0,
+                        out=prod[r][:], in_=chunk[a], func=ACT.Copy, scale=u[:, 2 * r : 2 * r + 1]
                     )
                 for r, c in enumerate((a, b)):
-                    nc.vector.scalar_tensor_tensor(
-                        out=new[:, c, :],
-                        in0=chunk[a],
-                        scalar=w[:, 2 * r : 2 * r + 1],
-                        in1=prod[:, r, :],
-                        op0=ALU.mult,
-                        op1=ALU.add,
-                    )
-                if gelu and i > 0:
-                    apply_gelu(order[i - 1])
-            if gelu:
-                apply_gelu(order[-1])
+                    multiply_add(new[:, c, :], chunk[b], u[:, 2 * r + 1 : 2 * r + 2], prod[r][:])
             return new
 
         def next_layout(chunk, layout):
@@ -263,9 +330,7 @@ def tile_butterflymlp_s_kernel(
             new = new_psum_chunks()
             for c in FILL_ORDER:
                 nc.tensor.transpose(new[c], by_token[:, c].rearrange("t c hi -> t (c hi)"), identity[:])
-            widen_pair_weights(layout)
-            if layout == 3:
-                nc.vector.tensor_copy(out=up_bias_f[:], in_=up_bias_bf[:])
+            prepare_scalars(layout)
             if 2 <= layout <= 5:
                 regroup_w_con(layout - 2)
             if layout == 6:
@@ -275,12 +340,8 @@ def tile_butterflymlp_s_kernel(
         for s in range(STAGES):
             if s > 0 and s % CHUNK_BITS == 0:
                 chunk = next_layout(chunk, s // CHUNK_BITS)
-            if s == 0:
-                hidden = stage(s, chunk, lambda c: stage0_bias[:, c >> 1, (c & 1) : (c & 1) + 1], False)
-            elif s == FEATURE_BITS - 1:
-                hidden = stage(s, chunk, lambda c: up_bias_f[:, c & 1, (c >> 1) : (c >> 1) + 1], True)
-            else:
-                hidden = stage(s, chunk, None, False)
+            last_of_layout = s % CHUNK_BITS == CHUNK_BITS - 1 or s == STAGES - 1
+            hidden = full_stage(s, chunk) if last_of_layout else unit_stage(s, chunk)
             chunk = [hidden[:, c, :] for c in range(CHUNKS)]
 
         h_view = hidden[:].rearrange("p (e g u) t -> p g t u e", e=2, g=2, u=2)

@@ -16,60 +16,30 @@ TOKENS = 128
 D_IN = 512
 HIDDEN = 1024
 D_OUT = 512
-FEATURE_BITS = 10
-STAGES = 2 * FEATURE_BITS
-CHUNKS = 8
-CHUNK_BITS = 3
+STREAMS = 2
+CHUNKS = 4
+STAGES = 20
 PACK = 4
-LAYOUTS = 7
-GELU_STAGE = FEATURE_BITS - 1
+LAYOUTS = 6
 MAX_RECIPROCAL = 2.0**40
 
 FLOPS = 2 * TOKENS * D_IN * HIDDEN + 2 * TOKENS * HIDDEN * D_OUT + STAGES * TOKENS * HIDDEN * 3
 
-PAIR_ORDER = ((0, 2, 4, 6), (0, 1, 4, 5), (0, 2, 1, 3))
-FILL_ORDER = (1, 3, 0, 2, 5, 7, 4, 6)
+CHUNK_ORDER = (1, 0, 3, 2)
+PAIRS = (((0, 1), (2, 3)), ((0, 2), (1, 3)))
+AFTER_PAIRS = (0, 2, 1, 3)
+
+FLIPS = (
+    (dict(a=2, b=8, c=2, d=4), "d c b a", "c"),
+    (dict(a=2, b=2, c=4, d=8), "c b a d", "a"),
+    (dict(a=2, b=8, c=2, d=4), "d c a b", "c"),
+    (dict(a=2, b=8, c=2, d=4), "d a b c", "a"),
+)
+LOW_RUN = (1, 8, 8, 16)
 
 
-def free_pair_bits(s):
-    st = s % FEATURE_BITS
-    found = []
-    for j in range(CHUNK_BITS):
-        feature_bit = (s - s % CHUNK_BITS + j) % FEATURE_BITS
-        if feature_bit != st:
-            found.append((feature_bit if feature_bit < st else feature_bit - 1, j))
-    return sorted(found)
-
-
-def load_pair_weights(queue, dst, stage_weights, s):
-    (low, j_low), (high, j_high) = free_pair_bits(s)
-    if high == low + 1:
-        n_lo = 2**low
-        n_hi = P // n_lo
-        if n_lo <= n_hi:
-            view = stage_weights.rearrange("(hi g lo) r c -> lo hi g (r c)", g=4, lo=n_lo)
-            for lo in range(n_lo):
-                queue.dma_start(out=dst[lo * n_hi : (lo + 1) * n_hi], in_=view[lo])
-        else:
-            view = stage_weights.rearrange("(hi g lo) r c -> hi lo g (r c)", g=4, lo=n_lo)
-            for hi in range(n_hi):
-                queue.dma_start(out=dst[hi:P:n_hi], in_=view[hi])
-    else:
-        assert (low, high) == (0, 8)
-        queue.dma_start(
-            out=dst.rearrange("p (x y) e -> p x (y e)", x=2),
-            in_=stage_weights.rearrange("(x p y) r c -> p x (y r c)", x=2, y=2),
-        )
-
-
-def group_of(s, chunk):
-    (low, j_low), (high, j_high) = free_pair_bits(s)
-    return 2 * ((chunk >> j_high) & 1) + ((chunk >> j_low) & 1)
-
-
-def by_chunk_bits(s, view):
-    (low, j_low), (high, j_high) = free_pair_bits(s)
-    return view.rearrange("p (x y) r -> p x y r" if j_high > j_low else "p (y x) r -> p x y r", x=2)
+def flip_of(n):
+    return 3 if n == LAYOUTS - 1 else n % 3
 
 
 def tile_butterflymlp_s_kernel(
@@ -80,166 +50,251 @@ def tile_butterflymlp_s_kernel(
         ctx.enter_context(tc.manual_schedule())
         keep = ctx.enter_context(tc.tile_pool(name="keep", bufs=1))
         data = ctx.enter_context(tc.tile_pool(name="data", bufs=3))
-        products = ctx.enter_context(tc.tile_pool(name="products", bufs=8))
+        products = ctx.enter_context(tc.tile_pool(name="products", bufs=24))
         psum = ctx.enter_context(tc.psum_pool(name="psum", bufs=1))
 
         x_sb = keep.tile([P, D_IN], BF16)
         w_exp_raw = keep.tile([P, PACK, HIDDEN], BF16)
-        pair_w = keep.tile([P, STAGES, 4, 4], BF16)
-        b_exp_sb = keep.tile([P, CHUNKS], BF16)
-        up_bias_sb = keep.tile([P, 2, 4], BF16)
+        unit_w = [None] * LAYOUTS
+        turn_w = [None] * LAYOUTS
+        rows = [None] * LAYOUTS
+        for n in (0, 3):
+            unit_w[n] = keep.tile([P, 8, 4], BF16, name="unit_w%d" % n)
+            turn_w[n] = keep.tile([P, 8, 4], BF16, name="turn_w%d" % n)
+        up_last_w = keep.tile([P, CHUNKS, 4], BF16)
+        down_last_w = keep.tile([P, CHUNKS, 4], BF16)
+        b_exp_sb = keep.tile([P, STREAMS, CHUNKS], BF16)
+        up_bias_sb = keep.tile([P, STREAMS, CHUNKS], BF16)
         w_con_raw = keep.tile([P, 2, PACK, D_OUT], BF16)
         b_con_rows = keep.tile([P, D_OUT], BF16)
         down_bias_rows = keep.tile([P, D_OUT], BF16)
 
-        def load_stage(queue, s):
-            weights = up_weights if s < FEATURE_BITS else down_weights
-            load_pair_weights(queue, pair_w[:, s], weights[s % FEATURE_BITS], s)
+        def weights_of(n, stage):
+            return (up_weights if n < 3 else down_weights)[3 * (n % 3) + stage]
 
-        for s in range(0, 3):
-            load_stage(nc.scalar, s)
-        nc.scalar.dma_start(out=b_exp_sb[:], in_=b_exp.rearrange("(p c) -> p c", c=CHUNKS))
-        nc.sync.dma_start(out=x_sb[:], in_=x.flatten_outer_dims())
-        for side in range(2):
-            cols = slice(HIDDEN // 2 * side, HIDDEN // 2 * (side + 1))
-            for u in range(2):
-                nc.sync.dma_start(
-                    out=w_exp_raw[:, 2 * u : 2 * u + 2, cols],
-                    in_=W_exp[256 * u : 256 * u + 256, cols].rearrange("(q e) c -> q e c", e=2),
-                )
-        for s in range(3, 6):
-            load_stage(nc.sync, s)
-        nc.sync.dma_start(
-            out=w_con_raw[:].rearrange("p g (u e) c -> p (g u) (e c)", u=2),
-            in_=W_con.rearrange("(a q e) c -> q a (e c)", a=4, e=2),
-        )
-        for s in range(6, 10):
-            load_stage(nc.sync, s)
-        nc.sync.dma_start(out=up_bias_sb[:], in_=up_bias.rearrange("(h p l) -> p h l", h=2, l=4))
-        for s in range(10, STAGES):
-            load_stage(nc.sync, s)
-        nc.sync.dma_start(out=b_con_rows[:], in_=b_con.partition_broadcast(P))
-        nc.sync.dma_start(out=down_bias_rows[:], in_=down_bias.partition_broadcast(P))
+        def load_low(queue, n):
+            for s in range(2):
+                view = weights_of(n, s).rearrange("(h q v g) r c -> v q h (g r c)", h=2, q=64, v=2, g=2)
+                for v in range(2):
+                    dst = unit_w[n][64 * v : 64 * v + 64, 4 * s : 4 * s + 4]
+                    queue.dma_start(out=dst.rearrange("q (h g) e -> q h (g e)", h=2), in_=view[v])
+            view = weights_of(n, 2).rearrange("(h q c) r s -> q h (c r s)", h=2, q=64)
+            for v in range(2):
+                dst = turn_w[n][64 * v : 64 * v + 64]
+                queue.dma_start(out=dst.rearrange("q (h c) e -> q h (c e)", h=2), in_=view)
 
-        identity = keep.tile([P, P], F32)
-        make_identity(nc, identity[:])
+        def load_rows(queue, n):
+            pairs = rows[n].rearrange("r (v e) -> r v e", v=2)
+            if n % 3 == 1:
+                for s in range(2):
+                    view = weights_of(n, s).rearrange("(h x v g y) r c -> h v g x (y r c)", h=2, x=8, v=2, g=2)
+                    for h in range(2):
+                        r = 4 * s + 2 * h
+                        for v in range(2):
+                            dst = pairs[r : r + 2, v].rearrange("g (x e) -> g x e", x=8)
+                            queue.dma_start(out=dst, in_=view[h, v])
+                view = weights_of(n, 2).rearrange("(h x c y) r s -> h c x (y r s)", h=2, x=8, c=4)
+                for h in range(2):
+                    r = 8 + 4 * h
+                    for v in range(2):
+                        queue.dma_start(out=pairs[r : r + 4, v].rearrange("c (x e) -> c x e", x=8), in_=view[h])
+            else:
+                view = weights_of(n, 0).rearrange("(h v g y) r c -> h g v (y r c)", h=2, v=2, g=2)
+                for h in range(2):
+                    queue.dma_start(out=pairs[2 * h : 2 * h + 2], in_=view[h])
+                view = weights_of(n, 1).rearrange("(h v g y) r c -> h g v (y r c)", h=2, v=2, g=2)
+                for h in range(2):
+                    queue.dma_start(out=pairs[4 + 2 * h : 6 + 2 * h], in_=view[h])
+                view = weights_of(n, 2).rearrange("(q y) r c -> q (y r c)", q=8)
+                for v in range(2):
+                    queue.dma_start(out=pairs[8:16, v], in_=view)
+
+        row_tiles = {}
+        for n in (1, 2, 4, 5):
+            row_tiles[n] = keep.tile([P, 2 * P], F32, name="rows%d" % n)
+            nc.vector.memset(row_tiles[n][:], 0.0)
+            rows[n] = row_tiles[n][:].bitcast(BF16)
         zero_column = keep.tile([P, 1], F32)
         gelu_of_zero = keep.tile([P, 1], F32)
         nc.vector.memset(zero_column[:], 0.0)
+
+        nc.sync.dma_start(out=x_sb[:], in_=x.flatten_outer_dims())
+        for h in range(STREAMS):
+            cols = slice(HIDDEN // 2 * h, HIDDEN // 2 * (h + 1))
+            nc.sync.dma_start(out=w_exp_raw[:, :, cols], in_=W_exp[:, cols].rearrange("(p t) c -> p t c", t=PACK))
+            if h == 0:
+                load_low(nc.sync, 0)
+        view = b_exp.rearrange("(h q v c) -> v q h c", h=2, q=64, v=2)
+        for v in range(2):
+            nc.sync.dma_start(out=b_exp_sb[64 * v : 64 * v + 64], in_=view[v])
+        load_rows(nc.sync, 1)
+        load_rows(nc.sync, 2)
+        view = up_weights[9].rearrange("(q v c) r s -> v q (c r s)", v=2, c=4)
+        for v in range(2):
+            dst = up_last_w[64 * v : 64 * v + 64]
+            nc.sync.dma_start(out=dst.rearrange("q c e -> q (c e)"), in_=view[v])
+        view = up_bias.rearrange("(h q v c) -> v q h c", h=2, q=64, v=2)
+        for v in range(2):
+            nc.sync.dma_start(out=up_bias_sb[64 * v : 64 * v + 64], in_=view[v])
+        load_low(nc.sync, 3)
+        nc.sync.dma_start(
+            out=w_con_raw[:].rearrange("p g t c -> p g (t c)"),
+            in_=W_con.rearrange("(g p t) c -> p g (t c)", g=2, t=PACK),
+        )
+        load_rows(nc.sync, 4)
+        load_rows(nc.sync, 5)
+        nc.sync.dma_start(
+            out=down_last_w[:].rearrange("p c e -> p (c e)"), in_=down_weights[9].rearrange("(p c) r s -> p (c r s)", c=4)
+        )
+        nc.sync.dma_start(out=b_con_rows[:], in_=b_con.partition_broadcast(P))
+        nc.sync.dma_start(out=down_bias_rows[:], in_=down_bias.partition_broadcast(P))
+
+        identity = keep.tile([P, P + 64], F32)
+        make_identity(nc, identity[:, 0:P])
         nc.scalar.activation(out=gelu_of_zero[:], in_=zero_column[:], func=ACT.Gelu)
+        nc.scalar.copy(out=identity[:, P : P + 64], in_=identity[:, 0:64])
+        flips = keep.tile([P, len(FLIPS), 2, P], F32)
+        for kind, (sizes, order, loop) in enumerate(FLIPS):
+            rest = [g for g in order.split(" ") if g != loop]
+            for turned in range(2):
+                src = identity[:, 64 * turned : 64 * turned + P].rearrange(
+                    "p (a b c d) -> p %s %s" % (loop, " ".join(rest)), **sizes
+                )
+                dst = flips[:, kind, turned].rearrange("p (%s) -> p %s %s" % (order, loop, " ".join(rest)), **sizes)
+                for i in range(sizes[loop]):
+                    nc.scalar.copy(out=dst[:, i], in_=src[:, i])
 
         out_bias = keep.tile([P, D_OUT], F32)
         nc.gpsimd.tensor_tensor(out=out_bias[:], in0=b_con_rows[:], in1=down_bias_rows[:], op=ALU.add)
 
+        steps = []
+
+        def run_steps(count):
+            for step in steps[:count]:
+                step()
+                steps.remove(step)
+
+        def multiply(out, in0, in1):
+            steps.append(lambda: nc.vector.tensor_tensor(out=out, in0=in0, in1=in1, op=ALU.mult))
+
+        def divide_out(w, name):
+            groups = w.shape[1]
+            rec = keep.tile([P, groups, 2], F32, name="rec" + name)
+            factor = keep.tile([P, groups, 2], F32, name="factor" + name)
+            div = keep.tile([P, groups, 2], F32, name="div" + name)
+            steps.append(lambda: nc.vector.reciprocal(out=rec[:], in_=w[:, :, 0:4:3]))
+            steps.append(
+                lambda: nc.vector.tensor_scalar(
+                    out=rec[:], in0=rec[:], scalar1=MAX_RECIPROCAL, scalar2=-MAX_RECIPROCAL, op0=ALU.min, op1=ALU.max
+                )
+            )
+            multiply(factor[:], w[:, :, 1:3], rec[:])
+            steps.append(lambda: nc.vector.reciprocal(out=div[:], in_=rec[:]))
+            return rec, factor, div
+
+        factors = [None] * LAYOUTS
+        turn_factors = [None] * LAYOUTS
+
+        def queue_scalars(n):
+            rec, factor, div = divide_out(unit_w[n][:], "%d" % n)
+            div0 = div[:, 0:4].rearrange("p (h x) z -> p h x z", h=2)
+            rec0 = rec[:, 0:4].rearrange("p (h x) z -> p h x z", h=2)
+            div1 = div[:, 4:8].rearrange("p (h z) x -> p h x z", h=2)
+            correction = keep.tile([P, 4, 2], F32, name="correction%d" % n)
+            carried = keep.tile([P, 8], F32, name="carried%d" % n)
+            for r in range(2):
+                multiply(
+                    correction[:, :, r].rearrange("p (h z) -> p h z", h=2), div0[:, :, 1 - r, :], rec0[:, :, r, :]
+                )
+            multiply(carried[:].rearrange("p (h x z) -> p h x z", h=2, x=2), div1, div0)
+            multiply(factor[:, 4:8], factor[:, 4:8], correction[:])
+            turn = keep.tile([P, 8, 2], F32, name="turn%d" % n)
+            w = turn_w[n]
+            for s, e in enumerate((0, 2)):
+                multiply(turn[0:64, :, s], w[0:64, :, e], carried[0:64])
+            for s, e in enumerate((3, 1)):
+                multiply(turn[64:128, :, s], w[64:128, :, e], carried[64:128])
+            factors[n] = factor
+            turn_factors[n] = turn
+
+        def turn_rows(n):
+            words = row_tiles[n]
+            turned = psum.tile([P, 2, P], F32, tag="spare0", name="turned%d" % n)
+            for w in range(2):
+                nc.tensor.transpose(turned[:, w, :], words[:, w : 2 * P : 2], identity[:, 0:P])
+            landed = keep.tile([P, 16, 2], F32, name="landed%d" % n)
+            steps.append(
+                lambda: nc.vector.tensor_copy(out=landed[:], in_=turned[:, :, 0:16].rearrange("p w r -> p r w"))
+            )
+            pairs = landed[:].rearrange("p r w -> p (r w)").bitcast(BF16).rearrange("p (r e) -> p r e", e=4)
+            unit_w[n] = pairs[:, 0:8]
+            turn_w[n] = pairs[:, 8:16]
+            queue_scalars(n)
+
+        queue_scalars(0)
+
         x_words = x_sb[:].bitcast(F32)
-        x_t = psum.tile([P, 2, TOKENS], F32, tag="tok0")
+        x_t = psum.tile([P, 2, TOKENS], F32, tag="spare1")
         for u in range(2):
-            nc.tensor.transpose(x_t[:, u, :], x_words[:, P * u : P * u + P], identity[:])
+            nc.tensor.transpose(x_t[:, u, :], x_words[:, u : 2 * P : 2], identity[:, 0:P])
         x_grouped = keep.tile([P, TOKENS, 2], F32, align_bytes=64)
         nc.vector.tensor_copy(out=x_grouped[:], in_=x_t[:].rearrange("p u t -> p t u"))
         x_codes = keep.tile([P, TOKENS], U32, align_bytes=64)
         x_scales = keep.tile([P, TOKENS], U8, align_bytes=64)
 
-        w_exp_grouped = keep.tile([P, CHUNKS, P, PACK], BF16, align_bytes=64)
-        w_exp_from = w_exp_raw[:].rearrange("p t (m c) -> p m t c", c=CHUNKS)
-        w_exp_to = w_exp_grouped[:].rearrange("p c m t -> p m t c")
-        w_exp_codes = keep.tile([P, CHUNKS, P], U32, align_bytes=64)
-        w_exp_scales = keep.tile([P, CHUNKS, P], U8, align_bytes=64)
-        left, right = slice(0, P // 2), slice(P // 2, P)
-        nc.vector.tensor_copy(out=w_exp_to[:, left, :, 0:4], in_=w_exp_from[:, left, :, 0:4])
+        w_exp_grouped = keep.tile([P, STREAMS, CHUNKS, P, PACK], BF16, align_bytes=64)
+        w_exp_codes = keep.tile([P, STREAMS, CHUNKS, P], U32, align_bytes=64)
+        w_exp_scales = keep.tile([P, STREAMS, CHUNKS, P], U8, align_bytes=64)
+
+        def regroup_w_exp(copy, h, v):
+            src = w_exp_raw[:, :, 512 * h : 512 * h + 512].rearrange("p t (q v c) -> p v q t c", v=2, c=CHUNKS)
+            dst = w_exp_grouped[:, h].rearrange("p c (v q) t -> p v q t c", v=2)
+            copy(out=dst[:, v], in_=src[:, v])
+
+        def quantise_w_exp(h):
+            nc.vector.quantize_mx(
+                out=w_exp_codes[:, h].rearrange("p c m -> p (c m)").bitcast(FP8X4),
+                scales=w_exp_scales[:, h].rearrange("p c m -> p (c m)"),
+                in_=w_exp_grouped[:, h].rearrange("p c m t -> p (c m t)"),
+            )
+
+        def new_psum_chunks(h):
+            banks = [
+                psum.tile([P, CHUNKS, TOKENS], F32, tag="stream%d_bank%d" % (h, i), name="stream%d_bank%d" % (h, i))
+                for i in range(2)
+            ]
+            return [banks[c & 1][:, c >> 1, :] for c in range(CHUNKS)]
+
+        def first_product(h):
+            chunk = new_psum_chunks(h)
+            for c in CHUNK_ORDER:
+                nc.tensor.matmul_mx(
+                    out=chunk[c],
+                    lhsT=w_exp_codes[:, h, c, :].bitcast(FP8X4),
+                    lhsT_scale=w_exp_scales[:, h, c, :],
+                    rhs=x_codes[:].bitcast(FP8X4),
+                    rhs_scale=x_scales[:],
+                    start=True,
+                    stop=True,
+                )
+            return chunk
+
+        regroup_w_exp(nc.vector.tensor_copy, 0, 0)
+        run_steps(1)
+        regroup_w_exp(nc.vector.tensor_copy, 0, 1)
+        run_steps(1)
         nc.vector.quantize_mx(
             out=x_codes[:].bitcast(FP8X4),
             scales=x_scales[:],
             in_=x_grouped[:].rearrange("p t u -> p (t u)").bitcast(BF16),
         )
-        nc.vector.tensor_copy(out=w_exp_to[:, left, :, 4:8], in_=w_exp_from[:, left, :, 4:8])
-        nc.scalar.copy(out=w_exp_to[:, right, :, 4:8], in_=w_exp_from[:, right, :, 4:8])
-        nc.vector.tensor_copy(out=w_exp_to[:, right, :, 0:4], in_=w_exp_from[:, right, :, 0:4])
-        for half in range(2):
-            chunks = slice(4 * half, 4 * half + 4)
-            nc.vector.quantize_mx(
-                out=w_exp_codes[:, chunks].rearrange("p c m -> p (c m)").bitcast(FP8X4),
-                scales=w_exp_scales[:, chunks].rearrange("p c m -> p (c m)"),
-                in_=w_exp_grouped[:, chunks].rearrange("p c m t -> p (c m t)"),
-            )
-
-        def new_psum_chunks():
-            banks = [psum.tile([P, 2, TOKENS], F32, tag="chunks%d" % i, name="chunks%d" % i) for i in range(4)]
-            return [banks[2 * (c >> 2) + (c & 1)][:, (c >> 1) & 1, :] for c in range(CHUNKS)]
-
-        chunk = new_psum_chunks()
-        for c in FILL_ORDER:
-            nc.tensor.matmul_mx(
-                out=chunk[c],
-                lhsT=w_exp_codes[:, c, :].bitcast(FP8X4),
-                lhsT_scale=w_exp_scales[:, c, :],
-                rhs=x_codes[:].bitcast(FP8X4),
-                rhs_scale=x_scales[:],
-                start=True,
-                stop=True,
-            )
-
-        reciprocal_w = keep.tile([P, LAYOUTS, 2, 4, 2], F32)
-        divisor = keep.tile([P, LAYOUTS, 2, 4, 2], F32)
-        ratio = keep.tile([P, LAYOUTS, 2, 4, 2], F32)
-        correction = keep.tile([P, LAYOUTS, 4, 2], F32)
-        carried = keep.tile([P, LAYOUTS, 4, 2], F32)
-        full_w = keep.tile([P, LAYOUTS, 4, 4], F32)
-
-        def prepare_scalars(n):
-            first = CHUNK_BITS * n
-            units = min(CHUNK_BITS - 1, STAGES - 1 - first)
-            rec = reciprocal_w[:, n, :units].rearrange("p j g r -> p (j g) r")
-            div = divisor[:, n, :units].rearrange("p j g r -> p (j g) r")
-            w = pair_w[:, first : first + units].rearrange("p j g e -> p (j g) e")
-            nc.vector.reciprocal(out=rec, in_=w[:, :, 0:4:3])
-            nc.vector.tensor_scalar(
-                out=rec, in0=rec, scalar1=MAX_RECIPROCAL, scalar2=-MAX_RECIPROCAL, op0=ALU.min, op1=ALU.max
-            )
-            nc.vector.tensor_tensor(
-                out=ratio[:, n, :units].rearrange("p j g r -> p (j g) r"), in0=w[:, :, 1:3], in1=rec, op=ALU.mult
-            )
-            nc.vector.reciprocal(out=div, in_=rec)
-            by_chunk = by_chunk_bits(first, divisor[:, n, 0])
-            rec_by_chunk = by_chunk_bits(first, reciprocal_w[:, n, 0])
-            last = [pair_w[:, first + units, :, 2 * r : 2 * r + 2] for r in range(2)]
-            full = [full_w[:, n, :, 2 * r : 2 * r + 2] for r in range(2)]
-            if units == 1:
-                for r in range(2):
-                    nc.vector.tensor_tensor(
-                        out=by_chunk_bits(first + 1, full[r]),
-                        in0=by_chunk_bits(first + 1, last[r]),
-                        in1=by_chunk.rearrange("p x y z -> p x z y"),
-                        op=ALU.mult,
-                    )
-                return
-            if first == GELU_STAGE:
-                both = by_chunk_bits(first + 1, divisor[:, n, 1])
-            else:
-                both = by_chunk_bits(first + 1, carried[:, n])
-                nc.vector.tensor_tensor(
-                    out=both,
-                    in0=by_chunk_bits(first + 1, divisor[:, n, 1]),
-                    in1=by_chunk.rearrange("p x y z -> p x z y"),
-                    op=ALU.mult,
-                )
-                for r in range(2):
-                    nc.vector.tensor_tensor(
-                        out=by_chunk_bits(first + 1, correction[:, n])[:, :, :, r],
-                        in0=by_chunk[:, :, 1 - r, :],
-                        in1=rec_by_chunk[:, :, r, :],
-                        op=ALU.mult,
-                    )
-                nc.vector.tensor_tensor(out=ratio[:, n, 1], in0=ratio[:, n, 1], in1=correction[:, n], op=ALU.mult)
-            for r in range(2):
-                nc.vector.tensor_tensor(
-                    out=by_chunk_bits(first + 2, full[r]),
-                    in0=by_chunk_bits(first + 2, last[r]),
-                    in1=both.rearrange("p x z y -> p y z x"),
-                    op=ALU.mult,
-                )
-
-        prepare_scalars(0)
+        quantise_w_exp(0)
+        run_steps(1)
+        regroup_w_exp(nc.scalar.copy, 1, 1)
+        regroup_w_exp(nc.vector.tensor_copy, 1, 0)
+        run_steps(1)
+        quantise_w_exp(1)
+        streams = [first_product(0), first_product(1)]
 
         w_con_grouped = keep.tile([P, 2, D_OUT, PACK], BF16, align_bytes=64)
         w_con_codes = keep.tile([P, 2, D_OUT], U32, align_bytes=64)
@@ -253,104 +308,163 @@ def tile_butterflymlp_s_kernel(
                 in_=w_con_raw[:, g, :, cols].rearrange("p t (c i) -> p c t i", i=4),
             )
 
-        def quantise_w_con():
+        def quantise_w_con(g):
             nc.vector.quantize_mx(
-                out=w_con_codes[:].rearrange("p g c -> p (g c)").bitcast(FP8X4),
-                scales=w_con_scales[:].rearrange("p g c -> p (g c)"),
-                in_=w_con_grouped[:].rearrange("p g c t -> p (g c t)"),
+                out=w_con_codes[:, g].bitcast(FP8X4),
+                scales=w_con_scales[:, g],
+                in_=w_con_grouped[:, g].rearrange("p c t -> p (c t)"),
             )
 
         def multiply_add(out, in0, scalar, in1):
             nc.vector.scalar_tensor_tensor(out=out, in0=in0, scalar=scalar, in1=in1, op0=ALU.mult, op1=ALU.add)
 
-        def unit_stage(s, chunk):
-            n, j = divmod(s, CHUNK_BITS)
-            new = data.tile([P, CHUNKS, TOKENS], F32, tag="chunks")
-            order = PAIR_ORDER[j]
+        def work_tile(name):
+            return products.tile([P, TOKENS], F32, tag="work", name=name)
 
-            def out_of_psum(c):
-                copied = products.tile([P, TOKENS], F32, tag="prod", name="copied")
-                if s == 0:
-                    nc.scalar.activation(
-                        out=copied[:], in_=chunk[c], func=ACT.Identity, bias=b_exp_sb[:, c : c + 1]
+        def out_of_psum(chunk, bias=None):
+            copied = work_tile("copied")
+            if bias is None:
+                nc.scalar.copy(out=copied[:], in_=chunk)
+            else:
+                nc.scalar.activation(out=copied[:], in_=chunk, func=ACT.Identity, bias=bias)
+            return copied[:]
+
+        def unit_stages(h, n, count):
+            chunk = list(streams[h])
+            if n == 0:
+                for c in CHUNK_ORDER:
+                    chunk[c] = out_of_psum(chunk[c], bias=b_exp_sb[:, h, c : c + 1])
+            elif n != 3:
+                for c in (1, 3):
+                    chunk[c] = out_of_psum(chunk[c])
+            for j in range(2):
+                new = data.tile([P, CHUNKS, TOKENS], F32, tag="chunks%d" % h, name="chunks%d" % h)
+                for i, (a, b) in enumerate(PAIRS[j]):
+                    factor = factors[n][:, 4 * j + 2 * h + i]
+                    multiply_add(new[:, a, :], chunk[b], factor[:, 0:1], chunk[a])
+                    multiply_add(new[:, b, :], chunk[a], factor[:, 1:2], chunk[b])
+                    run_steps(count)
+                chunk = [new[:, c, :] for c in range(CHUNKS)]
+            streams[h] = chunk
+
+        flipped = [None, None]
+
+        def turn_stage(h, n):
+            flipped[h] = psum.tile([P, CHUNKS, P], F32, tag="flipped%d" % h, name="flipped%d" % h)
+            prods = {}
+            for c in AFTER_PAIRS:
+                for s in range(2):
+                    prods[c, s] = work_tile("product")
+                    scalar = turn_factors[n][:, 4 * h + c, s : s + 1]
+                    if s == 1 and c >= 2:
+                        nc.vector.tensor_scalar(
+                            out=prods[c, s][:], in0=streams[h][c], scalar1=scalar, scalar2=None, op0=ALU.mult
+                        )
+                    else:
+                        nc.scalar.activation(out=prods[c, s][:], in_=streams[h][c], func=ACT.Copy, scale=scalar)
+                    nc.tensor.matmul(
+                        flipped[h][:, c, :],
+                        lhsT=prods[c, s][:],
+                        rhs=flips[:, flip_of(n), s, :],
+                        start=(s == 0),
+                        stop=(s == 1),
+                        is_transpose=True,
                     )
-                else:
-                    nc.scalar.copy(out=copied[:], in_=chunk[c])
-                return copied[:]
 
-            def gelu(a):
-                for r, c in enumerate((a, a + 1)):
-                    nc.scalar.activation(
-                        out=new[:, c, :],
-                        in_=new[:, c, :],
-                        func=ACT.Gelu,
-                        scale=divisor[:, n, 0, group_of(s, a), r : r + 1],
-                        bias=up_bias_sb[:, c & 1, (c >> 1) : (c >> 1) + 1],
-                    )
-
-            for i, a in enumerate(order):
-                b = a | (1 << j)
-                factor = ratio[:, n, j, group_of(s, a)]
-                in_b = out_of_psum(b) if j == 0 else chunk[b]
-                in_a = out_of_psum(a) if s == 0 else chunk[a]
-                multiply_add(new[:, a, :], in_b, factor[:, 0:1], in_a)
-                multiply_add(new[:, b, :], in_a, factor[:, 1:2], in_b)
-                if s == GELU_STAGE and i > 0:
-                    gelu(order[i - 1])
-            if s == GELU_STAGE:
-                gelu(order[-1])
-            return new
-
-        def full_stage(s, chunk):
-            n, j = divmod(s, CHUNK_BITS)
-            new = data.tile([P, CHUNKS, TOKENS], F32, tag="chunks")
-            for a in PAIR_ORDER[j]:
-                b = a | (1 << j)
-                u = full_w[:, n, group_of(s, a)]
-                prod = [products.tile([P, TOKENS], F32, tag="prod", name="prod") for r in range(2)]
-                for r in range(2):
-                    nc.scalar.activation(
-                        out=prod[r][:], in_=chunk[a], func=ACT.Copy, scale=u[:, 2 * r : 2 * r + 1]
-                    )
-                for r, c in enumerate((a, b)):
-                    multiply_add(new[:, c, :], chunk[b], u[:, 2 * r + 1 : 2 * r + 2], prod[r][:])
-            return new
-
-        def next_layout(chunk, layout):
-            by_token = data.tile([P, CHUNKS, CHUNKS, 16], F32, tag="by_token")
-            for i, a in enumerate(PAIR_ORDER[2]):
-                flipped = psum.tile([P, 2, P], F32, tag="tok%d" % i, name="flipped%d" % i)
-                nc.tensor.transpose(flipped[:, 0, :], chunk[a], identity[:])
-                nc.tensor.transpose(flipped[:, 1, :], chunk[a + 4], identity[:])
-                copy = nc.scalar.copy if i < 3 else nc.vector.tensor_copy
-                copy(
-                    out=by_token[:, :, a : a + 5 : 4, :],
-                    in_=flipped[:].rearrange("t s (hi lo) -> t lo s hi", lo=CHUNKS),
+        def turn_back(h, n):
+            by_token = data.tile([P, CHUNKS, P], F32, tag="by_token%d" % h, name="by_token%d" % h)
+            new = new_psum_chunks(h)
+            for c in CHUNK_ORDER:
+                run = LOW_RUN[flip_of(n)]
+                nc.scalar.copy(
+                    out=by_token[:, c].rearrange("t (x a y) -> t x a y", a=CHUNKS, y=run),
+                    in_=flipped[h][:, :, 32 * c : 32 * c + 32].rearrange("t a (x y) -> t x a y", y=run),
                 )
-            new = new_psum_chunks()
-            for c in FILL_ORDER:
-                nc.tensor.transpose(new[c], by_token[:, c].rearrange("t c hi -> t (c hi)"), identity[:])
-            prepare_scalars(layout)
-            if 2 <= layout <= 5:
-                regroup_w_con(layout - 2)
-            if layout == 6:
-                quantise_w_con()
-            return new
+                nc.tensor.transpose(new[c], by_token[:, c], identity[:, 0:P])
+            streams[h] = new
 
-        for s in range(STAGES):
-            if s > 0 and s % CHUNK_BITS == 0:
-                chunk = next_layout(chunk, s // CHUNK_BITS)
-            last_of_layout = s % CHUNK_BITS == CHUNK_BITS - 1 or s == STAGES - 1
-            hidden = full_stage(s, chunk) if last_of_layout else unit_stage(s, chunk)
-            chunk = [hidden[:, c, :] for c in range(CHUNKS)]
+        unit_stages(0, 0, 2)
+        run_steps(len(steps))
+        turn_stage(0, 0)
+        turn_rows(1)
+        unit_stages(1, 0, 1)
+        turn_back(0, 0)
+        turn_stage(1, 0)
+        run_steps(len(steps))
+        for n in (1, 2):
+            if n == 2:
+                queue_scalars(3)
+            else:
+                turn_rows(2)
+            if n == 2:
+                up_last_rec, up_last_factor, up_last_div = divide_out(up_last_w[:], "_last")
+            unit_stages(0, n, 1)
+            turn_back(1, n - 1)
+            turn_stage(0, n)
+            unit_stages(1, n, 2 if n == 2 else 1)
+            turn_back(0, n)
+            turn_stage(1, n)
+            run_steps(len(steps))
+        turn_back(1, 2)
 
-        h_view = hidden[:].rearrange("p (e g u) t -> p g t u e", e=2, g=2, u=2)
+        raised = [data.tile([P, CHUNKS, TOKENS], F32, tag="chunks%d" % h, name="raised%d" % h) for h in range(2)]
+        copied = [out_of_psum(streams[1][c]) for c in range(CHUNKS)]
+        for c in range(CHUNKS):
+            multiply_add(raised[0][:, c, :], copied[c], up_last_factor[:, c, 0:1], streams[0][c])
+        for c in range(CHUNKS):
+            multiply_add(raised[1][:, c, :], streams[0][c], up_last_factor[:, c, 1:2], copied[c])
+        for h in range(2):
+            for c in range(CHUNKS):
+                nc.scalar.activation(
+                    out=raised[h][:, c, :],
+                    in_=raised[h][:, c, :],
+                    func=ACT.Gelu,
+                    scale=up_last_div[:, c, h : h + 1],
+                    bias=up_bias_sb[:, h, c : c + 1],
+                )
+            streams[h] = [raised[h][:, c, :] for c in range(CHUNKS)]
+
+        down_last_f = keep.tile([P, CHUNKS, 4], F32)
+        for n in (3, 4, 5):
+            if n < 5:
+                turn_rows(n + 1)
+            else:
+                steps.append(lambda: nc.vector.tensor_copy(out=down_last_f[:], in_=down_last_w[:]))
+            unit_stages(0, n, 1)
+            if n > 3:
+                turn_back(1, n - 1)
+            turn_stage(0, n)
+            unit_stages(1, n, 1)
+            turn_back(0, n)
+            turn_stage(1, n)
+            run_steps(len(steps))
+            if n == 3:
+                regroup_w_con(0)
+                regroup_w_con(1)
+            if n == 4:
+                regroup_w_con(2)
+                regroup_w_con(3)
+            if n == 5:
+                quantise_w_con(0)
+                quantise_w_con(1)
+        turn_back(1, 5)
+
+        hidden = keep.tile([P, STREAMS, CHUNKS, TOKENS], F32)
+        for r in range(2):
+            for c in range(CHUNKS):
+                prod = work_tile("product")
+                w = down_last_f[:, c]
+                nc.scalar.activation(
+                    out=prod[:], in_=streams[1][c], func=ACT.Copy, scale=w[:, 2 * r + 1 : 2 * r + 2]
+                )
+                multiply_add(hidden[:, r, c, :], streams[0][c], w[:, 2 * r : 2 * r + 1], prod[:])
+
         h_grouped = keep.tile([P, 2, TOKENS, PACK], BF16, align_bytes=64)
         h_codes = keep.tile([P, 2, TOKENS], U32, align_bytes=64)
         h_scales = keep.tile([P, 2, TOKENS], U8, align_bytes=64)
-        nc.vector.tensor_copy(out=h_grouped[:, 0].rearrange("p t (u e) -> p t u e", u=2), in_=h_view[:, 0])
-        nc.scalar.copy(out=h_grouped[:, 1].rearrange("p t (u e) -> p t u e", u=2), in_=h_view[:, 1])
-        out_ps = psum.tile([P, D_OUT], F32, tag="tok1")
+        out_ps = psum.tile([P, D_OUT], F32, tag="spare1")
+        nc.scalar.copy(out=h_grouped[:, 0], in_=hidden[:, 0].rearrange("p k t -> p t k"))
+        nc.vector.tensor_copy(out=h_grouped[:, 1], in_=hidden[:, 1].rearrange("p k t -> p t k"))
         for g in range(2):
             nc.vector.quantize_mx(
                 out=h_codes[:, g, :].bitcast(FP8X4),

@@ -30,16 +30,12 @@ PAIRS = (((0, 1), (2, 3)), ((0, 2), (1, 3)))
 AFTER_PAIRS = (0, 2, 1, 3)
 
 FLIPS = (
-    (dict(a=2, b=8, c=2, d=4), "d c b a", "c"),
-    (dict(a=2, b=2, c=4, d=8), "c b a d", "a"),
-    (dict(a=2, b=8, c=2, d=4), "d c a b", "c"),
-    (dict(a=2, b=8, c=2, d=4), "d a b c", "a"),
+    (dict(a=16, b=4, c=2), "a b c", "b a c", "c", 1),
+    (dict(a=2, b=4, c=2, d=8), "a b c d", "b a c d", "c", 8),
+    (dict(a=2, b=16, d=4), "a b d", "d a b", "a", 64),
 )
-LOW_RUN = (1, 8, 8, 16)
-
-
-def flip_of(n):
-    return 3 if n == LAYOUTS - 1 else n % 3
+LOW_RUN = (1, 8, 16)
+VECTOR_PRODUCTS = ((2, 1), (3, 0), (3, 1))
 
 
 def tile_butterflymlp_s_kernel(
@@ -54,10 +50,9 @@ def tile_butterflymlp_s_kernel(
         psum = ctx.enter_context(tc.psum_pool(name="psum", bufs=1))
 
         x_sb = keep.tile([P, D_IN], BF16)
-        w_exp_raw = keep.tile([P, PACK, HIDDEN], BF16)
-        unit_w = [None] * LAYOUTS
-        turn_w = [None] * LAYOUTS
-        rows = [None] * LAYOUTS
+        w_exp_raw = [keep.tile([P, PACK, HIDDEN // 2], BF16, name="w_exp_raw%d" % h) for h in range(STREAMS)]
+        unit_w = {}
+        turn_w = {}
         for n in (0, 3):
             unit_w[n] = keep.tile([P, 8, 4], BF16, name="unit_w%d" % n)
             turn_w[n] = keep.tile([P, 8, 4], BF16, name="turn_w%d" % n)
@@ -74,46 +69,44 @@ def tile_butterflymlp_s_kernel(
 
         def load_low(queue, n):
             for s in range(2):
-                view = weights_of(n, s).rearrange("(h q v g) r c -> v q h (g r c)", h=2, q=64, v=2, g=2)
-                for v in range(2):
-                    dst = unit_w[n][64 * v : 64 * v + 64, 4 * s : 4 * s + 4]
-                    queue.dma_start(out=dst.rearrange("q (h g) e -> q h (g e)", h=2), in_=view[v])
+                queue.dma_start(
+                    out=unit_w[n][:, 4 * s : 4 * s + 4].rearrange("p (h g) e -> p h (g e)", h=2),
+                    in_=weights_of(n, s).rearrange("(h p g) r c -> p h (g r c)", h=2, p=P),
+                )
             view = weights_of(n, 2).rearrange("(h q c) r s -> q h (c r s)", h=2, q=64)
             for v in range(2):
-                dst = turn_w[n][64 * v : 64 * v + 64]
-                queue.dma_start(out=dst.rearrange("q (h c) e -> q h (c e)", h=2), in_=view)
+                queue.dma_start(out=turn_w[n][v:P:2].rearrange("q (h c) e -> q h (c e)", h=2), in_=view)
 
         def load_rows(queue, n):
-            pairs = rows[n].rearrange("r (v e) -> r v e", v=2)
-            if n % 3 == 1:
-                for s in range(2):
-                    view = weights_of(n, s).rearrange("(h x v g y) r c -> h v g x (y r c)", h=2, x=8, v=2, g=2)
+            pairs = row_tiles[n // 3][:].bitcast(BF16)
+            layout = n % 3 - 1
+            unit_row = [4 * layout, 8 + 4 * layout]
+            turn_row = 16 + 8 * layout
+            for s in range(2):
+                if n % 3 == 1:
+                    view = weights_of(n, s).rearrange("(h x g y) r c -> h g x (y r c)", h=2, x=16, g=2)
+                else:
+                    view = weights_of(n, s).rearrange("(h x g y) r c -> h g x (y r c)", h=2, x=2, g=2)
+                for h in range(2):
+                    r = unit_row[s] + 2 * h
+                    queue.dma_start(out=pairs[r : r + 2].rearrange("g (x e) -> g x e", x=view.shape[2]), in_=view[h])
+            for v in range(2):
+                if n % 3 == 1:
+                    view = weights_of(n, 2).rearrange("(h x c y) r s -> h c x (y r s)", h=2, x=8, c=4)
                     for h in range(2):
-                        r = 4 * s + 2 * h
-                        for v in range(2):
-                            dst = pairs[r : r + 2, v].rearrange("g (x e) -> g x e", x=8)
-                            queue.dma_start(out=dst, in_=view[h, v])
-                view = weights_of(n, 2).rearrange("(h x c y) r s -> h c x (y r s)", h=2, x=8, c=4)
-                for h in range(2):
-                    r = 8 + 4 * h
-                    for v in range(2):
-                        queue.dma_start(out=pairs[r : r + 4, v].rearrange("c (x e) -> c x e", x=8), in_=view[h])
-            else:
-                view = weights_of(n, 0).rearrange("(h v g y) r c -> h g v (y r c)", h=2, v=2, g=2)
-                for h in range(2):
-                    queue.dma_start(out=pairs[2 * h : 2 * h + 2], in_=view[h])
-                view = weights_of(n, 1).rearrange("(h v g y) r c -> h g v (y r c)", h=2, v=2, g=2)
-                for h in range(2):
-                    queue.dma_start(out=pairs[4 + 2 * h : 6 + 2 * h], in_=view[h])
-                view = weights_of(n, 2).rearrange("(q y) r c -> q (y r c)", q=8)
-                for v in range(2):
-                    queue.dma_start(out=pairs[8:16, v], in_=view)
+                        r = turn_row + 4 * h
+                        queue.dma_start(
+                            out=pairs[r : r + 4].rearrange("c (x v e) -> c v x e", x=8, v=2)[:, v], in_=view[h]
+                        )
+                else:
+                    queue.dma_start(
+                        out=pairs[turn_row : turn_row + 8].rearrange("q (v e) -> q v e", v=2)[:, v],
+                        in_=weights_of(n, 2).rearrange("(q y) r c -> q (y r c)", q=8),
+                    )
 
-        row_tiles = {}
-        for n in (1, 2, 4, 5):
-            row_tiles[n] = keep.tile([P, 2 * P], F32, name="rows%d" % n)
-            nc.vector.memset(row_tiles[n][:], 0.0)
-            rows[n] = row_tiles[n][:].bitcast(BF16)
+        row_tiles = [keep.tile([P, 2 * P], F32, name="rows%d" % i) for i in range(2)]
+        for i in range(2):
+            nc.vector.memset(row_tiles[i][:], 0.0)
         zero_column = keep.tile([P, 1], F32)
         gelu_of_zero = keep.tile([P, 1], F32)
         nc.vector.memset(zero_column[:], 0.0)
@@ -121,21 +114,16 @@ def tile_butterflymlp_s_kernel(
         nc.sync.dma_start(out=x_sb[:], in_=x.flatten_outer_dims())
         for h in range(STREAMS):
             cols = slice(HIDDEN // 2 * h, HIDDEN // 2 * (h + 1))
-            nc.sync.dma_start(out=w_exp_raw[:, :, cols], in_=W_exp[:, cols].rearrange("(p t) c -> p t c", t=PACK))
+            nc.sync.dma_start(out=w_exp_raw[h][:], in_=W_exp[:, cols].rearrange("(p t) c -> p t c", t=PACK))
             if h == 0:
                 load_low(nc.sync, 0)
-        view = b_exp.rearrange("(h q v c) -> v q h c", h=2, q=64, v=2)
-        for v in range(2):
-            nc.sync.dma_start(out=b_exp_sb[64 * v : 64 * v + 64], in_=view[v])
+        nc.sync.dma_start(out=b_exp_sb[:], in_=b_exp.rearrange("(h p c) -> p h c", h=2, c=CHUNKS))
         load_rows(nc.sync, 1)
         load_rows(nc.sync, 2)
-        view = up_weights[9].rearrange("(q v c) r s -> v q (c r s)", v=2, c=4)
-        for v in range(2):
-            dst = up_last_w[64 * v : 64 * v + 64]
-            nc.sync.dma_start(out=dst.rearrange("q c e -> q (c e)"), in_=view[v])
-        view = up_bias.rearrange("(h q v c) -> v q h c", h=2, q=64, v=2)
-        for v in range(2):
-            nc.sync.dma_start(out=up_bias_sb[64 * v : 64 * v + 64], in_=view[v])
+        nc.sync.dma_start(
+            out=up_last_w[:].rearrange("p c e -> p (c e)"), in_=up_weights[9].rearrange("(p c) r s -> p (c r s)", c=CHUNKS)
+        )
+        nc.sync.dma_start(out=up_bias_sb[:], in_=up_bias.rearrange("(h p c) -> p h c", h=2, c=CHUNKS))
         load_low(nc.sync, 3)
         nc.sync.dma_start(
             out=w_con_raw[:].rearrange("p g t c -> p g (t c)"),
@@ -149,23 +137,39 @@ def tile_butterflymlp_s_kernel(
         nc.sync.dma_start(out=b_con_rows[:], in_=b_con.partition_broadcast(P))
         nc.sync.dma_start(out=down_bias_rows[:], in_=down_bias.partition_broadcast(P))
 
-        identity = keep.tile([P, P + 64], F32)
-        make_identity(nc, identity[:, 0:P])
+        identity = keep.tile([P, P], F32)
+        make_identity(nc, identity[:])
         nc.scalar.activation(out=gelu_of_zero[:], in_=zero_column[:], func=ACT.Gelu)
-        nc.scalar.copy(out=identity[:, P : P + 64], in_=identity[:, 0:64])
         flips = keep.tile([P, len(FLIPS), 2, P], F32)
-        for kind, (sizes, order, loop) in enumerate(FLIPS):
-            rest = [g for g in order.split(" ") if g != loop]
-            for turned in range(2):
-                src = identity[:, 64 * turned : 64 * turned + P].rearrange(
-                    "p (a b c d) -> p %s %s" % (loop, " ".join(rest)), **sizes
-                )
-                dst = flips[:, kind, turned].rearrange("p (%s) -> p %s %s" % (order, loop, " ".join(rest)), **sizes)
-                for i in range(sizes[loop]):
-                    nc.scalar.copy(out=dst[:, i], in_=src[:, i])
+        bit_is = keep.tile([P, len(FLIPS), 2], F32)
+
+        def make_flips():
+            for k, (sizes, old, new, turned, weight) in enumerate(FLIPS):
+                src = identity[:].rearrange("p (%s) -> p %s" % (old, new), **sizes)
+                dst = flips[:, k, 0].rearrange("p (%s) -> p %s" % (new, new), **sizes)
+                if k == 1:
+                    src = src.rearrange("p b a c d -> p b a (c d)")
+                    dst = dst.rearrange("p b a c d -> p b a (c d)")
+                nc.vector.tensor_copy(out=dst, in_=src)
+                rest = [g for g in new.split(" ") if g != turned]
+                src = identity[:].rearrange("p (%s) -> p %s %s" % (old, turned, " ".join(rest)), **sizes)
+                dst = flips[:, k, 1].rearrange("p (%s) -> p %s %s" % (new, turned, " ".join(rest)), **sizes)
+                for r in range(2):
+                    nc.vector.tensor_copy(out=dst[:, r], in_=src[:, 1 - r])
+            for k, (sizes, old, new, turned, weight) in enumerate(FLIPS):
+                by_bit = identity[:].rearrange("p (x r y) -> p r x y", r=2, y=weight)
+                for r in range(2):
+                    nc.vector.tensor_reduce(
+                        out=bit_is[:, k, r : r + 1], in_=by_bit[:, r], op=ALU.add, axis=mybir.AxisListType.XY
+                    )
+
+        make_flips()
 
         out_bias = keep.tile([P, D_OUT], F32)
         nc.gpsimd.tensor_tensor(out=out_bias[:], in0=b_con_rows[:], in1=down_bias_rows[:], op=ALU.add)
+
+        def multiply_add(out, in0, scalar, in1):
+            nc.vector.scalar_tensor_tensor(out=out, in0=in0, scalar=scalar, in1=in1, op0=ALU.mult, op1=ALU.add)
 
         steps = []
 
@@ -192,51 +196,64 @@ def tile_butterflymlp_s_kernel(
             steps.append(lambda: nc.vector.reciprocal(out=div[:], in_=rec[:]))
             return rec, factor, div
 
-        factors = [None] * LAYOUTS
-        turn_factors = [None] * LAYOUTS
+        factors = {}
+        turn_factors = {}
 
-        def queue_scalars(n):
-            rec, factor, div = divide_out(unit_w[n][:], "%d" % n)
-            div0 = div[:, 0:4].rearrange("p (h x) z -> p h x z", h=2)
-            rec0 = rec[:, 0:4].rearrange("p (h x) z -> p h x z", h=2)
-            div1 = div[:, 4:8].rearrange("p (h z) x -> p h x z", h=2)
-            correction = keep.tile([P, 4, 2], F32, name="correction%d" % n)
-            carried = keep.tile([P, 8], F32, name="carried%d" % n)
-            for r in range(2):
-                multiply(
-                    correction[:, :, r].rearrange("p (h z) -> p h z", h=2), div0[:, :, 1 - r, :], rec0[:, :, r, :]
+        def queue_scalars(layouts, w_unit, w_turn):
+            name = "%d" % layouts[0]
+            size = len(layouts)
+            half = 4 * size
+            rec, factor, div = divide_out(w_unit, name)
+            div0 = div[:, 0:half].rearrange("p (h x) z -> p h x z", x=2)
+            rec0 = rec[:, 0:half].rearrange("p (h x) z -> p h x z", x=2)
+            div1 = div[:, half:].rearrange("p (h z) x -> p h x z", z=2)
+            correction = keep.tile([P, half, 2], F32, name="correction" + name)
+            carried = keep.tile([P, 2 * half], F32, name="carried" + name)
+            multiply(
+                correction[:].rearrange("p (h z) r -> p h z r", z=2),
+                div0.rearrange("p h x z -> p h z x")[:, :, :, ::-1],
+                rec0.rearrange("p h x z -> p h z x"),
+            )
+            multiply(carried[:].rearrange("p (h x z) -> p h x z", x=2, z=2), div1, div0)
+            multiply(factor[:, half:], factor[:, half:], correction[:])
+            turn = keep.tile([P, 2 * half, 2], F32, name="turn" + name)
+            pieces = [(i, n % 3, slice(8 * i, 8 * i + 8)) for i, n in enumerate(layouts)]
+
+            def select(k, cols):
+                steps.append(
+                    lambda: nc.vector.tensor_scalar(
+                        out=turn[:, cols], in0=w_turn[:, cols, 0:4:2], scalar1=bit_is[:, k, 0:1], scalar2=None, op0=ALU.mult
+                    )
                 )
-            multiply(carried[:].rearrange("p (h x z) -> p h x z", h=2, x=2), div1, div0)
-            multiply(factor[:, 4:8], factor[:, 4:8], correction[:])
-            turn = keep.tile([P, 8, 2], F32, name="turn%d" % n)
-            w = turn_w[n]
-            for s, e in enumerate((0, 2)):
-                multiply(turn[0:64, :, s], w[0:64, :, e], carried[0:64])
-            for s, e in enumerate((3, 1)):
-                multiply(turn[64:128, :, s], w[64:128, :, e], carried[64:128])
-            factors[n] = factor
-            turn_factors[n] = turn
+                steps.append(
+                    lambda: multiply_add(turn[:, cols], w_turn[:, cols, 3:0:-2], bit_is[:, k, 1:2], turn[:, cols])
+                )
+
+            for i, k, cols in pieces:
+                select(k, cols)
+            multiply(turn[:], turn[:], carried[:].unsqueeze(2).to_broadcast([P, 2 * half, 2]))
+            for i, n in enumerate(layouts):
+                factors[n] = [factor[:, half * j + 4 * i : half * j + 4 * i + 4] for j in range(2)]
+                turn_factors[n] = turn[:, 8 * i : 8 * i + 8]
 
         def turn_rows(n):
-            words = row_tiles[n]
+            words = row_tiles[n // 3]
             turned = psum.tile([P, 2, P], F32, tag="spare0", name="turned%d" % n)
             for w in range(2):
-                nc.tensor.transpose(turned[:, w, :], words[:, w : 2 * P : 2], identity[:, 0:P])
-            landed = keep.tile([P, 16, 2], F32, name="landed%d" % n)
+                nc.tensor.transpose(turned[:, w, :], words[:, w : 2 * P : 2], identity[:])
+            landed = keep.tile([P, 32, 2], F32, name="landed%d" % n)
             steps.append(
-                lambda: nc.vector.tensor_copy(out=landed[:], in_=turned[:, :, 0:16].rearrange("p w r -> p r w"))
+                lambda: nc.vector.tensor_copy(out=landed[:], in_=turned[:, :, 0:32].rearrange("p w r -> p r w"))
             )
             pairs = landed[:].rearrange("p r w -> p (r w)").bitcast(BF16).rearrange("p (r e) -> p r e", e=4)
-            unit_w[n] = pairs[:, 0:8]
-            turn_w[n] = pairs[:, 8:16]
-            queue_scalars(n)
+            queue_scalars((n, n + 1), pairs[:, 0:16], pairs[:, 16:32])
 
-        queue_scalars(0)
+        queue_scalars((0,), unit_w[0][:], turn_w[0][:])
 
         x_words = x_sb[:].bitcast(F32)
         x_t = psum.tile([P, 2, TOKENS], F32, tag="spare1")
         for u in range(2):
-            nc.tensor.transpose(x_t[:, u, :], x_words[:, u : 2 * P : 2], identity[:, 0:P])
+            nc.tensor.transpose(x_t[:, u, :], x_words[:, u : 2 * P : 2], identity[:])
         x_grouped = keep.tile([P, TOKENS, 2], F32, align_bytes=64)
         nc.vector.tensor_copy(out=x_grouped[:], in_=x_t[:].rearrange("p u t -> p t u"))
         x_codes = keep.tile([P, TOKENS], U32, align_bytes=64)
@@ -246,10 +263,11 @@ def tile_butterflymlp_s_kernel(
         w_exp_codes = keep.tile([P, STREAMS, CHUNKS, P], U32, align_bytes=64)
         w_exp_scales = keep.tile([P, STREAMS, CHUNKS, P], U8, align_bytes=64)
 
-        def regroup_w_exp(copy, h, v):
-            src = w_exp_raw[:, :, 512 * h : 512 * h + 512].rearrange("p t (q v c) -> p v q t c", v=2, c=CHUNKS)
-            dst = w_exp_grouped[:, h].rearrange("p c (v q) t -> p v q t c", v=2)
-            copy(out=dst[:, v], in_=src[:, v])
+        def regroup_w_exp(copy, h, half):
+            m = slice(P // 2 * half, P // 2 * (half + 1))
+            src = w_exp_raw[h][:].rearrange("p t (m c) -> p m t c", c=CHUNKS)
+            dst = w_exp_grouped[:, h].rearrange("p c m t -> p m t c")
+            copy(out=dst[:, m], in_=src[:, m])
 
         def quantise_w_exp(h):
             nc.vector.quantize_mx(
@@ -281,13 +299,13 @@ def tile_butterflymlp_s_kernel(
 
         regroup_w_exp(nc.vector.tensor_copy, 0, 0)
         run_steps(1)
-        regroup_w_exp(nc.vector.tensor_copy, 0, 1)
-        run_steps(1)
+        regroup_w_exp(nc.scalar.copy, 0, 1)
         nc.vector.quantize_mx(
             out=x_codes[:].bitcast(FP8X4),
             scales=x_scales[:],
             in_=x_grouped[:].rearrange("p t u -> p (t u)").bitcast(BF16),
         )
+        run_steps(1)
         quantise_w_exp(0)
         run_steps(1)
         regroup_w_exp(nc.scalar.copy, 1, 1)
@@ -315,9 +333,6 @@ def tile_butterflymlp_s_kernel(
                 in_=w_con_grouped[:, g].rearrange("p c t -> p (c t)"),
             )
 
-        def multiply_add(out, in0, scalar, in1):
-            nc.vector.scalar_tensor_tensor(out=out, in0=in0, scalar=scalar, in1=in1, op0=ALU.mult, op1=ALU.add)
-
         def work_tile(name):
             return products.tile([P, TOKENS], F32, tag="work", name=name)
 
@@ -329,43 +344,44 @@ def tile_butterflymlp_s_kernel(
                 nc.scalar.activation(out=copied[:], in_=chunk, func=ACT.Identity, bias=bias)
             return copied[:]
 
-        def unit_stages(h, n, count):
-            chunk = list(streams[h])
+        def copies(h, n):
             if n == 0:
                 for c in CHUNK_ORDER:
-                    chunk[c] = out_of_psum(chunk[c], bias=b_exp_sb[:, h, c : c + 1])
+                    streams[h][c] = out_of_psum(streams[h][c], bias=b_exp_sb[:, h, c : c + 1])
             elif n != 3:
                 for c in (1, 3):
-                    chunk[c] = out_of_psum(chunk[c])
+                    streams[h][c] = out_of_psum(streams[h][c])
+
+        def units(h, n, count):
             for j in range(2):
                 new = data.tile([P, CHUNKS, TOKENS], F32, tag="chunks%d" % h, name="chunks%d" % h)
+                chunk = streams[h]
                 for i, (a, b) in enumerate(PAIRS[j]):
-                    factor = factors[n][:, 4 * j + 2 * h + i]
+                    factor = factors[n][j][:, 2 * h + i]
                     multiply_add(new[:, a, :], chunk[b], factor[:, 0:1], chunk[a])
                     multiply_add(new[:, b, :], chunk[a], factor[:, 1:2], chunk[b])
                     run_steps(count)
-                chunk = [new[:, c, :] for c in range(CHUNKS)]
-            streams[h] = chunk
+                streams[h] = [new[:, c, :] for c in range(CHUNKS)]
 
         flipped = [None, None]
 
-        def turn_stage(h, n):
-            flipped[h] = psum.tile([P, CHUNKS, P], F32, tag="flipped%d" % h, name="flipped%d" % h)
-            prods = {}
-            for c in AFTER_PAIRS:
+        def turn_stage(h, n, chunks):
+            if chunks[0] == 0:
+                flipped[h] = psum.tile([P, CHUNKS, P], F32, tag="flipped%d" % h, name="flipped%d" % h)
+            for c in chunks:
                 for s in range(2):
-                    prods[c, s] = work_tile("product")
+                    prod = work_tile("product")
                     scalar = turn_factors[n][:, 4 * h + c, s : s + 1]
-                    if s == 1 and c >= 2:
+                    if (c, s) in VECTOR_PRODUCTS:
                         nc.vector.tensor_scalar(
-                            out=prods[c, s][:], in0=streams[h][c], scalar1=scalar, scalar2=None, op0=ALU.mult
+                            out=prod[:], in0=streams[h][c], scalar1=scalar, scalar2=None, op0=ALU.mult
                         )
                     else:
-                        nc.scalar.activation(out=prods[c, s][:], in_=streams[h][c], func=ACT.Copy, scale=scalar)
+                        nc.scalar.activation(out=prod[:], in_=streams[h][c], func=ACT.Copy, scale=scalar)
                     nc.tensor.matmul(
                         flipped[h][:, c, :],
-                        lhsT=prods[c, s][:],
-                        rhs=flips[:, flip_of(n), s, :],
+                        lhsT=prod[:],
+                        rhs=flips[:, n % 3, s, :],
                         start=(s == 0),
                         stop=(s == 1),
                         is_transpose=True,
@@ -374,47 +390,58 @@ def tile_butterflymlp_s_kernel(
         def turn_back(h, n):
             by_token = data.tile([P, CHUNKS, P], F32, tag="by_token%d" % h, name="by_token%d" % h)
             new = new_psum_chunks(h)
+            run = LOW_RUN[n % 3]
             for c in CHUNK_ORDER:
-                run = LOW_RUN[flip_of(n)]
                 nc.scalar.copy(
                     out=by_token[:, c].rearrange("t (x a y) -> t x a y", a=CHUNKS, y=run),
                     in_=flipped[h][:, :, 32 * c : 32 * c + 32].rearrange("t a (x y) -> t x a y", y=run),
                 )
-                nc.tensor.transpose(new[c], by_token[:, c], identity[:, 0:P])
+                nc.tensor.transpose(new[c], by_token[:, c], identity[:])
             streams[h] = new
 
-        unit_stages(0, 0, 2)
-        run_steps(len(steps))
-        turn_stage(0, 0)
-        turn_rows(1)
-        unit_stages(1, 0, 1)
-        turn_back(0, 0)
-        turn_stage(1, 0)
-        run_steps(len(steps))
-        for n in (1, 2):
-            if n == 2:
-                queue_scalars(3)
-            else:
-                turn_rows(2)
-            if n == 2:
-                up_last_rec, up_last_factor, up_last_div = divide_out(up_last_w[:], "_last")
-            unit_stages(0, n, 1)
-            turn_back(1, n - 1)
-            turn_stage(0, n)
-            unit_stages(1, n, 2 if n == 2 else 1)
+        def layout(n, first_steps, second_steps):
+            units(0, n, first_steps)
+            if n not in (0, 3):
+                turn_back(1, n - 1)
+            turn_stage(0, n, (0, 2, 3, 1))
+            copies(1, n)
+            units(1, n, second_steps)
             turn_back(0, n)
-            turn_stage(1, n)
+            turn_stage(1, n, (0, 2, 3, 1))
+            if n not in (2, 5):
+                copies(0, n + 1)
             run_steps(len(steps))
+
+        copies(0, 0)
+        units(0, 0, 2)
+        run_steps(len(steps))
+        copies(1, 0)
+        turn_stage(0, 0, (0,))
+        turn_stage(0, 0, (2,))
+        turn_rows(1)
+        turn_stage(0, 0, (3, 1))
+        units(1, 0, 2)
+        turn_back(0, 0)
+        turn_stage(1, 0, (0,))
+        copies(0, 1)
+        turn_stage(1, 0, (2, 3, 1))
+        run_steps(len(steps))
+        layout(1, 0, 0)
+        queue_scalars((3,), unit_w[3][:], turn_w[3][:])
+        up_last_rec, up_last_factor, up_last_div = divide_out(up_last_w[:], "_last")
+        layout(2, 1, 1)
         turn_back(1, 2)
 
         raised = [data.tile([P, CHUNKS, TOKENS], F32, tag="chunks%d" % h, name="raised%d" % h) for h in range(2)]
-        copied = [out_of_psum(streams[1][c]) for c in range(CHUNKS)]
-        for c in range(CHUNKS):
+        for quarter in range(3):
+            regroup_w_con(quarter)
+        copied = {c: out_of_psum(streams[1][c]) for c in CHUNK_ORDER}
+        for c in CHUNK_ORDER:
             multiply_add(raised[0][:, c, :], copied[c], up_last_factor[:, c, 0:1], streams[0][c])
-        for c in range(CHUNKS):
+        for c in CHUNK_ORDER:
             multiply_add(raised[1][:, c, :], streams[0][c], up_last_factor[:, c, 1:2], copied[c])
         for h in range(2):
-            for c in range(CHUNKS):
+            for c in CHUNK_ORDER:
                 nc.scalar.activation(
                     out=raised[h][:, c, :],
                     in_=raised[h][:, c, :],
@@ -425,33 +452,19 @@ def tile_butterflymlp_s_kernel(
             streams[h] = [raised[h][:, c, :] for c in range(CHUNKS)]
 
         down_last_f = keep.tile([P, CHUNKS, 4], F32)
-        for n in (3, 4, 5):
-            if n < 5:
-                turn_rows(n + 1)
-            else:
-                steps.append(lambda: nc.vector.tensor_copy(out=down_last_f[:], in_=down_last_w[:]))
-            unit_stages(0, n, 1)
-            if n > 3:
-                turn_back(1, n - 1)
-            turn_stage(0, n)
-            unit_stages(1, n, 1)
-            turn_back(0, n)
-            turn_stage(1, n)
-            run_steps(len(steps))
-            if n == 3:
-                regroup_w_con(0)
-                regroup_w_con(1)
-            if n == 4:
-                regroup_w_con(2)
-                regroup_w_con(3)
-            if n == 5:
-                quantise_w_con(0)
-                quantise_w_con(1)
+        turn_rows(4)
+        layout(3, 1, 1)
+        layout(4, 0, 0)
+        layout(5, 0, 0)
+        nc.vector.tensor_copy(out=down_last_f[:], in_=down_last_w[:])
         turn_back(1, 5)
+        regroup_w_con(3)
+        quantise_w_con(0)
+        quantise_w_con(1)
 
         hidden = keep.tile([P, STREAMS, CHUNKS, TOKENS], F32)
         for r in range(2):
-            for c in range(CHUNKS):
+            for c in CHUNK_ORDER:
                 prod = work_tile("product")
                 w = down_last_f[:, c]
                 nc.scalar.activation(
@@ -462,24 +475,30 @@ def tile_butterflymlp_s_kernel(
         h_grouped = keep.tile([P, 2, TOKENS, PACK], BF16, align_bytes=64)
         h_codes = keep.tile([P, 2, TOKENS], U32, align_bytes=64)
         h_scales = keep.tile([P, 2, TOKENS], U8, align_bytes=64)
-        out_ps = psum.tile([P, D_OUT], F32, tag="spare1")
         nc.scalar.copy(out=h_grouped[:, 0], in_=hidden[:, 0].rearrange("p k t -> p t k"))
         nc.vector.tensor_copy(out=h_grouped[:, 1], in_=hidden[:, 1].rearrange("p k t -> p t k"))
+        half_cols = D_OUT // 2
+        out_ps = [psum.tile([P, half_cols], F32, tag="spare%d" % i, name="out_ps%d" % i) for i in range(2)]
+        out_sb = keep.tile([P, 2, half_cols], F32)
         for g in range(2):
             nc.vector.quantize_mx(
                 out=h_codes[:, g, :].bitcast(FP8X4),
                 scales=h_scales[:, g, :],
                 in_=h_grouped[:, g].rearrange("p t k -> p (t k)"),
             )
-            nc.tensor.matmul_mx(
-                out=out_ps[:],
-                lhsT=h_codes[:, g, :].bitcast(FP8X4),
-                lhsT_scale=h_scales[:, g, :],
-                rhs=w_con_codes[:, g, :].bitcast(FP8X4),
-                rhs_scale=w_con_scales[:, g, :],
-                start=(g == 0),
-                stop=(g == 1),
-            )
-        out_sb = keep.tile([P, D_OUT], F32)
-        nc.vector.tensor_tensor(out=out_sb[:], in0=out_ps[:], in1=out_bias[:], op=ALU.add)
-        nc.sync.dma_start(out=out.flatten_outer_dims(), in_=out_sb[:])
+        for g in range(2):
+            for i in range(2):
+                cols = slice(half_cols * i, half_cols * (i + 1))
+                nc.tensor.matmul_mx(
+                    out=out_ps[i][:],
+                    lhsT=h_codes[:, g, :].bitcast(FP8X4),
+                    lhsT_scale=h_scales[:, g, :],
+                    rhs=w_con_codes[:, g, cols].bitcast(FP8X4),
+                    rhs_scale=w_con_scales[:, g, cols],
+                    start=(g == 0),
+                    stop=(g == 1),
+                )
+        for i in range(2):
+            cols = slice(half_cols * i, half_cols * (i + 1))
+            nc.vector.tensor_tensor(out=out_sb[:, i], in0=out_ps[i][:], in1=out_bias[:, cols], op=ALU.add)
+            nc.sync.dma_start(out=out.flatten_outer_dims()[:, cols], in_=out_sb[:, i])

@@ -27,7 +27,6 @@ FLOPS = 2 * TOKENS * D_IN * HIDDEN + 2 * TOKENS * HIDDEN * D_OUT + STAGES * TOKE
 
 CHUNK_ORDER = (1, 0, 3, 2)
 PAIRS = (((0, 1), (2, 3)), ((0, 2), (1, 3)))
-AFTER_PAIRS = (0, 2, 1, 3)
 
 FLIPS = (
     (dict(a=16, b=4, c=2), "a b c", "b a c", "c", 1),
@@ -35,7 +34,8 @@ FLIPS = (
     (dict(a=2, b=16, d=4), "a b d", "d a b", "a", 64),
 )
 LOW_RUN = (1, 8, 16)
-VECTOR_PRODUCTS = ((2, 1), (3, 0), (3, 1))
+TURN_ORDER = (0, 2, 3, 1)
+VECTOR_PRODUCTS = ((1, 1), (2, 1), (3, 0), (3, 1))
 
 
 def tile_butterflymlp_s_kernel(
@@ -214,8 +214,8 @@ def tile_butterflymlp_s_kernel(
                 div0.rearrange("p h x z -> p h z x")[:, :, :, ::-1],
                 rec0.rearrange("p h x z -> p h z x"),
             )
-            multiply(carried[:].rearrange("p (h x z) -> p h x z", x=2, z=2), div1, div0)
             multiply(factor[:, half:], factor[:, half:], correction[:])
+            multiply(carried[:].rearrange("p (h x z) -> p h x z", x=2, z=2), div1, div0)
             turn = keep.tile([P, 2 * half, 2], F32, name="turn" + name)
             pieces = [(i, n % 3, slice(8 * i, 8 * i + 8)) for i, n in enumerate(layouts)]
 
@@ -238,7 +238,7 @@ def tile_butterflymlp_s_kernel(
 
         def turn_rows(n):
             words = row_tiles[n // 3]
-            turned = psum.tile([P, 2, P], F32, tag="spare0", name="turned%d" % n)
+            turned = psum.tile([P, 2, P], F32, tag="flip0_1", name="turned%d" % n)
             for w in range(2):
                 nc.tensor.transpose(turned[:, w, :], words[:, w : 2 * P : 2], identity[:])
             landed = keep.tile([P, 32, 2], F32, name="landed%d" % n)
@@ -251,7 +251,7 @@ def tile_butterflymlp_s_kernel(
         queue_scalars((0,), unit_w[0][:], turn_w[0][:])
 
         x_words = x_sb[:].bitcast(F32)
-        x_t = psum.tile([P, 2, TOKENS], F32, tag="spare1")
+        x_t = psum.tile([P, 2, TOKENS], F32, tag="flip0_0", name="x_t")
         for u in range(2):
             nc.tensor.transpose(x_t[:, u, :], x_words[:, u : 2 * P : 2], identity[:])
         x_grouped = keep.tile([P, TOKENS, 2], F32, align_bytes=64)
@@ -352,23 +352,32 @@ def tile_butterflymlp_s_kernel(
                 for c in (1, 3):
                     streams[h][c] = out_of_psum(streams[h][c])
 
-        def units(h, n, count):
+        def units(h, n, step_count=0):
+            left = step_count
             for j in range(2):
                 new = data.tile([P, CHUNKS, TOKENS], F32, tag="chunks%d" % h, name="chunks%d" % h)
                 chunk = streams[h]
                 for i, (a, b) in enumerate(PAIRS[j]):
                     factor = factors[n][j][:, 2 * h + i]
                     multiply_add(new[:, a, :], chunk[b], factor[:, 0:1], chunk[a])
+                    run_steps(min(left, 1))
                     multiply_add(new[:, b, :], chunk[a], factor[:, 1:2], chunk[b])
-                    run_steps(count)
+                    run_steps(min(left - 1, 1) if left else 0)
+                    left = max(left - 2, 0)
                 streams[h] = [new[:, c, :] for c in range(CHUNKS)]
 
-        flipped = [None, None]
+        flipped = {}
 
-        def turn_stage(h, n, chunks):
-            if chunks[0] == 0:
-                flipped[h] = psum.tile([P, CHUNKS, P], F32, tag="flipped%d" % h, name="flipped%d" % h)
-            for c in chunks:
+        def turn_stage(h, n):
+            banks = [
+                psum.tile([P, CHUNKS, P], F32, tag="flip%d_%d" % (h, i), name="flip%d_%d" % (h, i)) for i in range(1 if LOW_RUN[n % 3] == 1 else 2)
+            ]
+            if LOW_RUN[n % 3] == 1:
+                flipped[h] = {c: banks[0][:, c, :] for c in range(CHUNKS)}
+            else:
+                flipped[h] = {c: banks[c & 1][:, c >> 1, :] for c in range(CHUNKS)}
+            flipped[h, "banks"] = banks
+            for c in TURN_ORDER:
                 for s in range(2):
                     prod = work_tile("product")
                     scalar = turn_factors[n][:, 4 * h + c, s : s + 1]
@@ -379,7 +388,7 @@ def tile_butterflymlp_s_kernel(
                     else:
                         nc.scalar.activation(out=prod[:], in_=streams[h][c], func=ACT.Copy, scale=scalar)
                     nc.tensor.matmul(
-                        flipped[h][:, c, :],
+                        flipped[h][c],
                         lhsT=prod[:],
                         rhs=flips[:, n % 3, s, :],
                         start=(s == 0),
@@ -391,45 +400,50 @@ def tile_butterflymlp_s_kernel(
             by_token = data.tile([P, CHUNKS, P], F32, tag="by_token%d" % h, name="by_token%d" % h)
             new = new_psum_chunks(h)
             run = LOW_RUN[n % 3]
-            for c in CHUNK_ORDER:
-                nc.scalar.copy(
-                    out=by_token[:, c].rearrange("t (x a y) -> t x a y", a=CHUNKS, y=run),
-                    in_=flipped[h][:, :, 32 * c : 32 * c + 32].rearrange("t a (x y) -> t x a y", y=run),
-                )
-                nc.tensor.transpose(new[c], by_token[:, c], identity[:])
+            banks = flipped[h, "banks"]
+            if run == 1:
+                for c in CHUNK_ORDER:
+                    nc.scalar.copy(
+                        out=by_token[:, c].rearrange("t (x a) -> t x a", a=CHUNKS),
+                        in_=banks[0][:, :, 32 * c : 32 * c + 32].rearrange("t a x -> t x a"),
+                    )
+                    nc.tensor.transpose(new[c], by_token[:, c], identity[:])
+            else:
+                to = by_token[:].rearrange("t c (x a b y) -> t b (c x) a y", a=2, b=2, y=run)
+                for b in range(2):
+                    nc.scalar.copy(out=to[:, b], in_=banks[b][:, 0:2, :].rearrange("t a (x y) -> t x a y", y=run))
+                for c in CHUNK_ORDER:
+                    nc.tensor.transpose(new[c], by_token[:, c], identity[:])
             streams[h] = new
 
-        def layout(n, first_steps, second_steps):
-            units(0, n, first_steps)
+        def layout(n, steps0=0, steps1=0, steps2=0):
+            units(0, n, steps0)
             if n not in (0, 3):
                 turn_back(1, n - 1)
-            turn_stage(0, n, (0, 2, 3, 1))
+            turn_stage(0, n)
             copies(1, n)
-            units(1, n, second_steps)
+            units(1, n, steps1)
             turn_back(0, n)
-            turn_stage(1, n, (0, 2, 3, 1))
+            turn_stage(1, n)
+            run_steps(steps2)
             if n not in (2, 5):
                 copies(0, n + 1)
-            run_steps(len(steps))
 
         copies(0, 0)
-        units(0, 0, 2)
+        units(0, 0, 8)
         run_steps(len(steps))
         copies(1, 0)
-        turn_stage(0, 0, (0,))
-        turn_stage(0, 0, (2,))
+        turn_stage(0, 0)
+        units(1, 0)
         turn_rows(1)
-        turn_stage(0, 0, (3, 1))
-        units(1, 0, 2)
         turn_back(0, 0)
-        turn_stage(1, 0, (0,))
+        turn_stage(1, 0)
         copies(0, 1)
-        turn_stage(1, 0, (2, 3, 1))
-        run_steps(len(steps))
-        layout(1, 0, 0)
+        run_steps(9)
         queue_scalars((3,), unit_w[3][:], turn_w[3][:])
         up_last_rec, up_last_factor, up_last_div = divide_out(up_last_w[:], "_last")
-        layout(2, 1, 1)
+        layout(1, 4, 4, 0)
+        layout(2, 4, 4, len(steps))
         turn_back(1, 2)
 
         raised = [data.tile([P, CHUNKS, TOKENS], F32, tag="chunks%d" % h, name="raised%d" % h) for h in range(2)]
@@ -453,9 +467,9 @@ def tile_butterflymlp_s_kernel(
 
         down_last_f = keep.tile([P, CHUNKS, 4], F32)
         turn_rows(4)
-        layout(3, 1, 1)
-        layout(4, 0, 0)
-        layout(5, 0, 0)
+        layout(3, 1, 8, len(steps))
+        layout(4)
+        layout(5)
         nc.vector.tensor_copy(out=down_last_f[:], in_=down_last_w[:])
         turn_back(1, 5)
         regroup_w_con(3)
@@ -478,7 +492,7 @@ def tile_butterflymlp_s_kernel(
         nc.scalar.copy(out=h_grouped[:, 0], in_=hidden[:, 0].rearrange("p k t -> p t k"))
         nc.vector.tensor_copy(out=h_grouped[:, 1], in_=hidden[:, 1].rearrange("p k t -> p t k"))
         half_cols = D_OUT // 2
-        out_ps = [psum.tile([P, half_cols], F32, tag="spare%d" % i, name="out_ps%d" % i) for i in range(2)]
+        out_ps = [psum.tile([P, half_cols], F32, tag="flip0_%d" % i, name="out_ps%d" % i) for i in range(2)]
         out_sb = keep.tile([P, 2, half_cols], F32)
         for g in range(2):
             nc.vector.quantize_mx(

@@ -34,6 +34,7 @@ FLIPS = (
     (dict(a=2, b=16, d=4), "a b d", "d a b", "a", 64),
 )
 LOW_RUN = (1, 8, 16)
+WARM = 2
 TURN_ORDER = (0, 2, 3, 1)
 VECTOR_PRODUCTS = ((1, 1), (2, 1), (3, 0), (3, 1))
 
@@ -238,7 +239,7 @@ def tile_butterflymlp_s_kernel(
 
         def turn_rows(n):
             words = row_tiles[n // 3]
-            turned = psum.tile([P, 2, P], F32, tag="flip0_1", name="turned%d" % n)
+            turned = psum.tile([P, 2, P], F32, tag="spare", name="turned%d" % n)
             for w in range(2):
                 nc.tensor.transpose(turned[:, w, :], words[:, w : 2 * P : 2], identity[:])
             landed = keep.tile([P, 32, 2], F32, name="landed%d" % n)
@@ -251,7 +252,7 @@ def tile_butterflymlp_s_kernel(
         queue_scalars((0,), unit_w[0][:], turn_w[0][:])
 
         x_words = x_sb[:].bitcast(F32)
-        x_t = psum.tile([P, 2, TOKENS], F32, tag="flip0_0", name="x_t")
+        x_t = psum.tile([P, 2, TOKENS], F32, tag="spare", name="x_t")
         for u in range(2):
             nc.tensor.transpose(x_t[:, u, :], x_words[:, u : 2 * P : 2], identity[:])
         x_grouped = keep.tile([P, TOKENS, 2], F32, align_bytes=64)
@@ -367,16 +368,26 @@ def tile_butterflymlp_s_kernel(
                 streams[h] = [new[:, c, :] for c in range(CHUNKS)]
 
         flipped = {}
+        flip_banks = [psum.tile([P, CHUNKS, P], F32, tag="flip%d" % i, name="flip%d" % i) for i in range(2)]
+        warm_bank = psum.tile([P, 4 * P], F32, tag="warm")
+
+        def keep_warm(count):
+            for i in range(count):
+                nc.tensor.matmul_mx(
+                    out=warm_bank[:],
+                    lhsT=x_codes[:].bitcast(FP8X4),
+                    lhsT_scale=x_scales[:],
+                    rhs=w_exp_codes[:, 0].rearrange("p c m -> p (c m)").bitcast(FP8X4),
+                    rhs_scale=w_exp_scales[:, 0].rearrange("p c m -> p (c m)"),
+                    start=True,
+                    stop=True,
+                )
 
         def turn_stage(h, n):
-            banks = [
-                psum.tile([P, CHUNKS, P], F32, tag="flip%d_%d" % (h, i), name="flip%d_%d" % (h, i)) for i in range(1 if LOW_RUN[n % 3] == 1 else 2)
-            ]
             if LOW_RUN[n % 3] == 1:
-                flipped[h] = {c: banks[0][:, c, :] for c in range(CHUNKS)}
+                flipped[h] = [flip_banks[h][:, c, :] for c in range(CHUNKS)]
             else:
-                flipped[h] = {c: banks[c & 1][:, c >> 1, :] for c in range(CHUNKS)}
-            flipped[h, "banks"] = banks
+                flipped[h] = [flip_banks[c & 1][:, 2 * h + (c >> 1), :] for c in range(CHUNKS)]
             for c in TURN_ORDER:
                 for s in range(2):
                     prod = work_tile("product")
@@ -395,23 +406,23 @@ def tile_butterflymlp_s_kernel(
                         stop=(s == 1),
                         is_transpose=True,
                     )
+            keep_warm(WARM)
 
         def turn_back(h, n):
             by_token = data.tile([P, CHUNKS, P], F32, tag="by_token%d" % h, name="by_token%d" % h)
             new = new_psum_chunks(h)
             run = LOW_RUN[n % 3]
-            banks = flipped[h, "banks"]
             if run == 1:
                 for c in CHUNK_ORDER:
                     nc.scalar.copy(
                         out=by_token[:, c].rearrange("t (x a) -> t x a", a=CHUNKS),
-                        in_=banks[0][:, :, 32 * c : 32 * c + 32].rearrange("t a x -> t x a"),
+                        in_=flip_banks[h][:, :, 32 * c : 32 * c + 32].rearrange("t a x -> t x a"),
                     )
                     nc.tensor.transpose(new[c], by_token[:, c], identity[:])
             else:
                 to = by_token[:].rearrange("t c (x a b y) -> t b (c x) a y", a=2, b=2, y=run)
                 for b in range(2):
-                    nc.scalar.copy(out=to[:, b], in_=banks[b][:, 0:2, :].rearrange("t a (x y) -> t x a y", y=run))
+                    nc.scalar.copy(out=to[:, b], in_=flip_banks[b][:, 2 * h : 2 * h + 2, :].rearrange("t a (x y) -> t x a y", y=run))
                 for c in CHUNK_ORDER:
                     nc.tensor.transpose(new[c], by_token[:, c], identity[:])
             streams[h] = new
@@ -492,7 +503,7 @@ def tile_butterflymlp_s_kernel(
         nc.scalar.copy(out=h_grouped[:, 0], in_=hidden[:, 0].rearrange("p k t -> p t k"))
         nc.vector.tensor_copy(out=h_grouped[:, 1], in_=hidden[:, 1].rearrange("p k t -> p t k"))
         half_cols = D_OUT // 2
-        out_ps = [psum.tile([P, half_cols], F32, tag="flip0_%d" % i, name="out_ps%d" % i) for i in range(2)]
+        out_ps = [psum.tile([P, half_cols], F32, tag=("spare", "warm")[i], name="out_ps%d" % i) for i in range(2)]
         out_sb = keep.tile([P, 2, half_cols], F32)
         for g in range(2):
             nc.vector.quantize_mx(

@@ -35,6 +35,10 @@ FLIPS = (
 )
 LOW_RUN = (1, 8, 16)
 WARM = 2
+VECTOR_JOIN = (
+    [(3, r, k) for r in range(2) for k in range(2)],
+    [(c, r, k) for c in (1, 3) for r in range(2) for k in range(2)] + [(2, 1, 0), (2, 1, 1)],
+)
 TURN_ORDER = (0, 2, 3, 1)
 VECTOR_PRODUCTS = ((1, 1), (2, 1), (3, 0), (3, 1))
 
@@ -49,6 +53,9 @@ def tile_butterflymlp_s_kernel(
         data = ctx.enter_context(tc.tile_pool(name="data", bufs=3))
         products = ctx.enter_context(tc.tile_pool(name="products", bufs=24))
         psum = ctx.enter_context(tc.psum_pool(name="psum", bufs=1))
+        banks = [psum.tile([P, CHUNKS, P], F32, tag="bank%d" % i, name="bank%d" % i) for i in range(8)]
+        flip_banks = banks[4:6]
+        warm_bank, spare_bank = banks[6:8]
 
         x_sb = keep.tile([P, D_IN], BF16)
         w_exp_raw = [keep.tile([P, PACK, HIDDEN // 2], BF16, name="w_exp_raw%d" % h) for h in range(STREAMS)]
@@ -57,8 +64,7 @@ def tile_butterflymlp_s_kernel(
         for n in (0, 3):
             unit_w[n] = keep.tile([P, 8, 4], BF16, name="unit_w%d" % n)
             turn_w[n] = keep.tile([P, 8, 4], BF16, name="turn_w%d" % n)
-        up_last_w = keep.tile([P, CHUNKS, 4], BF16)
-        down_last_w = keep.tile([P, CHUNKS, 4], BF16)
+        last_w = {n: keep.tile([P, 2, CHUNKS, 4], BF16, name="last_w%d" % n) for n in (2, 5)}
         b_exp_sb = keep.tile([P, STREAMS, CHUNKS], BF16)
         up_bias_sb = keep.tile([P, STREAMS, CHUNKS], BF16)
         w_con_raw = keep.tile([P, 2, PACK, D_OUT], BF16)
@@ -105,6 +111,12 @@ def tile_butterflymlp_s_kernel(
                         in_=weights_of(n, 2).rearrange("(q y) r c -> q (y r c)", q=8),
                     )
 
+        def load_last(queue, n):
+            view = weights_of(n, 3).rearrange("(v c q) r s -> v q c (r s)", v=2, c=CHUNKS)
+            for partner in range(2):
+                for v in range(2):
+                    queue.dma_start(out=last_w[n][64 * v : 64 * v + 64, partner], in_=view[v ^ partner])
+
         row_tiles = [keep.tile([P, 2 * P], F32, name="rows%d" % i) for i in range(2)]
         for i in range(2):
             nc.vector.memset(row_tiles[i][:], 0.0)
@@ -121,9 +133,7 @@ def tile_butterflymlp_s_kernel(
         nc.sync.dma_start(out=b_exp_sb[:], in_=b_exp.rearrange("(h p c) -> p h c", h=2, c=CHUNKS))
         load_rows(nc.sync, 1)
         load_rows(nc.sync, 2)
-        nc.sync.dma_start(
-            out=up_last_w[:].rearrange("p c e -> p (c e)"), in_=up_weights[9].rearrange("(p c) r s -> p (c r s)", c=CHUNKS)
-        )
+        load_last(nc.sync, 2)
         nc.sync.dma_start(out=up_bias_sb[:], in_=up_bias.rearrange("(h p c) -> p h c", h=2, c=CHUNKS))
         load_low(nc.sync, 3)
         nc.sync.dma_start(
@@ -132,9 +142,7 @@ def tile_butterflymlp_s_kernel(
         )
         load_rows(nc.sync, 4)
         load_rows(nc.sync, 5)
-        nc.sync.dma_start(
-            out=down_last_w[:].rearrange("p c e -> p (c e)"), in_=down_weights[9].rearrange("(p c) r s -> p (c r s)", c=4)
-        )
+        load_last(nc.sync, 5)
         nc.sync.dma_start(out=b_con_rows[:], in_=b_con.partition_broadcast(P))
         nc.sync.dma_start(out=down_bias_rows[:], in_=down_bias.partition_broadcast(P))
 
@@ -167,7 +175,6 @@ def tile_butterflymlp_s_kernel(
         make_flips()
 
         out_bias = keep.tile([P, D_OUT], F32)
-        nc.gpsimd.tensor_tensor(out=out_bias[:], in0=b_con_rows[:], in1=down_bias_rows[:], op=ALU.add)
 
         def multiply_add(out, in0, scalar, in1):
             nc.vector.scalar_tensor_tensor(out=out, in0=in0, scalar=scalar, in1=in1, op0=ALU.mult, op1=ALU.add)
@@ -175,26 +182,41 @@ def tile_butterflymlp_s_kernel(
         steps = []
 
         def run_steps(count):
-            for step in steps[:count]:
-                step()
-                steps.remove(step)
+            while count > 0 and steps:
+                done = 0
+                for on_vector, step in list(steps):
+                    if on_vector and done:
+                        break
+                    step()
+                    steps.remove((on_vector, step))
+                    done += on_vector
+                count -= 1
+
+        def add_step(step, on_vector=True):
+            steps.append((on_vector, step))
+
+        def combine(out, in0, in1, op=ALU.mult):
+            engine = nc.gpsimd if aside[0] else nc.vector
+            add_step(lambda: engine.tensor_tensor(out=out, in0=in0, in1=in1, op=op), not aside[0])
 
         def multiply(out, in0, in1):
-            steps.append(lambda: nc.vector.tensor_tensor(out=out, in0=in0, in1=in1, op=ALU.mult))
+            combine(out, in0, in1)
+
+        aside = [False]
 
         def divide_out(w, name):
             groups = w.shape[1]
             rec = keep.tile([P, groups, 2], F32, name="rec" + name)
             factor = keep.tile([P, groups, 2], F32, name="factor" + name)
             div = keep.tile([P, groups, 2], F32, name="div" + name)
-            steps.append(lambda: nc.vector.reciprocal(out=rec[:], in_=w[:, :, 0:4:3]))
-            steps.append(
+            add_step(lambda: nc.vector.reciprocal(out=rec[:], in_=w[:, :, 0:4:3]))
+            add_step(
                 lambda: nc.vector.tensor_scalar(
                     out=rec[:], in0=rec[:], scalar1=MAX_RECIPROCAL, scalar2=-MAX_RECIPROCAL, op0=ALU.min, op1=ALU.max
                 )
             )
             multiply(factor[:], w[:, :, 1:3], rec[:])
-            steps.append(lambda: nc.vector.reciprocal(out=div[:], in_=rec[:]))
+            add_step(lambda: nc.vector.reciprocal(out=div[:], in_=rec[:]))
             return rec, factor, div
 
         factors = {}
@@ -204,6 +226,28 @@ def tile_butterflymlp_s_kernel(
             name = "%d" % layouts[0]
             size = len(layouts)
             half = 4 * size
+            turn = keep.tile([P, 2 * half, 2], F32, name="turn" + name)
+            pieces = [(i, n % 3, slice(8 * i, 8 * i + 8)) for i, n in enumerate(layouts)]
+
+            other = keep.tile([P, 2 * half, 2], F32, name="other" + name)
+
+            def select(k, cols):
+                for r, (dst, src) in enumerate(((turn, w_turn[:, cols, 0:4:2]), (other, w_turn[:, cols, 3:0:-2]))):
+                    add_step(
+                        lambda dst=dst, src=src, r=r: nc.gpsimd.tensor_scalar(
+                            out=dst[:, cols], in0=src, scalar1=bit_is[:, k, r : r + 1], scalar2=None, op0=ALU.mult
+                        ),
+                        False,
+                    )
+                add_step(
+                    lambda: nc.gpsimd.tensor_tensor(
+                        out=turn[:, cols], in0=turn[:, cols], in1=other[:, cols], op=ALU.add
+                    ),
+                    False,
+                )
+
+            for i, k, cols in pieces:
+                select(k, cols)
             rec, factor, div = divide_out(w_unit, name)
             div0 = div[:, 0:half].rearrange("p (h x) z -> p h x z", x=2)
             rec0 = rec[:, 0:half].rearrange("p (h x) z -> p h x z", x=2)
@@ -217,46 +261,45 @@ def tile_butterflymlp_s_kernel(
             )
             multiply(factor[:, half:], factor[:, half:], correction[:])
             multiply(carried[:].rearrange("p (h x z) -> p h x z", x=2, z=2), div1, div0)
-            turn = keep.tile([P, 2 * half, 2], F32, name="turn" + name)
-            pieces = [(i, n % 3, slice(8 * i, 8 * i + 8)) for i, n in enumerate(layouts)]
-
-            def select(k, cols):
-                steps.append(
-                    lambda: nc.vector.tensor_scalar(
-                        out=turn[:, cols], in0=w_turn[:, cols, 0:4:2], scalar1=bit_is[:, k, 0:1], scalar2=None, op0=ALU.mult
-                    )
-                )
-                steps.append(
-                    lambda: multiply_add(turn[:, cols], w_turn[:, cols, 3:0:-2], bit_is[:, k, 1:2], turn[:, cols])
-                )
-
-            for i, k, cols in pieces:
-                select(k, cols)
             multiply(turn[:], turn[:], carried[:].unsqueeze(2).to_broadcast([P, 2 * half, 2]))
             for i, n in enumerate(layouts):
                 factors[n] = [factor[:, half * j + 4 * i : half * j + 4 * i + 4] for j in range(2)]
                 turn_factors[n] = turn[:, 8 * i : 8 * i + 8]
 
+        join_factors = {}
+
+        def queue_join_factors(n):
+            joined = keep.tile([P, STREAMS, CHUNKS, 2, STREAMS], F32, name="joined%d" % n)
+            for s in range(STREAMS):
+                for k in range(2):
+                    multiply(
+                        joined[:, s, :, k, :],
+                        last_w[n][:, k, :, s:4:2],
+                        turn_factors[n][:, 4 * s : 4 * s + 4, k : k + 1].to_broadcast([P, CHUNKS, STREAMS]),
+                    )
+            join_factors[n] = joined
+
         def turn_rows(n):
             words = row_tiles[n // 3]
-            turned = psum.tile([P, 2, P], F32, tag="spare", name="turned%d" % n)
+            turned = spare_bank[:, 0:2, :]
             for w in range(2):
                 nc.tensor.transpose(turned[:, w, :], words[:, w : 2 * P : 2], identity[:])
             landed = keep.tile([P, 32, 2], F32, name="landed%d" % n)
-            steps.append(
+            add_step(
                 lambda: nc.vector.tensor_copy(out=landed[:], in_=turned[:, :, 0:32].rearrange("p w r -> p r w"))
             )
             pairs = landed[:].rearrange("p r w -> p (r w)").bitcast(BF16).rearrange("p (r e) -> p r e", e=4)
             queue_scalars((n, n + 1), pairs[:, 0:16], pairs[:, 16:32])
 
         queue_scalars((0,), unit_w[0][:], turn_w[0][:])
+        aside = [False]
 
         x_words = x_sb[:].bitcast(F32)
-        x_t = psum.tile([P, 2, TOKENS], F32, tag="spare", name="x_t")
+        x_t = spare_bank[:, 0:2, :]
         for u in range(2):
             nc.tensor.transpose(x_t[:, u, :], x_words[:, u : 2 * P : 2], identity[:])
         x_grouped = keep.tile([P, TOKENS, 2], F32, align_bytes=64)
-        nc.vector.tensor_copy(out=x_grouped[:], in_=x_t[:].rearrange("p u t -> p t u"))
+        nc.vector.tensor_copy(out=x_grouped[:], in_=x_t.rearrange("p u t -> p t u"))
         x_codes = keep.tile([P, TOKENS], U32, align_bytes=64)
         x_scales = keep.tile([P, TOKENS], U8, align_bytes=64)
 
@@ -277,15 +320,11 @@ def tile_butterflymlp_s_kernel(
                 in_=w_exp_grouped[:, h].rearrange("p c m t -> p (c m t)"),
             )
 
-        def new_psum_chunks(h):
-            banks = [
-                psum.tile([P, CHUNKS, TOKENS], F32, tag="stream%d_bank%d" % (h, i), name="stream%d_bank%d" % (h, i))
-                for i in range(2)
-            ]
-            return [banks[c & 1][:, c >> 1, :] for c in range(CHUNKS)]
+        def psum_chunks(h):
+            return [banks[2 * h + (c & 1)][:, c >> 1, :] for c in range(CHUNKS)]
 
         def first_product(h):
-            chunk = new_psum_chunks(h)
+            chunk = psum_chunks(h)
             for c in CHUNK_ORDER:
                 nc.tensor.matmul_mx(
                     out=chunk[c],
@@ -319,20 +358,24 @@ def tile_butterflymlp_s_kernel(
         w_con_codes = keep.tile([P, 2, D_OUT], U32, align_bytes=64)
         w_con_scales = keep.tile([P, 2, D_OUT], U8, align_bytes=64)
 
-        def regroup_w_con(quarter):
-            g, half = divmod(quarter, 2)
-            cols = slice(256 * half, 256 * half + 256)
-            nc.vector.tensor_copy(
-                out=w_con_grouped[:, g, cols, :].rearrange("p (c i) t -> p c t i", i=4),
-                in_=w_con_raw[:, g, :, cols].rearrange("p t (c i) -> p c t i", i=4),
-            )
+        def regroup_w_con(copy, eighths):
+            for eighth in eighths:
+                g, part = divmod(eighth, 4)
+                cols = slice(128 * part, 128 * part + 128)
+                copy(
+                    out=w_con_grouped[:, g, cols, :].rearrange("p (c i) t -> p c t i", i=4),
+                    in_=w_con_raw[:, g, :, cols].rearrange("p t (c i) -> p c t i", i=4),
+                )
 
-        def quantise_w_con(g):
-            nc.vector.quantize_mx(
-                out=w_con_codes[:, g].bitcast(FP8X4),
-                scales=w_con_scales[:, g],
-                in_=w_con_grouped[:, g].rearrange("p c t -> p (c t)"),
-            )
+        def quantise_w_con(halves):
+            for half in halves:
+                g, part = divmod(half, 2)
+                cols = slice(256 * part, 256 * part + 256)
+                nc.vector.quantize_mx(
+                    out=w_con_codes[:, g, cols].bitcast(FP8X4),
+                    scales=w_con_scales[:, g, cols],
+                    in_=w_con_grouped[:, g, cols].rearrange("p c t -> p (c t)"),
+                )
 
         def work_tile(name):
             return products.tile([P, TOKENS], F32, tag="work", name=name)
@@ -368,13 +411,10 @@ def tile_butterflymlp_s_kernel(
                 streams[h] = [new[:, c, :] for c in range(CHUNKS)]
 
         flipped = {}
-        flip_banks = [psum.tile([P, CHUNKS, P], F32, tag="flip%d" % i, name="flip%d" % i) for i in range(2)]
-        warm_bank = psum.tile([P, 4 * P], F32, tag="warm")
-
         def keep_warm(count):
             for i in range(count):
                 nc.tensor.matmul_mx(
-                    out=warm_bank[:],
+                    out=warm_bank[:].rearrange("p c t -> p (c t)"),
                     lhsT=x_codes[:].bitcast(FP8X4),
                     lhsT_scale=x_scales[:],
                     rhs=w_exp_codes[:, 0].rearrange("p c m -> p (c m)").bitcast(FP8X4),
@@ -383,7 +423,7 @@ def tile_butterflymlp_s_kernel(
                     stop=True,
                 )
 
-        def turn_stage(h, n):
+        def turn_stage(h, n, step_count=0, warm=WARM):
             if LOW_RUN[n % 3] == 1:
                 flipped[h] = [flip_banks[h][:, c, :] for c in range(CHUNKS)]
             else:
@@ -396,6 +436,8 @@ def tile_butterflymlp_s_kernel(
                         nc.vector.tensor_scalar(
                             out=prod[:], in0=streams[h][c], scalar1=scalar, scalar2=None, op0=ALU.mult
                         )
+                        run_steps(min(step_count, 1))
+                        step_count -= min(step_count, 1)
                     else:
                         nc.scalar.activation(out=prod[:], in_=streams[h][c], func=ACT.Copy, scale=scalar)
                     nc.tensor.matmul(
@@ -406,11 +448,11 @@ def tile_butterflymlp_s_kernel(
                         stop=(s == 1),
                         is_transpose=True,
                     )
-            keep_warm(WARM)
+            keep_warm(warm)
 
         def turn_back(h, n):
             by_token = data.tile([P, CHUNKS, P], F32, tag="by_token%d" % h, name="by_token%d" % h)
-            new = new_psum_chunks(h)
+            new = psum_chunks(h)
             run = LOW_RUN[n % 3]
             if run == 1:
                 for c in CHUNK_ORDER:
@@ -427,83 +469,144 @@ def tile_butterflymlp_s_kernel(
                     nc.tensor.transpose(new[c], by_token[:, c], identity[:])
             streams[h] = new
 
-        def layout(n, steps0=0, steps1=0, steps2=0):
+        JOIN_BANKS = {0: (7, 6), 2: (0, 1), 1: (4, 5), 3: (2, 3)}
+
+        def join_products(s, n, chunks):
+            by_scalar, by_vector = [], []
+            for c in chunks:
+                for r in range(STREAMS):
+                    for k in range(2):
+                        prod = work_tile("product")
+                        scalar = join_factors[n][:, s, c, k, r : r + 1]
+                        (by_vector if (c, r, k) in VECTOR_JOIN[s] else by_scalar).append((c, r, k, prod))
+                        if (c, r, k) in VECTOR_JOIN[s]:
+                            nc.vector.tensor_scalar(
+                                out=prod[:], in0=streams[s][c], scalar1=scalar, scalar2=None, op0=ALU.mult
+                            )
+                        else:
+                            nc.scalar.activation(out=prod[:], in_=streams[s][c], func=ACT.Copy, scale=scalar)
+
+            def turn():
+                both = max(len(by_scalar), len(by_vector))
+                turns = [t for i in range(both) for t in by_vector[i : i + 1] + by_scalar[i : i + 1]]
+                for c, r, k, prod in turns:
+                    nc.tensor.matmul(
+                        banks[JOIN_BANKS[c][r]][:, 0, :],
+                        lhsT=prod[:],
+                        rhs=flips[:, n % 3, k, :],
+                        start=(s == 0 and k == 0),
+                        stop=(s == 1 and k == 1),
+                        is_transpose=True,
+                    )
+
+            return turn
+
+        def join_back(n, place):
+            run = LOW_RUN[n % 3]
+            by_token = [
+                data.tile([P, CHUNKS, P], F32, tag="by_token%d" % r, name="by_token%d" % r) for r in range(STREAMS)
+            ]
+            for r in range(STREAMS):
+                to = by_token[r][:].rearrange("t c (x a y) -> t a (c x) y", a=CHUNKS, y=run)
+                copy = (nc.scalar.copy, nc.vector.tensor_copy)[r]
+                for c in TURN_ORDER:
+                    copy(
+                        out=to[:, c], in_=banks[JOIN_BANKS[c][r]][:, 0, :].rearrange("t (x y) -> t x y", y=run)
+                    )
+            for r in range(STREAMS):
+                streams[r] = place(r)
+                for c in CHUNK_ORDER:
+                    nc.tensor.transpose(streams[r][c], by_token[r][:, c], identity[:])
+
+        def joining_layout(n, steps0, steps1, gap, place):
+            units(0, n, steps0)
+            turn_back(1, n - 1)
+            turn = join_products(0, n, (0,))
+            turn()
+            copies(1, n)
+            turn = join_products(0, n, (2, 1))
+            turn()
+            turn = join_products(0, n, (3,))
+            units(1, n, steps1)
+            turn()
+            turn = join_products(1, n, TURN_ORDER)
+            turn()
+            gap()
+            join_back(n, place)
+
+        def layout(n, steps0=0, steps1=0, steps2=0, gap0=None, gap1=None):
             units(0, n, steps0)
             if n not in (0, 3):
                 turn_back(1, n - 1)
             turn_stage(0, n)
             copies(1, n)
+            if gap0:
+                gap0()
             units(1, n, steps1)
             turn_back(0, n)
             turn_stage(1, n)
             run_steps(steps2)
-            if n not in (2, 5):
-                copies(0, n + 1)
+            if gap1:
+                gap1()
+            copies(0, n + 1)
 
+        keep_warm(2)
         copies(0, 0)
-        units(0, 0, 8)
+        units(0, 0, 5)
         run_steps(len(steps))
         copies(1, 0)
-        turn_stage(0, 0)
-        units(1, 0)
+        turn_stage(0, 0, warm=0)
         turn_rows(1)
+        keep_warm(WARM)
+        units(1, 0)
         turn_back(0, 0)
-        turn_stage(1, 0)
+        run_steps(1)
+        turn_stage(1, 0, 3)
         copies(0, 1)
-        run_steps(9)
+        run_steps(4)
+        aside[0] = True
+        queue_join_factors(2)
         queue_scalars((3,), unit_w[3][:], turn_w[3][:])
-        up_last_rec, up_last_factor, up_last_div = divide_out(up_last_w[:], "_last")
-        layout(1, 4, 4, 0)
-        layout(2, 4, 4, len(steps))
-        turn_back(1, 2)
+        def fill(eighths, count):
+            for eighth in eighths:
+                run_steps(count)
+                regroup_w_con(nc.vector.tensor_copy, (eighth,))
 
-        raised = [data.tile([P, CHUNKS, TOKENS], F32, tag="chunks%d" % h, name="raised%d" % h) for h in range(2)]
-        for quarter in range(3):
-            regroup_w_con(quarter)
-        copied = {c: out_of_psum(streams[1][c]) for c in CHUNK_ORDER}
-        for c in CHUNK_ORDER:
-            multiply_add(raised[0][:, c, :], copied[c], up_last_factor[:, c, 0:1], streams[0][c])
-        for c in CHUNK_ORDER:
-            multiply_add(raised[1][:, c, :], streams[0][c], up_last_factor[:, c, 1:2], copied[c])
-        for h in range(2):
+        def prepare_down():
+            turn_rows(4)
+            queue_join_factors(5)
+
+        layout(1, 1, 3, 0, prepare_down, lambda: fill((0,), 0))
+        joining_layout(2, 2, 2, lambda: fill((1,), 0), psum_chunks)
+        keep_warm(4)
+        fill((2, 3), 0)
+        regroup_w_con(nc.scalar.copy, (7,))
+
+        for h in range(STREAMS):
+            raised = data.tile([P, CHUNKS, TOKENS], F32, tag="chunks%d" % h, name="raised%d" % h)
             for c in CHUNK_ORDER:
                 nc.scalar.activation(
-                    out=raised[h][:, c, :],
-                    in_=raised[h][:, c, :],
+                    out=raised[:, c, :],
+                    in_=streams[h][c],
                     func=ACT.Gelu,
-                    scale=up_last_div[:, c, h : h + 1],
                     bias=up_bias_sb[:, h, c : c + 1],
                 )
-            streams[h] = [raised[h][:, c, :] for c in range(CHUNKS)]
+            streams[h] = [raised[:, c, :] for c in range(CHUNKS)]
 
-        down_last_f = keep.tile([P, CHUNKS, 4], F32)
-        turn_rows(4)
-        layout(3, 1, 8, len(steps))
-        layout(4)
-        layout(5)
-        nc.vector.tensor_copy(out=down_last_f[:], in_=down_last_w[:])
-        turn_back(1, 5)
-        regroup_w_con(3)
-        quantise_w_con(0)
-        quantise_w_con(1)
+        layout(3, 0, 0, len(steps), lambda: fill((4,), 0))
+        layout(4, 0, 0, 0, lambda: fill((5,), 0), lambda: fill((6,), 0))
+        joining_layout(5, 0, 0, lambda: quantise_w_con((0, 1)), lambda r: [banks[2 * r][:, c, :] for c in range(CHUNKS)])
+        quantise_w_con((2, 3))
 
-        hidden = keep.tile([P, STREAMS, CHUNKS, TOKENS], F32)
-        for r in range(2):
-            for c in CHUNK_ORDER:
-                prod = work_tile("product")
-                w = down_last_f[:, c]
-                nc.scalar.activation(
-                    out=prod[:], in_=streams[1][c], func=ACT.Copy, scale=w[:, 2 * r + 1 : 2 * r + 2]
-                )
-                multiply_add(hidden[:, r, c, :], streams[0][c], w[:, 2 * r : 2 * r + 1], prod[:])
+        nc.gpsimd.tensor_tensor(out=out_bias[:], in0=b_con_rows[:], in1=down_bias_rows[:], op=ALU.add)
 
         h_grouped = keep.tile([P, 2, TOKENS, PACK], BF16, align_bytes=64)
         h_codes = keep.tile([P, 2, TOKENS], U32, align_bytes=64)
         h_scales = keep.tile([P, 2, TOKENS], U8, align_bytes=64)
-        nc.scalar.copy(out=h_grouped[:, 0], in_=hidden[:, 0].rearrange("p k t -> p t k"))
-        nc.vector.tensor_copy(out=h_grouped[:, 1], in_=hidden[:, 1].rearrange("p k t -> p t k"))
+        nc.scalar.copy(out=h_grouped[:, 0], in_=banks[0][:].rearrange("p k t -> p t k"))
+        nc.vector.tensor_copy(out=h_grouped[:, 1], in_=banks[2][:].rearrange("p k t -> p t k"))
         half_cols = D_OUT // 2
-        out_ps = [psum.tile([P, half_cols], F32, tag=("spare", "warm")[i], name="out_ps%d" % i) for i in range(2)]
+        out_ps = [bank[:, 0:2, :].rearrange("p c t -> p (c t)") for bank in (spare_bank, warm_bank)]
         out_sb = keep.tile([P, 2, half_cols], F32)
         for g in range(2):
             nc.vector.quantize_mx(
@@ -515,7 +618,7 @@ def tile_butterflymlp_s_kernel(
             for i in range(2):
                 cols = slice(half_cols * i, half_cols * (i + 1))
                 nc.tensor.matmul_mx(
-                    out=out_ps[i][:],
+                    out=out_ps[i],
                     lhsT=h_codes[:, g, :].bitcast(FP8X4),
                     lhsT_scale=h_scales[:, g, :],
                     rhs=w_con_codes[:, g, cols].bitcast(FP8X4),
@@ -525,5 +628,5 @@ def tile_butterflymlp_s_kernel(
                 )
         for i in range(2):
             cols = slice(half_cols * i, half_cols * (i + 1))
-            nc.vector.tensor_tensor(out=out_sb[:, i], in0=out_ps[i][:], in1=out_bias[:, cols], op=ALU.add)
+            nc.vector.tensor_tensor(out=out_sb[:, i], in0=out_ps[i], in1=out_bias[:, cols], op=ALU.add)
             nc.sync.dma_start(out=out.flatten_outer_dims()[:, cols], in_=out_sb[:, i])

@@ -34,7 +34,7 @@ FLIPS = (
     (dict(a=2, b=16, d=4), "a b d", "d a b", "a", 64),
 )
 LOW_RUN = (1, 8, 16)
-WARM = 2
+WARM = 3
 VECTOR_JOIN = (
     [(3, r, k) for r in range(2) for k in range(2)],
     [(c, r, k) for c in (1, 3) for r in range(2) for k in range(2)] + [(2, 1, 0), (2, 1, 1)],
@@ -307,17 +307,19 @@ def tile_butterflymlp_s_kernel(
         w_exp_codes = keep.tile([P, STREAMS, CHUNKS, P], U32, align_bytes=64)
         w_exp_scales = keep.tile([P, STREAMS, CHUNKS, P], U8, align_bytes=64)
 
-        def regroup_w_exp(copy, h, half):
-            m = slice(P // 2 * half, P // 2 * (half + 1))
+        def regroup_w_exp(h):
             src = w_exp_raw[h][:].rearrange("p t (m c) -> p m t c", c=CHUNKS)
             dst = w_exp_grouped[:, h].rearrange("p c m t -> p m t c")
-            copy(out=dst[:, m], in_=src[:, m])
+            cut = 5 * P // 8
+            nc.vector.tensor_copy(out=dst[:, :cut], in_=src[:, :cut])
+            nc.scalar.copy(out=dst[:, cut:], in_=src[:, cut:])
 
-        def quantise_w_exp(h):
+        def quantise_w_exp(h, half):
+            chunks = slice(2 * half, 2 * half + 2)
             nc.vector.quantize_mx(
-                out=w_exp_codes[:, h].rearrange("p c m -> p (c m)").bitcast(FP8X4),
-                scales=w_exp_scales[:, h].rearrange("p c m -> p (c m)"),
-                in_=w_exp_grouped[:, h].rearrange("p c m t -> p (c m t)"),
+                out=w_exp_codes[:, h, chunks].rearrange("p c m -> p (c m)").bitcast(FP8X4),
+                scales=w_exp_scales[:, h, chunks].rearrange("p c m -> p (c m)"),
+                in_=w_exp_grouped[:, h, chunks].rearrange("p c m t -> p (c m t)"),
             )
 
         def psum_chunks(h):
@@ -337,22 +339,25 @@ def tile_butterflymlp_s_kernel(
                 )
             return chunk
 
-        regroup_w_exp(nc.vector.tensor_copy, 0, 0)
+        regroup_w_exp(0)
         run_steps(1)
-        regroup_w_exp(nc.scalar.copy, 0, 1)
         nc.vector.quantize_mx(
             out=x_codes[:].bitcast(FP8X4),
             scales=x_scales[:],
             in_=x_grouped[:].rearrange("p t u -> p (t u)").bitcast(BF16),
         )
+        quantise_w_exp(0, 0)
         run_steps(1)
-        quantise_w_exp(0)
+        quantise_w_exp(0, 1)
         run_steps(1)
-        regroup_w_exp(nc.scalar.copy, 1, 1)
-        regroup_w_exp(nc.vector.tensor_copy, 1, 0)
+        regroup_w_exp(1)
         run_steps(1)
-        quantise_w_exp(1)
-        streams = [first_product(0), first_product(1)]
+        streams = [first_product(0), None]
+
+        def start_stream_1():
+            for half in range(2):
+                quantise_w_exp(1, half)
+            streams[1] = first_product(1)
 
         w_con_grouped = keep.tile([P, 2, D_OUT, PACK], BF16, align_bytes=64)
         w_con_codes = keep.tile([P, 2, D_OUT], U32, align_bytes=64)
@@ -396,7 +401,7 @@ def tile_butterflymlp_s_kernel(
                 for c in (1, 3):
                     streams[h][c] = out_of_psum(streams[h][c])
 
-        def units(h, n, step_count=0):
+        def units(h, n, step_count=0, between=None):
             left = step_count
             for j in range(2):
                 new = data.tile([P, CHUNKS, TOKENS], F32, tag="chunks%d" % h, name="chunks%d" % h)
@@ -409,12 +414,14 @@ def tile_butterflymlp_s_kernel(
                     run_steps(min(left - 1, 1) if left else 0)
                     left = max(left - 2, 0)
                 streams[h] = [new[:, c, :] for c in range(CHUNKS)]
+                if j == 0 and between:
+                    between()
 
         flipped = {}
-        def keep_warm(count):
+        def keep_warm(count, bank=warm_bank):
             for i in range(count):
                 nc.tensor.matmul_mx(
-                    out=warm_bank[:].rearrange("p c t -> p (c t)"),
+                    out=bank[:].rearrange("p c t -> p (c t)"),
                     lhsT=x_codes[:].bitcast(FP8X4),
                     lhsT_scale=x_scales[:],
                     rhs=w_exp_codes[:, 0].rearrange("p c m -> p (c m)").bitcast(FP8X4),
@@ -523,11 +530,13 @@ def tile_butterflymlp_s_kernel(
             turn_back(1, n - 1)
             turn = join_products(0, n, (0,))
             turn()
+            keep_warm(2, banks[4])
             copies(1, n)
             turn = join_products(0, n, (2, 1))
             turn()
             turn = join_products(0, n, (3,))
             units(1, n, steps1)
+            keep_warm(0, banks[2])
             turn()
             turn = join_products(1, n, TURN_ORDER)
             turn()
@@ -550,8 +559,9 @@ def tile_butterflymlp_s_kernel(
                 gap1()
             copies(0, n + 1)
 
-        keep_warm(2)
         copies(0, 0)
+        start_stream_1()
+        keep_warm(2)
         units(0, 0, 5)
         run_steps(len(steps))
         copies(1, 0)
@@ -567,6 +577,7 @@ def tile_butterflymlp_s_kernel(
         aside[0] = True
         queue_join_factors(2)
         queue_scalars((3,), unit_w[3][:], turn_w[3][:])
+
         def fill(eighths, count):
             for eighth in eighths:
                 run_steps(count)
@@ -596,6 +607,7 @@ def tile_butterflymlp_s_kernel(
         layout(3, 0, 0, len(steps), lambda: fill((4,), 0))
         layout(4, 0, 0, 0, lambda: fill((5,), 0), lambda: fill((6,), 0))
         joining_layout(5, 0, 0, lambda: quantise_w_con((0, 1)), lambda r: [banks[2 * r][:, c, :] for c in range(CHUNKS)])
+        keep_warm(2)
         quantise_w_con((2, 3))
 
         nc.gpsimd.tensor_tensor(out=out_bias[:], in0=b_con_rows[:], in1=down_bias_rows[:], op=ALU.add)

@@ -39,7 +39,8 @@ VECTOR_JOIN = (
     [(3, r, k) for r in range(2) for k in range(2)],
     [(c, r, k) for c in (1, 3) for r in range(2) for k in range(2)] + [(2, 1, 0), (2, 1, 1)],
 )
-TURN_ORDER = (0, 2, 3, 1)
+TURN_ORDER = (0, 2, 1, 3)
+UNIT_ORDER = ((0, 0), (0, 2), (0, 1), (1, 0), (0, 3), (1, 2), (1, 1), (1, 3))
 VECTOR_PRODUCTS = ((1, 1), (2, 1), (3, 0), (3, 1))
 
 
@@ -125,12 +126,11 @@ def tile_butterflymlp_s_kernel(
         nc.vector.memset(zero_column[:], 0.0)
 
         nc.sync.dma_start(out=x_sb[:], in_=x.flatten_outer_dims())
+        load_low(nc.scalar, 0)
+        nc.scalar.dma_start(out=b_exp_sb[:], in_=b_exp.rearrange("(h p c) -> p h c", h=2, c=CHUNKS))
         for h in range(STREAMS):
             cols = slice(HIDDEN // 2 * h, HIDDEN // 2 * (h + 1))
             nc.sync.dma_start(out=w_exp_raw[h][:], in_=W_exp[:, cols].rearrange("(p t) c -> p t c", t=PACK))
-            if h == 0:
-                load_low(nc.sync, 0)
-        nc.sync.dma_start(out=b_exp_sb[:], in_=b_exp.rearrange("(h p c) -> p h c", h=2, c=CHUNKS))
         load_rows(nc.sync, 1)
         load_rows(nc.sync, 2)
         load_last(nc.sync, 2)
@@ -401,21 +401,27 @@ def tile_butterflymlp_s_kernel(
                 for c in (1, 3):
                     streams[h][c] = out_of_psum(streams[h][c])
 
-        def units(h, n, step_count=0, between=None):
-            left = step_count
-            for j in range(2):
-                new = data.tile([P, CHUNKS, TOKENS], F32, tag="chunks%d" % h, name="chunks%d" % h)
-                chunk = streams[h]
-                for i, (a, b) in enumerate(PAIRS[j]):
-                    factor = factors[n][j][:, 2 * h + i]
-                    multiply_add(new[:, a, :], chunk[b], factor[:, 0:1], chunk[a])
-                    run_steps(min(left, 1))
-                    multiply_add(new[:, b, :], chunk[a], factor[:, 1:2], chunk[b])
-                    run_steps(min(left - 1, 1) if left else 0)
-                    left = max(left - 2, 0)
-                streams[h] = [new[:, c, :] for c in range(CHUNKS)]
-                if j == 0 and between:
-                    between()
+        def units(h, n, step_count=0):
+            old = streams[h]
+            first, second = [
+                data.tile([P, CHUNKS, TOKENS], F32, tag="chunks%d_%d" % (h, j), name="chunks%d_%d" % (h, j))
+                for j in range(2)
+            ]
+            middle, last = [first[:, c, :] for c in range(CHUNKS)], [second[:, c, :] for c in range(CHUNKS)]
+
+            def one(j, c):
+                source, target = ((old, middle), (middle, last))[j]
+                partner = c ^ (1 << j)
+                group = (c >> 1, c & 1)[j]
+                r = (c >> j) & 1
+                multiply_add(target[c], source[partner], factors[n][j][:, 2 * h + group, r : r + 1], source[c])
+
+            for j, c in UNIT_ORDER:
+                one(j, c)
+                if step_count > 0:
+                    run_steps(1)
+                    step_count -= 1
+            streams[h] = last
 
         flipped = {}
         def keep_warm(count, bank=warm_bank):
@@ -594,7 +600,7 @@ def tile_butterflymlp_s_kernel(
         regroup_w_con(nc.scalar.copy, (7,))
 
         for h in range(STREAMS):
-            raised = data.tile([P, CHUNKS, TOKENS], F32, tag="chunks%d" % h, name="raised%d" % h)
+            raised = data.tile([P, CHUNKS, TOKENS], F32, tag="chunks%d_0" % h, name="raised%d" % h)
             for c in CHUNK_ORDER:
                 nc.scalar.activation(
                     out=raised[:, c, :],

@@ -40,6 +40,7 @@ VECTOR_JOIN = (
     [(c, r, k) for c in (1, 3) for r in range(2) for k in range(2)] + [(2, 1, 0), (2, 1, 1)],
 )
 TURN_ORDER = (0, 2, 1, 3)
+UNIT_ORDER_AFTER_GELU = ((0, 0), (0, 1), (0, 2), (0, 3), (1, 0), (1, 2), (1, 1), (1, 3))
 UNIT_ORDER = ((0, 0), (0, 2), (0, 1), (1, 0), (0, 3), (1, 2), (1, 1), (1, 3))
 VECTOR_PRODUCTS = ((1, 1), (2, 1), (3, 0), (3, 1))
 
@@ -127,22 +128,24 @@ def tile_butterflymlp_s_kernel(
 
         nc.sync.dma_start(out=x_sb[:], in_=x.flatten_outer_dims())
         load_low(nc.scalar, 0)
-        nc.scalar.dma_start(out=b_exp_sb[:], in_=b_exp.rearrange("(h p c) -> p h c", h=2, c=CHUNKS))
         for h in range(STREAMS):
             cols = slice(HIDDEN // 2 * h, HIDDEN // 2 * (h + 1))
-            nc.sync.dma_start(out=w_exp_raw[h][:], in_=W_exp[:, cols].rearrange("(p t) c -> p t c", t=PACK))
+            view = W_exp[:, cols].rearrange("(p t) c -> p t c", t=PACK)
+            for t in (slice(0, 2), slice(2, 4)) if h == 0 else (slice(0, 4),):
+                nc.sync.dma_start(out=w_exp_raw[h][:, t], in_=view[:, t])
+        nc.sync.dma_start(out=b_exp_sb[:], in_=b_exp.rearrange("(h p c) -> p h c", h=2, c=CHUNKS))
         load_rows(nc.sync, 1)
         load_rows(nc.sync, 2)
         load_last(nc.sync, 2)
         nc.sync.dma_start(out=up_bias_sb[:], in_=up_bias.rearrange("(h p c) -> p h c", h=2, c=CHUNKS))
         load_low(nc.sync, 3)
+        load_rows(nc.sync, 4)
+        load_rows(nc.sync, 5)
+        load_last(nc.sync, 5)
         nc.sync.dma_start(
             out=w_con_raw[:].rearrange("p g t c -> p g (t c)"),
             in_=W_con.rearrange("(g p t) c -> p g (t c)", g=2, t=PACK),
         )
-        load_rows(nc.sync, 4)
-        load_rows(nc.sync, 5)
-        load_last(nc.sync, 5)
         nc.sync.dma_start(out=b_con_rows[:], in_=b_con.partition_broadcast(P))
         nc.sync.dma_start(out=down_bias_rows[:], in_=down_bias.partition_broadcast(P))
 
@@ -261,7 +264,12 @@ def tile_butterflymlp_s_kernel(
             )
             multiply(factor[:, half:], factor[:, half:], correction[:])
             multiply(carried[:].rearrange("p (h x z) -> p h x z", x=2, z=2), div1, div0)
-            multiply(turn[:], turn[:], carried[:].unsqueeze(2).to_broadcast([P, 2 * half, 2]))
+            add_step(
+                lambda: nc.gpsimd.tensor_tensor(
+                    out=turn[:], in0=turn[:], in1=carried[:].unsqueeze(2).to_broadcast([P, 2 * half, 2]), op=ALU.mult
+                ),
+                False,
+            )
             for i, n in enumerate(layouts):
                 factors[n] = [factor[:, half * j + 4 * i : half * j + 4 * i + 4] for j in range(2)]
                 turn_factors[n] = turn[:, 8 * i : 8 * i + 8]
@@ -416,9 +424,10 @@ def tile_butterflymlp_s_kernel(
                 r = (c >> j) & 1
                 multiply_add(target[c], source[partner], factors[n][j][:, 2 * h + group, r : r + 1], source[c])
 
-            for j, c in UNIT_ORDER:
+            every = 1 if step_count > 4 else 2
+            for i, (j, c) in enumerate(UNIT_ORDER_AFTER_GELU if n == 3 else UNIT_ORDER):
                 one(j, c)
-                if step_count > 0:
+                if i % every == 0 and step_count > 0:
                     run_steps(1)
                     step_count -= 1
             streams[h] = last
@@ -521,8 +530,8 @@ def tile_butterflymlp_s_kernel(
             ]
             for r in range(STREAMS):
                 to = by_token[r][:].rearrange("t c (x a y) -> t a (c x) y", a=CHUNKS, y=run)
-                copy = (nc.scalar.copy, nc.vector.tensor_copy)[r]
                 for c in TURN_ORDER:
+                    copy = (nc.scalar.copy, nc.vector.tensor_copy)[c & 1]
                     copy(
                         out=to[:, c], in_=banks[JOIN_BANKS[c][r]][:, 0, :].rearrange("t (x y) -> t x y", y=run)
                     )
@@ -549,11 +558,11 @@ def tile_butterflymlp_s_kernel(
             gap()
             join_back(n, place)
 
-        def layout(n, steps0=0, steps1=0, steps2=0, gap0=None, gap1=None):
+        def layout(n, steps0=0, steps1=0, steps2=0, gap0=None, gap1=None, warm=WARM):
             units(0, n, steps0)
             if n not in (0, 3):
                 turn_back(1, n - 1)
-            turn_stage(0, n)
+            turn_stage(0, n, warm=warm)
             copies(1, n)
             if gap0:
                 gap0()
@@ -566,8 +575,9 @@ def tile_butterflymlp_s_kernel(
             copies(0, n + 1)
 
         copies(0, 0)
-        start_stream_1()
         keep_warm(2)
+        start_stream_1()
+        keep_warm(1)
         units(0, 0, 5)
         run_steps(len(steps))
         copies(1, 0)
@@ -593,10 +603,10 @@ def tile_butterflymlp_s_kernel(
             turn_rows(4)
             queue_join_factors(5)
 
-        layout(1, 1, 3, 0, prepare_down, lambda: fill((0,), 0))
-        joining_layout(2, 2, 2, lambda: fill((1,), 0), psum_chunks)
+        layout(1, 0, 3, 0, prepare_down, None, 2)
+        joining_layout(2, 2, 2, lambda: fill((0,), 0), psum_chunks)
         keep_warm(4)
-        fill((2, 3), 0)
+        fill((1, 2), 0)
         regroup_w_con(nc.scalar.copy, (7,))
 
         for h in range(STREAMS):
@@ -610,7 +620,7 @@ def tile_butterflymlp_s_kernel(
                 )
             streams[h] = [raised[:, c, :] for c in range(CHUNKS)]
 
-        layout(3, 0, 0, len(steps), lambda: fill((4,), 0))
+        layout(3, 0, 0, len(steps), lambda: fill((3,), 0), lambda: fill((4,), 0))
         layout(4, 0, 0, 0, lambda: fill((5,), 0), lambda: fill((6,), 0))
         joining_layout(5, 0, 0, lambda: quantise_w_con((0, 1)), lambda r: [banks[2 * r][:, c, :] for c in range(CHUNKS)])
         keep_warm(2)

@@ -32,9 +32,15 @@ FLIPS = (
     (dict(a=16, b=4, c=2), "a b c", "b a c", "c", 1),
     (dict(a=2, b=4, c=2, d=8), "a b c d", "b a c d", "c", 8),
     (dict(a=2, b=16, d=4), "a b d", "d a b", "a", 64),
+    (dict(a=2, b=16, d=2, e=2), "a b d e", "d a b e", "a", 64),
 )
-LOW_RUN = (1, 8, 16)
-WARM = 3
+LOW_RUN = (1, 8, 16, 32)
+
+
+def flip_of(n):
+    return 3 if n == LAYOUTS - 1 else n % 3
+
+WARM = 2
 VECTOR_JOIN = (
     [(3, r, k) for r in range(2) for k in range(2)],
     [(c, r, k) for c in (1, 3) for r in range(2) for k in range(2)] + [(2, 1, 0), (2, 1, 1)],
@@ -157,17 +163,12 @@ def tile_butterflymlp_s_kernel(
 
         def make_flips():
             for k, (sizes, old, new, turned, weight) in enumerate(FLIPS):
-                src = identity[:].rearrange("p (%s) -> p %s" % (old, new), **sizes)
-                dst = flips[:, k, 0].rearrange("p (%s) -> p %s" % (new, new), **sizes)
-                if k == 1:
-                    src = src.rearrange("p b a c d -> p b a (c d)")
-                    dst = dst.rearrange("p b a c d -> p b a (c d)")
-                nc.vector.tensor_copy(out=dst, in_=src)
-                rest = [g for g in new.split(" ") if g != turned]
-                src = identity[:].rearrange("p (%s) -> p %s %s" % (old, turned, " ".join(rest)), **sizes)
-                dst = flips[:, k, 1].rearrange("p (%s) -> p %s %s" % (new, turned, " ".join(rest)), **sizes)
-                for r in range(2):
-                    nc.vector.tensor_copy(out=dst[:, r], in_=src[:, 1 - r])
+                rest = " ".join(g for g in new.split(" ") if g != turned)
+                src = identity[:].rearrange("p (%s) -> p %s %s" % (old, turned, rest), **sizes)
+                for inverted in range(2):
+                    dst = flips[:, k, inverted].rearrange("p (%s) -> p %s %s" % (new, turned, rest), **sizes)
+                    for r in range(2):
+                        nc.vector.tensor_copy(out=dst[:, r], in_=src[:, r ^ inverted])
             for k, (sizes, old, new, turned, weight) in enumerate(FLIPS):
                 by_bit = identity[:].rearrange("p (x r y) -> p r x y", r=2, y=weight)
                 for r in range(2):
@@ -515,7 +516,7 @@ def tile_butterflymlp_s_kernel(
                     nc.tensor.matmul(
                         banks[JOIN_BANKS[c][r]][:, 0, :],
                         lhsT=prod[:],
-                        rhs=flips[:, n % 3, k, :],
+                        rhs=flips[:, flip_of(n), k, :],
                         start=(s == 0 and k == 0),
                         stop=(s == 1 and k == 1),
                         is_transpose=True,
@@ -523,24 +524,25 @@ def tile_butterflymlp_s_kernel(
 
             return turn
 
-        def join_back(n, place):
-            run = LOW_RUN[n % 3]
+        def join_back(n):
+            last = n == LAYOUTS - 1
+            run = LOW_RUN[flip_of(n)]
             by_token = [
-                data.tile([P, CHUNKS, P], F32, tag="by_token%d" % r, name="by_token%d" % r) for r in range(STREAMS)
+                data.tile([P, CHUNKS * P], BF16 if last else F32, tag="joined%d_%d" % (last, r), name="joined%d_%d" % (last, r))
+                for r in range(STREAMS)
             ]
             for r in range(STREAMS):
-                to = by_token[r][:].rearrange("t c (x a y) -> t a (c x) y", a=CHUNKS, y=run)
+                to = by_token[r][:].rearrange("t (x a y) -> t a x y", a=CHUNKS, y=run)
                 for c in TURN_ORDER:
                     copy = (nc.scalar.copy, nc.vector.tensor_copy)[c & 1]
-                    copy(
-                        out=to[:, c], in_=banks[JOIN_BANKS[c][r]][:, 0, :].rearrange("t (x y) -> t x y", y=run)
-                    )
+                    copy(out=to[:, c], in_=banks[JOIN_BANKS[c][r]][:, 0, :].rearrange("t (x y) -> t x y", y=run))
             for r in range(STREAMS):
-                streams[r] = place(r)
-                for c in CHUNK_ORDER:
-                    nc.tensor.transpose(streams[r][c], by_token[r][:, c], identity[:])
+                words = by_token[r][:].bitcast(F32)
+                streams[r] = [banks[2 * r][:, c, :] for c in range(2)] if last else psum_chunks(r)
+                for c in (0, 1) if last else CHUNK_ORDER:
+                    nc.tensor.transpose(streams[r][c], words[:, P * c : P * (c + 1)], identity[:])
 
-        def joining_layout(n, steps0, steps1, gap, place):
+        def joining_layout(n, steps0, steps1, gap):
             units(0, n, steps0)
             turn_back(1, n - 1)
             turn = join_products(0, n, (0,))
@@ -556,7 +558,7 @@ def tile_butterflymlp_s_kernel(
             turn = join_products(1, n, TURN_ORDER)
             turn()
             gap()
-            join_back(n, place)
+            join_back(n)
 
         def layout(n, steps0=0, steps1=0, steps2=0, gap0=None, gap1=None, warm=WARM):
             units(0, n, steps0)
@@ -604,8 +606,8 @@ def tile_butterflymlp_s_kernel(
             queue_join_factors(5)
 
         layout(1, 0, 3, 0, prepare_down, None, 2)
-        joining_layout(2, 2, 2, lambda: fill((0,), 0), psum_chunks)
-        keep_warm(4)
+        joining_layout(2, 2, 2, lambda: fill((0,), 0))
+        keep_warm(3)
         fill((1, 2), 0)
         regroup_w_con(nc.scalar.copy, (7,))
 
@@ -622,7 +624,7 @@ def tile_butterflymlp_s_kernel(
 
         layout(3, 0, 0, len(steps), lambda: fill((3,), 0), lambda: fill((4,), 0))
         layout(4, 0, 0, 0, lambda: fill((5,), 0), lambda: fill((6,), 0))
-        joining_layout(5, 0, 0, lambda: quantise_w_con((0, 1)), lambda r: [banks[2 * r][:, c, :] for c in range(CHUNKS)])
+        joining_layout(5, 0, 0, lambda: quantise_w_con((0, 1)))
         keep_warm(2)
         quantise_w_con((2, 3))
 
@@ -631,8 +633,11 @@ def tile_butterflymlp_s_kernel(
         h_grouped = keep.tile([P, 2, TOKENS, PACK], BF16, align_bytes=64)
         h_codes = keep.tile([P, 2, TOKENS], U32, align_bytes=64)
         h_scales = keep.tile([P, 2, TOKENS], U8, align_bytes=64)
-        nc.scalar.copy(out=h_grouped[:, 0], in_=banks[0][:].rearrange("p k t -> p t k"))
-        nc.vector.tensor_copy(out=h_grouped[:, 1], in_=banks[2][:].rearrange("p k t -> p t k"))
+        for copy, r in ((nc.scalar.copy, 0), (nc.vector.tensor_copy, 1)):
+            copy(
+                out=h_grouped[:, r].rearrange("p t k -> p (t k)").bitcast(F32).rearrange("p (t u) -> p t u", u=2),
+                in_=banks[2 * r][:, 0:2, :].rearrange("p u t -> p t u"),
+            )
         half_cols = D_OUT // 2
         out_ps = [bank[:, 0:2, :].rearrange("p c t -> p (c t)") for bank in (spare_bank, warm_bank)]
         out_sb = keep.tile([P, 2, half_cols], F32)

from contextlib import ExitStack

import concourse.mybir as mybir
from concourse.masks import make_identity

F32 = mybir.dt.float32
BF16 = mybir.dt.bfloat16
U32 = mybir.dt.uint32
U8 = mybir.dt.uint8
FP8X4 = mybir.dt.float8_e4m3fn_x4
ACT = mybir.ActivationFunctionType
ALU = mybir.AluOpType

P = 128
TOKENS = 128
D_IN = 512
HIDDEN = 1024
D_OUT = 512
STREAMS = 2
CHUNKS = 4
STAGES = 20
PACK = 4
LAYOUTS = 6
MAX_RECIPROCAL = 2.0**40

FLOPS = 2 * TOKENS * D_IN * HIDDEN + 2 * TOKENS * HIDDEN * D_OUT + STAGES * TOKENS * HIDDEN * 3

CHUNK_ORDER = (1, 0, 3, 2)
PAIRS = (((0, 1), (2, 3)), ((0, 2), (1, 3)))

FLIPS = (
    (dict(a=16, b=4, c=2), "a b c", "b a c", "c", 1),
    (dict(a=2, b=4, c=2, d=8), "a b c d", "b a c d", "c", 8),
    (dict(a=2, b=16, d=4), "a b d", "d a b", "a", 64),
    (dict(a=2, b=16, d=2, e=2), "a b d e", "d a b e", "a", 64),
)
LOW_RUN = (1, 8, 16, 32)


def flip_of(n):
    return 3 if n == LAYOUTS - 1 else n % 3

WARM = 2
VECTOR_JOIN = (
    [(3, r, k) for r in range(2) for k in range(2)],
    [(c, r, k) for c in (1, 3) for r in range(2) for k in range(2)] + [(2, 1, 0), (2, 1, 1)],
)
TURN_ORDER = (0, 2, 1, 3)
UNIT_ORDER_AFTER_GELU = ((0, 0), (0, 1), (0, 2), (0, 3), (1, 0), (1, 2), (1, 1), (1, 3))
UNIT_ORDER = ((0, 0), (0, 2), (0, 1), (1, 0), (0, 3), (1, 2), (1, 1), (1, 3))
VECTOR_PRODUCTS = ((1, 1), (2, 1), (3, 0), (3, 1))


def tile_butterflymlp_s_kernel(
    tc, x, W_exp, b_exp, up_weights, up_bias, down_weights, W_con, b_con, down_bias, out
):
    nc = tc.nc
    with ExitStack() as ctx:
        ctx.enter_context(tc.manual_schedule())
        keep = ctx.enter_context(tc.tile_pool(name="keep", bufs=1))
        data = ctx.enter_context(tc.tile_pool(name="data", bufs=3))
        products = ctx.enter_context(tc.tile_pool(name="products", bufs=24))
        psum = ctx.enter_context(tc.psum_pool(name="psum", bufs=1))
        banks = [psum.tile([P, CHUNKS, P], F32, tag="bank%d" % i, name="bank%d" % i) for i in range(8)]
        flip_banks = banks[4:6]
        warm_bank, spare_bank = banks[6:8]

        x_sb = keep.tile([P, D_IN], BF16)
        w_exp_raw = [keep.tile([P, PACK, HIDDEN // 2], BF16, name="w_exp_raw%d" % h) for h in range(STREAMS)]
        unit_w = {}
        turn_w = {}
        for n in (0, 3):
            unit_w[n] = keep.tile([P, 8, 4], BF16, name="unit_w%d" % n)
            turn_w[n] = keep.tile([P, 8, 4], BF16, name="turn_w%d" % n)
        last_w = {n: keep.tile([P, 2, CHUNKS, 4], BF16, name="last_w%d" % n) for n in (2, 5)}
        b_exp_sb = keep.tile([P, STREAMS, CHUNKS], BF16)
        up_bias_sb = keep.tile([P, STREAMS, CHUNKS], BF16)
        w_con_raw = keep.tile([P, 2, PACK, D_OUT], BF16)
        b_con_rows = keep.tile([P, D_OUT], BF16)
        down_bias_rows = keep.tile([P, D_OUT], BF16)

        def weights_of(n, stage):
            return (up_weights if n < 3 else down_weights)[3 * (n % 3) + stage]

        def load_low(queue, n):
            for s in range(2):
                queue.dma_start(
                    out=unit_w[n][:, 4 * s : 4 * s + 4].rearrange("p (h g) e -> p h (g e)", h=2),
                    in_=weights_of(n, s).rearrange("(h p g) r c -> p h (g r c)", h=2, p=P),
                )
            view = weights_of(n, 2).rearrange("(h q c) r s -> q h (c r s)", h=2, q=64)
            for v in range(2):
                queue.dma_start(out=turn_w[n][v:P:2].rearrange("q (h c) e -> q h (c e)", h=2), in_=view)

        def load_rows(queue, n):
            pairs = row_tiles[n // 3][:].bitcast(BF16)
            layout = n % 3 - 1
            unit_row = [4 * layout, 8 + 4 * layout]
            turn_row = 16 + 8 * layout
            for s in range(2):
                if n % 3 == 1:
                    view = weights_of(n, s).rearrange("(h x g y) r c -> h g x (y r c)", h=2, x=16, g=2)
                else:
                    view = weights_of(n, s).rearrange("(h x g y) r c -> h g x (y r c)", h=2, x=2, g=2)
                for h in range(2):
                    r = unit_row[s] + 2 * h
                    queue.dma_start(out=pairs[r : r + 2].rearrange("g (x e) -> g x e", x=view.shape[2]), in_=view[h])
            for v in range(2):
                if n % 3 == 1:
                    view = weights_of(n, 2).rearrange("(h x c y) r s -> h c x (y r s)", h=2, x=8, c=4)
                    for h in range(2):
                        r = turn_row + 4 * h
                        queue.dma_start(
                            out=pairs[r : r + 4].rearrange("c (x v e) -> c v x e", x=8, v=2)[:, v], in_=view[h]
                        )
                else:
                    queue.dma_start(
                        out=pairs[turn_row : turn_row + 8].rearrange("q (v e) -> q v e", v=2)[:, v],
                        in_=weights_of(n, 2).rearrange("(q y) r c -> q (y r c)", q=8),
                    )

        def load_last(queue, n):
            view = weights_of(n, 3).rearrange("(v c q) r s -> v q c (r s)", v=2, c=CHUNKS)
            for partner in range(2):
                for v in range(2):
                    queue.dma_start(out=last_w[n][64 * v : 64 * v + 64, partner], in_=view[v ^ partner])

        row_tiles = [keep.tile([P, 2 * P], F32, name="rows%d" % i) for i in range(2)]
        for i in range(2):
            nc.vector.memset(row_tiles[i][:], 0.0)
        zero_column = keep.tile([P, 1], F32)
        gelu_of_zero = keep.tile([P, 1], F32)
        nc.vector.memset(zero_column[:], 0.0)

        nc.sync.dma_start(out=x_sb[:], in_=x.flatten_outer_dims())
        load_low(nc.scalar, 0)
        for h in range(STREAMS):
            cols = slice(HIDDEN // 2 * h, HIDDEN // 2 * (h + 1))
            view = W_exp[:, cols].rearrange("(p t) c -> p t c", t=PACK)
            for t in (slice(0, 2), slice(2, 4)) if h == 0 else (slice(0, 4),):
                nc.sync.dma_start(out=w_exp_raw[h][:, t], in_=view[:, t])
        nc.sync.dma_start(out=b_exp_sb[:], in_=b_exp.rearrange("(h p c) -> p h c", h=2, c=CHUNKS))
        load_rows(nc.sync, 1)
        load_rows(nc.sync, 2)
        load_last(nc.sync, 2)
        nc.sync.dma_start(out=up_bias_sb[:], in_=up_bias.rearrange("(h p c) -> p h c", h=2, c=CHUNKS))
        load_low(nc.sync, 3)
        load_rows(nc.sync, 4)
        load_rows(nc.sync, 5)
        load_last(nc.sync, 5)
        nc.sync.dma_start(
            out=w_con_raw[:].rearrange("p g t c -> p g (t c)"),
            in_=W_con.rearrange("(g p t) c -> p g (t c)", g=2, t=PACK),
        )
        nc.sync.dma_start(out=b_con_rows[:], in_=b_con.partition_broadcast(P))
        nc.sync.dma_start(out=down_bias_rows[:], in_=down_bias.partition_broadcast(P))

        identity = keep.tile([P, P], F32)
        make_identity(nc, identity[:])
        nc.scalar.activation(out=gelu_of_zero[:], in_=zero_column[:], func=ACT.Gelu)
        flips = keep.tile([P, len(FLIPS), 2, P], F32)
        bit_is = keep.tile([P, len(FLIPS), 2], F32)

        def make_flips():
            for k, (sizes, old, new, turned, weight) in enumerate(FLIPS):
                rest = " ".join(g for g in new.split(" ") if g != turned)
                src = identity[:].rearrange("p (%s) -> p %s %s" % (old, turned, rest), **sizes)
                for inverted in range(2):
                    dst = flips[:, k, inverted].rearrange("p (%s) -> p %s %s" % (new, turned, rest), **sizes)
                    for r in range(2):
                        nc.vector.tensor_copy(out=dst[:, r], in_=src[:, r ^ inverted])
            for k, (sizes, old, new, turned, weight) in enumerate(FLIPS):
                by_bit = identity[:].rearrange("p (x r y) -> p r x y", r=2, y=weight)
                for r in range(2):
                    nc.vector.tensor_reduce(
                        out=bit_is[:, k, r : r + 1], in_=by_bit[:, r], op=ALU.add, axis=mybir.AxisListType.XY
                    )

        make_flips()

        out_bias = keep.tile([P, D_OUT], F32)

        def multiply_add(out, in0, scalar, in1):
            nc.vector.scalar_tensor_tensor(out=out, in0=in0, scalar=scalar, in1=in1, op0=ALU.mult, op1=ALU.add)

        steps = []

        def run_steps(count):
            while count > 0 and steps:
                done = 0
                for on_vector, step in list(steps):
                    if on_vector and done:
                        break
                    step()
                    steps.remove((on_vector, step))
                    done += on_vector
                count -= 1

        def add_step(step, on_vector=True):
            steps.append((on_vector, step))

        def combine(out, in0, in1, op=ALU.mult):
            engine = nc.gpsimd if aside[0] else nc.vector
            add_step(lambda: engine.tensor_tensor(out=out, in0=in0, in1=in1, op=op), not aside[0])

        def multiply(out, in0, in1):
            combine(out, in0, in1)

        aside = [False]

        def divide_out(w, name):
            groups = w.shape[1]
            rec = keep.tile([P, groups, 2], F32, name="rec" + name)
            factor = keep.tile([P, groups, 2], F32, name="factor" + name)
            div = keep.tile([P, groups, 2], F32, name="div" + name)
            add_step(lambda: nc.vector.reciprocal(out=rec[:], in_=w[:, :, 0:4:3]))
            add_step(
                lambda: nc.vector.tensor_scalar(
                    out=rec[:], in0=rec[:], scalar1=MAX_RECIPROCAL, scalar2=-MAX_RECIPROCAL, op0=ALU.min, op1=ALU.max
                )
            )
            multiply(factor[:], w[:, :, 1:3], rec[:])
            add_step(lambda: nc.vector.reciprocal(out=div[:], in_=rec[:]))
            return rec, factor, div

        factors = {}
        turn_factors = {}

        def queue_scalars(layouts, w_unit, w_turn):
            name = "%d" % layouts[0]
            size = len(layouts)
            half = 4 * size
            turn = keep.tile([P, 2 * half, 2], F32, name="turn" + name)
            pieces = [(i, n % 3, slice(8 * i, 8 * i + 8)) for i, n in enumerate(layouts)]

            other = keep.tile([P, 2 * half, 2], F32, name="other" + name)

            def select(k, cols):
                for r, (dst, src) in enumerate(((turn, w_turn[:, cols, 0:4:2]), (other, w_turn[:, cols, 3:0:-2]))):
                    add_step(
                        lambda dst=dst, src=src, r=r: nc.gpsimd.tensor_scalar(
                            out=dst[:, cols], in0=src, scalar1=bit_is[:, k, r : r + 1], scalar2=None, op0=ALU.mult
                        ),
                        False,
                    )
                add_step(
                    lambda: nc.gpsimd.tensor_tensor(
                        out=turn[:, cols], in0=turn[:, cols], in1=other[:, cols], op=ALU.add
                    ),
                    False,
                )

            for i, k, cols in pieces:
                select(k, cols)
            rec, factor, div = divide_out(w_unit, name)
            div0 = div[:, 0:half].rearrange("p (h x) z -> p h x z", x=2)
            rec0 = rec[:, 0:half].rearrange("p (h x) z -> p h x z", x=2)
            div1 = div[:, half:].rearrange("p (h z) x -> p h x z", z=2)
            correction = keep.tile([P, half, 2], F32, name="correction" + name)
            carried = keep.tile([P, 2 * half], F32, name="carried" + name)
            multiply(
                correction[:].rearrange("p (h z) r -> p h z r", z=2),
                div0.rearrange("p h x z -> p h z x")[:, :, :, ::-1],
                rec0.rearrange("p h x z -> p h z x"),
            )
            multiply(factor[:, half:], factor[:, half:], correction[:])
            multiply(carried[:].rearrange("p (h x z) -> p h x z", x=2, z=2), div1, div0)
            add_step(
                lambda: nc.gpsimd.tensor_tensor(
                    out=turn[:], in0=turn[:], in1=carried[:].unsqueeze(2).to_broadcast([P, 2 * half, 2]), op=ALU.mult
                ),
                False,
            )
            for i, n in enumerate(layouts):
                factors[n] = [factor[:, half * j + 4 * i : half * j + 4 * i + 4] for j in range(2)]
                turn_factors[n] = turn[:, 8 * i : 8 * i + 8]

        join_factors = {}

        def queue_join_factors(n):
            joined = keep.tile([P, STREAMS, CHUNKS, 2, STREAMS], F32, name="joined%d" % n)
            for s in range(STREAMS):
                for k in range(2):
                    multiply(
                        joined[:, s, :, k, :],
                        last_w[n][:, k, :, s:4:2],
                        turn_factors[n][:, 4 * s : 4 * s + 4, k : k + 1].to_broadcast([P, CHUNKS, STREAMS]),
                    )
            join_factors[n] = joined

        def turn_rows(n):
            words = row_tiles[n // 3]
            turned = spare_bank[:, 0:2, :]
            for w in range(2):
                nc.tensor.transpose(turned[:, w, :], words[:, w : 2 * P : 2], identity[:])
            landed = keep.tile([P, 32, 2], F32, name="landed%d" % n)
            add_step(
                lambda: nc.vector.tensor_copy(out=landed[:], in_=turned[:, :, 0:32].rearrange("p w r -> p r w"))
            )
            pairs = landed[:].rearrange("p r w -> p (r w)").bitcast(BF16).rearrange("p (r e) -> p r e", e=4)
            queue_scalars((n, n + 1), pairs[:, 0:16], pairs[:, 16:32])

        queue_scalars((0,), unit_w[0][:], turn_w[0][:])
        aside = [False]

        x_words = x_sb[:].bitcast(F32)
        x_t = spare_bank[:, 0:2, :]
        for u in range(2):
            nc.tensor.transpose(x_t[:, u, :], x_words[:, u : 2 * P : 2], identity[:])
        x_grouped = keep.tile([P, TOKENS, 2], F32, align_bytes=64)
        nc.vector.tensor_copy(out=x_grouped[:], in_=x_t.rearrange("p u t -> p t u"))
        x_codes = keep.tile([P, TOKENS], U32, align_bytes=64)
        x_scales = keep.tile([P, TOKENS], U8, align_bytes=64)

        w_exp_grouped = keep.tile([P, STREAMS, CHUNKS, P, PACK], BF16, align_bytes=64)
        w_exp_codes = keep.tile([P, STREAMS, CHUNKS, P], U32, align_bytes=64)
        w_exp_scales = keep.tile([P, STREAMS, CHUNKS, P], U8, align_bytes=64)

        def regroup_w_exp(h):
            src = w_exp_raw[h][:].rearrange("p t (m c) -> p m t c", c=CHUNKS)
            dst = w_exp_grouped[:, h].rearrange("p c m t -> p m t c")
            cut = 5 * P // 8
            nc.vector.tensor_copy(out=dst[:, :cut], in_=src[:, :cut])
            nc.scalar.copy(out=dst[:, cut:], in_=src[:, cut:])

        def quantise_w_exp(h, half):
            chunks = slice(2 * half, 2 * half + 2)
            nc.vector.quantize_mx(
                out=w_exp_codes[:, h, chunks].rearrange("p c m -> p (c m)").bitcast(FP8X4),
                scales=w_exp_scales[:, h, chunks].rearrange("p c m -> p (c m)"),
                in_=w_exp_grouped[:, h, chunks].rearrange("p c m t -> p (c m t)"),
            )

        def psum_chunks(h):
            return [banks[2 * h + (c & 1)][:, c >> 1, :] for c in range(CHUNKS)]

        def first_product(h):
            chunk = psum_chunks(h)
            for c in CHUNK_ORDER:
                nc.tensor.matmul_mx(
                    out=chunk[c],
                    lhsT=w_exp_codes[:, h, c, :].bitcast(FP8X4),
                    lhsT_scale=w_exp_scales[:, h, c, :],
                    rhs=x_codes[:].bitcast(FP8X4),
                    rhs_scale=x_scales[:],
                    start=True,
                    stop=True,
                )
            return chunk

        regroup_w_exp(0)
        run_steps(1)
        nc.vector.quantize_mx(
            out=x_codes[:].bitcast(FP8X4),
            scales=x_scales[:],
            in_=x_grouped[:].rearrange("p t u -> p (t u)").bitcast(BF16),
        )
        quantise_w_exp(0, 0)
        run_steps(1)
        quantise_w_exp(0, 1)
        run_steps(1)
        regroup_w_exp(1)
        run_steps(1)
        streams = [first_product(0), None]

        def start_stream_1():
            for half in range(2):
                quantise_w_exp(1, half)
            streams[1] = first_product(1)

        w_con_grouped = keep.tile([P, 2, D_OUT, PACK], BF16, align_bytes=64)
        w_con_codes = keep.tile([P, 2, D_OUT], U32, align_bytes=64)
        w_con_scales = keep.tile([P, 2, D_OUT], U8, align_bytes=64)

        def regroup_w_con(copy, eighths):
            for eighth in eighths:
                g, part = divmod(eighth, 4)
                cols = slice(128 * part, 128 * part + 128)
                copy(
                    out=w_con_grouped[:, g, cols, :].rearrange("p (c i) t -> p c t i", i=4),
                    in_=w_con_raw[:, g, :, cols].rearrange("p t (c i) -> p c t i", i=4),
                )

        def quantise_w_con(halves):
            for half in halves:
                g, part = divmod(half, 2)
                cols = slice(256 * part, 256 * part + 256)
                nc.vector.quantize_mx(
                    out=w_con_codes[:, g, cols].bitcast(FP8X4),
                    scales=w_con_scales[:, g, cols],
                    in_=w_con_grouped[:, g, cols].rearrange("p c t -> p (c t)"),
                )

        def work_tile(name):
            return products.tile([P, TOKENS], F32, tag="work", name=name)

        def out_of_psum(chunk, bias=None):
            copied = work_tile("copied")
            if bias is None:
                nc.scalar.copy(out=copied[:], in_=chunk)
            else:
                nc.scalar.activation(out=copied[:], in_=chunk, func=ACT.Identity, bias=bias)
            return copied[:]

        def copies(h, n):
            if n == 0:
                for c in CHUNK_ORDER:
                    streams[h][c] = out_of_psum(streams[h][c], bias=b_exp_sb[:, h, c : c + 1])
            elif n != 3:
                for c in (1, 3):
                    streams[h][c] = out_of_psum(streams[h][c])

        def units(h, n, step_count=0):
            old = streams[h]
            first, second = [
                data.tile([P, CHUNKS, TOKENS], F32, tag="chunks%d_%d" % (h, j), name="chunks%d_%d" % (h, j))
                for j in range(2)
            ]
            middle, last = [first[:, c, :] for c in range(CHUNKS)], [second[:, c, :] for c in range(CHUNKS)]

            def one(j, c):
                source, target = ((old, middle), (middle, last))[j]
                partner = c ^ (1 << j)
                group = (c >> 1, c & 1)[j]
                r = (c >> j) & 1
                multiply_add(target[c], source[partner], factors[n][j][:, 2 * h + group, r : r + 1], source[c])

            every = 1 if step_count > 4 else 2
            for i, (j, c) in enumerate(UNIT_ORDER_AFTER_GELU if n == 3 else UNIT_ORDER):
                one(j, c)
                if i % every == 0 and step_count > 0:
                    run_steps(1)
                    step_count -= 1
            streams[h] = last

        flipped = {}
        def keep_warm(count, bank=warm_bank):
            for i in range(count):
                nc.tensor.matmul_mx(
                    out=bank[:].rearrange("p c t -> p (c t)"),
                    lhsT=x_codes[:].bitcast(FP8X4),
                    lhsT_scale=x_scales[:],
                    rhs=w_exp_codes[:, 0].rearrange("p c m -> p (c m)").bitcast(FP8X4),
                    rhs_scale=w_exp_scales[:, 0].rearrange("p c m -> p (c m)"),
                    start=True,
                    stop=True,
                )

        def turn_stage(h, n, step_count=0, warm=WARM):
            if LOW_RUN[n % 3] == 1:
                flipped[h] = [flip_banks[h][:, c, :] for c in range(CHUNKS)]
            else:
                flipped[h] = [flip_banks[c & 1][:, 2 * h + (c >> 1), :] for c in range(CHUNKS)]
            for c in TURN_ORDER:
                for s in range(2):
                    prod = work_tile("product")
                    scalar = turn_factors[n][:, 4 * h + c, s : s + 1]
                    if (c, s) in VECTOR_PRODUCTS:
                        nc.vector.tensor_scalar(
                            out=prod[:], in0=streams[h][c], scalar1=scalar, scalar2=None, op0=ALU.mult
                        )
                        run_steps(min(step_count, 1))
                        step_count -= min(step_count, 1)
                    else:
                        nc.scalar.activation(out=prod[:], in_=streams[h][c], func=ACT.Copy, scale=scalar)
                    nc.tensor.matmul(
                        flipped[h][c],
                        lhsT=prod[:],
                        rhs=flips[:, n % 3, s, :],
                        start=(s == 0),
                        stop=(s == 1),
                        is_transpose=True,
                    )
            keep_warm(warm)

        def turn_back(h, n):
            by_token = data.tile([P, CHUNKS, P], F32, tag="by_token%d" % h, name="by_token%d" % h)
            new = psum_chunks(h)
            run = LOW_RUN[n % 3]
            if run == 1:
                for c in CHUNK_ORDER:
                    nc.scalar.copy(
                        out=by_token[:, c].rearrange("t (x a) -> t x a", a=CHUNKS),
                        in_=flip_banks[h][:, :, 32 * c : 32 * c + 32].rearrange("t a x -> t x a"),
                    )
                    nc.tensor.transpose(new[c], by_token[:, c], identity[:])
            else:
                to = by_token[:].rearrange("t c (x a b y) -> t b (c x) a y", a=2, b=2, y=run)
                for b in range(2):
                    nc.scalar.copy(out=to[:, b], in_=flip_banks[b][:, 2 * h : 2 * h + 2, :].rearrange("t a (x y) -> t x a y", y=run))
                for c in CHUNK_ORDER:
                    nc.tensor.transpose(new[c], by_token[:, c], identity[:])
            streams[h] = new

        JOIN_BANKS = {0: (7, 6), 2: (0, 1), 1: (4, 5), 3: (2, 3)}

        def join_products(s, n, chunks):
            by_scalar, by_vector = [], []
            for c in chunks:
                for r in range(STREAMS):
                    for k in range(2):
                        prod = work_tile("product")
                        scalar = join_factors[n][:, s, c, k, r : r + 1]
                        (by_vector if (c, r, k) in VECTOR_JOIN[s] else by_scalar).append((c, r, k, prod))
                        if (c, r, k) in VECTOR_JOIN[s]:
                            nc.vector.tensor_scalar(
                                out=prod[:], in0=streams[s][c], scalar1=scalar, scalar2=None, op0=ALU.mult
                            )
                        else:
                            nc.scalar.activation(out=prod[:], in_=streams[s][c], func=ACT.Copy, scale=scalar)

            def turn():
                both = max(len(by_scalar), len(by_vector))
                turns = [t for i in range(both) for t in by_vector[i : i + 1] + by_scalar[i : i + 1]]
                for c, r, k, prod in turns:
                    nc.tensor.matmul(
                        banks[JOIN_BANKS[c][r]][:, 0, :],
                        lhsT=prod[:],
                        rhs=flips[:, flip_of(n), k, :],
                        start=(s == 0 and k == 0),
                        stop=(s == 1 and k == 1),
                        is_transpose=True,
                    )

            return turn

        def join_back(n):
            last = n == LAYOUTS - 1
            run = LOW_RUN[flip_of(n)]
            by_token = [
                data.tile([P, CHUNKS * P], BF16 if last else F32, tag="joined%d_%d" % (last, r), name="joined%d_%d" % (last, r))
                for r in range(STREAMS)
            ]
            for r in range(STREAMS):
                to = by_token[r][:].rearrange("t (x a y) -> t a x y", a=CHUNKS, y=run)
                for c in TURN_ORDER:
                    copy = (nc.scalar.copy, nc.vector.tensor_copy)[c & 1]
                    copy(out=to[:, c], in_=banks[JOIN_BANKS[c][r]][:, 0, :].rearrange("t (x y) -> t x y", y=run))
            for r in range(STREAMS):
                words = by_token[r][:].bitcast(F32)
                streams[r] = [banks[2 * r][:, c, :] for c in range(2)] if last else psum_chunks(r)
                for c in (0, 1) if last else CHUNK_ORDER:
                    nc.tensor.transpose(streams[r][c], words[:, P * c : P * (c + 1)], identity[:])

        def joining_layout(n, steps0, steps1, gap):
            units(0, n, steps0)
            turn_back(1, n - 1)
            turn = join_products(0, n, (0,))
            turn()
            keep_warm(2, banks[4])
            copies(1, n)
            turn = join_products(0, n, (2, 1))
            turn()
            turn = join_products(0, n, (3,))
            units(1, n, steps1)
            keep_warm(0, banks[2])
            turn()
            turn = join_products(1, n, TURN_ORDER)
            turn()
            gap()
            join_back(n)

        def layout(n, steps0=0, steps1=0, steps2=0, gap0=None, gap1=None, warm=WARM):
            units(0, n, steps0)
            if n not in (0, 3):
                turn_back(1, n - 1)
            turn_stage(0, n, warm=warm)
            copies(1, n)
            if gap0:
                gap0()
            units(1, n, steps1)
            turn_back(0, n)
            turn_stage(1, n)
            run_steps(steps2)
            if gap1:
                gap1()
            copies(0, n + 1)

        copies(0, 0)
        keep_warm(2)
        start_stream_1()
        keep_warm(1)
        units(0, 0, 5)
        run_steps(len(steps))
        copies(1, 0)
        turn_stage(0, 0, warm=0)
        turn_rows(1)
        keep_warm(WARM)
        units(1, 0)
        turn_back(0, 0)
        run_steps(1)
        turn_stage(1, 0, 3)
        copies(0, 1)
        run_steps(4)
        aside[0] = True
        queue_join_factors(2)
        queue_scalars((3,), unit_w[3][:], turn_w[3][:])

        def fill(eighths, count):
            for eighth in eighths:
                run_steps(count)
                regroup_w_con(nc.vector.tensor_copy, (eighth,))

        def prepare_down():
            turn_rows(4)
            queue_join_factors(5)

        layout(1, 0, 3, 0, prepare_down, None, 2)
        joining_layout(2, 2, 2, lambda: fill((0,), 0))
        keep_warm(3)
        fill((1, 2), 0)
        regroup_w_con(nc.scalar.copy, (7,))

        for h in range(STREAMS):
            raised = data.tile([P, CHUNKS, TOKENS], F32, tag="chunks%d_0" % h, name="raised%d" % h)
            for c in CHUNK_ORDER:
                nc.scalar.activation(
                    out=raised[:, c, :],
                    in_=streams[h][c],
                    func=ACT.Gelu,
                    bias=up_bias_sb[:, h, c : c + 1],
                )
            streams[h] = [raised[:, c, :] for c in range(CHUNKS)]

        layout(3, 0, 0, len(steps), lambda: fill((3,), 0), lambda: fill((4,), 0))
        layout(4, 0, 0, 0, lambda: fill((5,), 0), lambda: fill((6,), 0))
        joining_layout(5, 0, 0, lambda: quantise_w_con((0, 1)))
        keep_warm(2)
        quantise_w_con((2, 3))

        nc.gpsimd.tensor_tensor(out=out_bias[:], in0=b_con_rows[:], in1=down_bias_rows[:], op=ALU.add)

        h_grouped = keep.tile([P, 2, TOKENS, PACK], BF16, align_bytes=64)
        h_codes = keep.tile([P, 2, TOKENS], U32, align_bytes=64)
        h_scales = keep.tile([P, 2, TOKENS], U8, align_bytes=64)
        for copy, r in ((nc.scalar.copy, 0), (nc.vector.tensor_copy, 1)):
            copy(
                out=h_grouped[:, r].rearrange("p t k -> p (t k)").bitcast(F32).rearrange("p (t u) -> p t u", u=2),
                in_=banks[2 * r][:, 0:2, :].rearrange("p u t -> p t u"),
            )
        half_cols = D_OUT // 2
        out_ps = [bank[:, 0:2, :].rearrange("p c t -> p (c t)") for bank in (spare_bank, warm_bank)]
        out_sb = keep.tile([P, 2, half_cols], F32)
        for g in range(2):
            nc.vector.quantize_mx(
                out=h_codes[:, g, :].bitcast(FP8X4),
                scales=h_scales[:, g, :],
                in_=h_grouped[:, g].rearrange("p t k -> p (t k)"),
            )
        for g in range(2):
            for i in range(2):
                cols = slice(half_cols * i, half_cols * (i + 1))
                nc.tensor.matmul_mx(
                    out=out_ps[i],
                    lhsT=h_codes[:, g, :].bitcast(FP8X4),
                    lhsT_scale=h_scales[:, g, :],
                    rhs=w_con_codes[:, g, cols].bitcast(FP8X4),
                    rhs_scale=w_con_scales[:, g, cols],
                    start=(g == 0),
                    stop=(g == 1),
                )
        for i in range(2):
            cols = slice(half_cols * i, half_cols * (i + 1))
            nc.vector.tensor_tensor(out=out_sb[:, i], in0=out_ps[i], in1=out_bias[:, cols], op=ALU.add)
            nc.sync.dma_start(out=out.flatten_outer_dims()[:, cols], in_=out_sb[:, i])
